import numpy as np
import ml_dtypes


def mxq(x, axis, fmt="e4m3"):
    dtype, down = {"e4m3": (ml_dtypes.float8_e4m3fn, 7), "e5m2": (ml_dtypes.float8_e5m2, 14)}[fmt]
    v = np.moveaxis(np.asarray(x, np.float32).astype(ml_dtypes.bfloat16).astype(np.float64), axis, -1)
    blocks = v.reshape(v.shape[:-1] + (-1, 32))
    amax = np.abs(blocks).max(-1, keepdims=True)
    byte = np.maximum(np.where(amax > 0, np.frexp(amax)[1] - 1 + 127, 0) - down, 1)
    scale = np.exp2(byte - 127.0)
    codes = (blocks / scale).astype(np.float32).astype(dtype).astype(np.float64)
    return np.moveaxis((codes * scale).reshape(v.shape), -1, axis)


WIDE = False


def mx_kscale(k):
    if not WIDE:
        return np.ones(k)
    levels = np.array([10, -10, 5, -5, 0])
    a = np.random.permutation(np.resize(levels, k // 512 * 4)).reshape(k // 512, 4)
    idx = np.arange(k)
    return np.exp2(a[idx // 512, idx % 128 // 32])


BF16 = ml_dtypes.bfloat16


def bf(x):
    return np.asarray(x, np.float32).astype(BF16)


def f64(x):
    return np.asarray(x).astype(np.float64)


E2M1 = np.array([0.0, 0.5, 1.0, 1.5, 2.0, 3.0, 4.0, 6.0, -0.0, -0.5, -1.0, -1.5, -2.0, -3.0, -4.0, -6.0])


def pack_weight(w, fmt):
    k, n = w.shape
    w = f64(bf(w)).reshape(k // 32, 32, n)
    amax = np.abs(w).max(1)
    if fmt == "e4m3":
        byte = np.frexp(amax)[1] - 1 + 127 - 7
    else:
        mant, ex = np.frexp(amax / 6.0)
        byte = np.where(mant > 0.5, ex, ex - 1) + 127
    byte = np.clip(np.where(amax > 0, byte, 1), 1, 254)
    scaled = (w * np.exp2(127.0 - byte)[:, None, :]).reshape(k, n).astype(np.float32)
    by_word = np.ascontiguousarray(scaled.reshape(k // 512, 128, 4, n).transpose(0, 1, 3, 2))
    if fmt == "e4m3":
        words = by_word.astype(ml_dtypes.float8_e4m3fn).view(np.uint8)
    else:
        c = by_word.astype(ml_dtypes.float4_e2m1fn).view(np.uint8) & 0xF
        words = c[..., 0::2] | (c[..., 1::2] << 4)
    return np.ascontiguousarray(words), np.ascontiguousarray(byte.astype(np.uint8).reshape(k // 512, 16, n))


def unpack_weight(words, scales, fmt):
    g, p, n, _ = words.shape
    if fmt == "e4m3":
        vals = np.ascontiguousarray(words).view(ml_dtypes.float8_e4m3fn).astype(np.float64)
    else:
        nib = np.empty((g, p, n, 4), np.uint8)
        nib[..., 0::2] = words & 0xF
        nib[..., 1::2] = words >> 4
        vals = E2M1[nib]
    vals = vals * np.repeat(np.exp2(scales.astype(np.float64) - 127.0), 8, axis=1)[..., None]
    return vals.transpose(0, 1, 3, 2).reshape(g * 512, n)


B, C, H, W, R, G, K = 1, 512, 32, 32, 512, 128, 7
PAD = K // 2
KK = K * K
FMT = "e4m3"


def setup_inputs():
    t = mx_kscale(R)
    x = bf(np.random.standard_normal((B, C, H, W)))
    w_reduce = np.random.standard_normal((R, C)) * 1.0 / np.sqrt(C) * t[:, None]
    b_reduce = bf(np.random.standard_normal(R) * 0.5 * t)
    w_span = np.random.standard_normal((KK * G, R)) * 1.5 / np.sqrt(R) / t[None, :]
    b_span = bf(np.random.standard_normal(KK * G) * 0.5)
    w_reduce_words, w_reduce_scales = pack_weight(np.ascontiguousarray(w_reduce.T), FMT)
    w_span_words, w_span_scales = pack_weight(np.ascontiguousarray(w_span.T), FMT)
    return {"x": x,
            "w_reduce_words": w_reduce_words,
            "w_reduce_scales": w_reduce_scales,
            "b_reduce": b_reduce,
            "w_span_words": w_span_words,
            "w_span_scales": w_span_scales,
            "b_span": b_span}


def reference(x, w_reduce_words, w_reduce_scales, b_reduce, w_span_words, w_span_scales, b_span):
    x = f64(x)
    red = np.maximum((unpack_weight(w_reduce_words, w_reduce_scales, FMT).T @ mxq(x.reshape(B, C, H * W), 1, "e4m3")) + f64(b_reduce)[None, :, None], 0.0)
    kern = (unpack_weight(w_span_words, w_span_scales, FMT).T @ mxq(red, 1, "e4m3")) + f64(b_span)[None, :, None]
    kern = kern.reshape(B, G, KK, H, W)
    e = np.exp(kern - kern.max(axis=2, keepdims=True))
    kern = e / e.sum(axis=2, keepdims=True)
    xp = np.pad(x, ((0, 0), (0, 0), (PAD, PAD), (PAD, PAD)))
    xg = xp.reshape(B, G, C // G, H + 2 * PAD, W + 2 * PAD)
    out = np.zeros((B, G, C // G, H, W))
    for i in range(K):
        for j in range(K):
            out = out + kern[:, :, None, i * K + j] * xg[:, :, :, i:i + H, j:j + W]
    return out.reshape(B, C, H, W)

@@ -1,0 +1,323 @@
+from contextlib import ExitStack
+
+import concourse.mybir as mybir
+from concourse.masks import make_identity
+
+F32 = mybir.dt.float32
+BF16 = mybir.dt.bfloat16
+I32 = mybir.dt.int32
+U32 = mybir.dt.uint32
+U8 = mybir.dt.uint8
+FP8X4 = mybir.dt.float8_e4m3fn_x4
+ADD = mybir.AluOpType.add
+MULT = mybir.AluOpType.mult
+MAX = mybir.AluOpType.max
+EXP = mybir.ActivationFunctionType.Exp
+RELU = mybir.ActivationFunctionType.Relu
+
+P = 128
+PACK = 4
+C = 512
+R = 512
+GROUPS = 128
+CH = C // GROUPS
+KS = 7
+PAD = KS // 2
+TAPS = KS * KS
+O = GROUPS * TAPS
+H = 32
+W = 32
+PIX = H * W
+N_MAX = 512
+PIX_TILES = PIX // P
+TILE_ROWS = P // W
+BLOCK_TILES = 2
+BLOCK_PIX = BLOCK_TILES * P
+BLOCK_ROWS = BLOCK_TILES * TILE_ROWS
+N_BLOCKS = PIX_TILES // BLOCK_TILES
+STEPS = N_BLOCKS * TAPS
+LOGIT_CHUNKS = -(-O // N_MAX)
+VECTOR_STEPS = LOGIT_CHUNKS + 1
+EXPS_PER_STEP = 8
+EXP_STEPS = GROUPS // EXPS_PER_STEP
+GPSIMD_EVERY = 2
+AHEAD = 2
+LAG = 4
+assert BLOCK_TILES * VECTOR_STEPS <= TAPS
+assert VECTOR_STEPS + BLOCK_TILES * EXP_STEPS <= TAPS
+
+FLOPS = 2 * PIX * (C * R + R * O) + 2 * TAPS * C * PIX
+
+
+def load_scale_plane(nc, plane, scales):
+    nc.vector.memset(plane[:].bitcast(I32), 0)
+    for quadrant in range(4):
+        nc.sync.dma_start(
+            out=plane[32 * quadrant : 32 * quadrant + 4, :].bitcast(I32),
+            in_=scales[0, 4 * quadrant : 4 * quadrant + 4, :].bitcast(I32),
+        )
+
+
+def tile_involution_kernel(
+    tc, x, w_reduce_words, w_reduce_scales, b_reduce, w_span_words, w_span_scales, b_span, out
+):
+    nc = tc.nc
+    x_by_group = x.rearrange("b (g c) h w -> (b g) c (h w)", c=CH)
+    out_by_group = out.rearrange("b (g c) h w -> (b g) c (h w)", c=CH)
+
+    with ExitStack() as stack:
+        stack.enter_context(tc.manual_schedule())
+        keep = stack.enter_context(tc.tile_pool(name="keep", bufs=1))
+        logit_pool = stack.enter_context(tc.tile_pool(name="logits", bufs=2 * BLOCK_TILES))
+        stat_pool = stack.enter_context(tc.tile_pool(name="stats", bufs=2 * BLOCK_TILES))
+        psum_sums = stack.enter_context(tc.psum_pool(name="psum_sums", bufs=BLOCK_TILES + 1))
+        psum_turned = stack.enter_context(tc.psum_pool(name="psum_turned", bufs=AHEAD))
+        psum_kern = stack.enter_context(tc.psum_pool(name="psum_kern", bufs=2))
+        psum_back = stack.enter_context(tc.psum_pool(name="psum_back", bufs=1))
+
+        x_sb = keep.tile([P, CH, PIX], BF16)
+        nc.sync.dma_start(out=x_sb[:], in_=x_by_group)
+        x_pad = keep.tile([P, CH, H + 2 * PAD, W + 2 * PAD], BF16)
+        nc.vector.memset(x_pad[:], 0.0)
+        span_bias = keep.tile([P, O], BF16)
+        span_words = keep.tile([P, O], I32, align_bytes=64)
+        span_plane = keep.tile([P, O], U8, align_bytes=64)
+        red_words = keep.tile([P, PIX], U32, align_bytes=64)
+        red_plane = keep.tile([P, PIX], U8, align_bytes=64)
+        ident_f32 = keep.tile([P, P], F32)
+        ident_bf16 = keep.tile([P, P], BF16)
+        make_identity(nc, ident_f32[:])
+        make_identity(nc, ident_bf16[:])
+
+        with tc.tile_pool(name="first", bufs=1) as first, tc.tile_pool(name="first_work", bufs=2) as work:
+            reduce_words = first.tile([P, R], I32, align_bytes=64)
+            reduce_plane = first.tile([P, R], U8, align_bytes=64)
+            reduce_bias = first.tile([P, R], BF16)
+            nc.sync.dma_start(
+                out=reduce_words[:],
+                in_=w_reduce_words.rearrange("o p n t -> (o p) (n t)").bitcast(I32),
+            )
+            load_scale_plane(nc, reduce_plane, w_reduce_scales)
+            nc.scalar.dma_start(out=reduce_bias[:], in_=b_reduce.partition_broadcast(P))
+            load_scale_plane(nc, span_plane, w_span_scales)
+            span_words_dram = w_span_words.rearrange("o p n t -> (o p) (n t)").bitcast(I32)
+            for quarter in range(4):
+                cols = slice(quarter * (O // 4), (quarter + 1) * (O // 4))
+                nc.sync.dma_start(out=span_words[:, cols], in_=span_words_dram[:, cols])
+            nc.scalar.dma_start(out=span_bias[:], in_=b_span.partition_broadcast(P))
+
+            x_grouped = first.tile([P, PIX, PACK], BF16, align_bytes=64)
+            x_words = first.tile([P, PIX], U32, align_bytes=64)
+            x_plane = first.tile([P, PIX], U8, align_bytes=64)
+            halves = [slice(0, PIX // 2), slice(PIX // 2, PIX)]
+            for half in halves:
+                nc.vector.tensor_copy(
+                    out=x_grouped[:, half, :], in_=x_sb[:, :, half].rearrange("p t w -> p w t")
+                )
+            for half in halves:
+                nc.vector.quantize_mx(
+                    out=x_words[:, half].bitcast(FP8X4),
+                    scales=x_plane[:, half],
+                    in_=x_grouped[:, half, :].rearrange("p w t -> p (w t)"),
+                )
+
+            red_rows = {}
+
+            def project(pt):
+                pixels = slice(pt * P, (pt + 1) * P)
+                red_ps = psum_sums.tile([P, R], F32, tag="sums")
+                nc.tensor.matmul_mx(
+                    out=red_ps[:],
+                    lhsT=x_words[:, pixels].bitcast(FP8X4),
+                    lhsT_scale=x_plane[:, pixels],
+                    rhs=reduce_words[:].bitcast(FP8X4),
+                    rhs_scale=reduce_plane[:],
+                    start=True,
+                    stop=True,
+                )
+                red_f32 = work.tile([P, R], F32)
+                nc.vector.tensor_tensor(out=red_f32[:], in0=red_ps[:], in1=reduce_bias[:], op=ADD)
+                red_bf16 = work.tile([P, R], BF16)
+                nc.scalar.activation(out=red_bf16[:], in_=red_f32[:], func=RELU)
+                red_rows[pt] = red_bf16
+
+            def requantise(pt):
+                pixels = slice(pt * P, (pt + 1) * P)
+                red_bf16 = red_rows[pt]
+                red_t = psum_sums.tile([P, PACK, P], BF16, tag="sums")
+                for t in range(PACK):
+                    nc.tensor.transpose(red_t[:, t, :], red_bf16[:, t:R:PACK], ident_bf16[:])
+                red_grouped = work.tile([P, P, PACK], BF16, align_bytes=64)
+                nc.vector.tensor_copy(out=red_grouped[:], in_=red_t[:].rearrange("p t w -> p w t"))
+                nc.vector.quantize_mx(
+                    out=red_words[:, pixels].bitcast(FP8X4),
+                    scales=red_plane[:, pixels],
+                    in_=red_grouped[:].rearrange("p w t -> p (w t)"),
+                )
+
+            project(0)
+            for pt in range(PIX_TILES):
+                if pt + 1 < PIX_TILES:
+                    project(pt + 1)
+                requantise(pt)
+
+        nc.scalar.copy(
+            out=x_pad[:, :, PAD : PAD + H, PAD : PAD + W],
+            in_=x_sb[:].rearrange("p c (h w) -> p c h w", w=W),
+        )
+
+        prod_pool = stack.enter_context(tc.tile_pool(name="products", bufs=2 * LAG))
+        copy_pool = stack.enter_context(tc.tile_pool(name="copies", bufs=3))
+        out_pool = stack.enter_context(tc.tile_pool(name="results", bufs=2))
+
+        kern_of = {}
+        minus_top_of = {}
+        total_of = {}
+        inverse_of = {}
+        turned_of = {}
+        prod_of = {}
+        sums_of = {}
+
+        def vector_step(pt, k):
+            pixels = slice(pt * P, (pt + 1) * P)
+            if k == 0:
+                kern = logit_pool.tile([P, GROUPS, TAPS], F32)
+                kern_of[pt] = kern
+            kern = kern_of[pt]
+            if k < LOGIT_CHUNKS:
+                n0 = k * N_MAX
+                width = min(N_MAX, O - n0)
+                kern_ps = psum_kern.tile([P, N_MAX], F32)
+                nc.tensor.matmul_mx(
+                    out=kern_ps[:, :width],
+                    lhsT=red_words[:, pixels].bitcast(FP8X4),
+                    lhsT_scale=red_plane[:, pixels],
+                    rhs=span_words[:, n0 : n0 + width].bitcast(FP8X4),
+                    rhs_scale=span_plane[:, n0 : n0 + width],
+                    start=True,
+                    stop=True,
+                )
+                nc.vector.tensor_tensor(
+                    out=kern[:].rearrange("p g k -> p (g k)")[:, n0 : n0 + width],
+                    in0=kern_ps[:, :width],
+                    in1=span_bias[:, n0 : n0 + width],
+                    op=ADD,
+                )
+            else:
+                top = stat_pool.tile([P, GROUPS], F32)
+                nc.vector.tensor_reduce(out=top[:], in_=kern[:], axis=mybir.AxisListType.X, op=MAX)
+                minus_top = stat_pool.tile([P, GROUPS], F32)
+                nc.vector.tensor_scalar_mul(out=minus_top[:], in0=top[:], scalar1=-1.0)
+                minus_top_of[pt] = minus_top
+                total = stat_pool.tile([P, GROUPS], F32)
+                total_of[pt] = total
+
+        def scalar_step(pt, k):
+            kern = kern_of[pt]
+            for g in range(k * EXPS_PER_STEP, (k + 1) * EXPS_PER_STEP):
+                nc.scalar.activation(
+                    out=kern[:, g, :],
+                    in_=kern[:, g, :],
+                    func=EXP,
+                    bias=minus_top_of[pt][:, g : g + 1],
+                    scale=1.0,
+                    accum_out=total_of[pt][:, g : g + 1],
+                )
+
+        def turn(step):
+            block, tap = divmod(step, TAPS)
+            turned = psum_turned.tile([P, BLOCK_PIX], F32)
+            for j in range(BLOCK_TILES):
+                nc.tensor.transpose(
+                    turned[:, j * P : (j + 1) * P],
+                    kern_of[block * BLOCK_TILES + j][:, :, tap],
+                    ident_f32[:],
+                )
+            turned_of[step] = turned
+
+        def multiply(step):
+            block, tap = divmod(step, TAPS)
+            row = block * BLOCK_ROWS + tap // KS
+            col = tap % KS
+            window = x_pad[:, :, row : row + BLOCK_ROWS, col : col + W]
+            prod = prod_pool.tile([P, CH, BLOCK_PIX], F32)
+            prod_img = prod[:].rearrange("p c (h w) -> p c h w", w=W)
+            if tap % GPSIMD_EVERY == GPSIMD_EVERY - 1:
+                copied = copy_pool.tile([P, BLOCK_PIX], F32)
+                nc.scalar.copy(out=copied[:], in_=turned_of[step][:])
+                engine, factor = nc.gpsimd, copied
+            else:
+                engine, factor = nc.vector, turned_of[step]
+            engine.tensor_tensor(
+                out=prod_img,
+                in0=factor[:]
+                .rearrange("p (h w) -> p h w", w=W)
+                .unsqueeze(1)
+                .to_broadcast([P, CH, BLOCK_ROWS, W]),
+                in1=window,
+                op=MULT,
+            )
+            prod_of[step] = prod
+
+        def accumulate(step):
+            block, tap = divmod(step, TAPS)
+            for j in range(BLOCK_TILES):
+                pt = block * BLOCK_TILES + j
+                if tap == 0:
+                    sums = psum_sums.tile([P, CH, GROUPS], F32, tag="sums")
+                    sums_of[pt] = sums
+                for c in range(CH):
+                    nc.tensor.matmul(
+                        out=sums_of[pt][:, c, :],
+                        lhsT=prod_of[step][:, c, j * P : (j + 1) * P],
+                        rhs=ident_f32[:],
+                        start=(tap == 0 and c == 0),
+                        stop=(tap == TAPS - 1 and c == CH - 1),
+                        is_transpose=True,
+                    )
+
+        def finish(block):
+            for pt in range(block * BLOCK_TILES, (block + 1) * BLOCK_TILES):
+                scaled = out_pool.tile([P, CH, GROUPS], F32)
+                nc.vector.tensor_tensor(
+                    out=scaled[:],
+                    in0=sums_of[pt][:],
+                    in1=inverse_of[pt][:].unsqueeze(1).to_broadcast([P, CH, GROUPS]),
+                    op=MULT,
+                )
+                back = psum_back.tile([P, CH, P], F32)
+                for c in range(CH):
+                    nc.tensor.transpose(back[:, c, :], scaled[:, c, :], ident_f32[:])
+                result = out_pool.tile([P, CH, P], F32)
+                nc.scalar.copy(out=result[:], in_=back[:])
+                nc.sync.dma_start(out=out_by_group[:, :, pt * P : (pt + 1) * P], in_=result[:])
+
+        for pt in range(BLOCK_TILES):
+            for k in range(VECTOR_STEPS):
+                vector_step(pt, k)
+            for k in range(EXP_STEPS):
+                scalar_step(pt, k)
+        for step in range(AHEAD):
+            turn(step)
+        for step in range(STEPS + LAG + 1):
+            if step < STEPS:
+                block, tap = divmod(step, TAPS)
+                if tap == 0:
+                    for pt in range(block * BLOCK_TILES, (block + 1) * BLOCK_TILES):
+                        inverse = stat_pool.tile([P, GROUPS], F32)
+                        nc.vector.reciprocal(out=inverse[:], in_=total_of[pt][:])
+                        inverse_of[pt] = inverse
+                multiply(step)
+                if step + AHEAD < STEPS:
+                    turn(step + AHEAD)
+                if block + 1 < N_BLOCKS:
+                    next_tile = (block + 1) * BLOCK_TILES
+                    if tap < BLOCK_TILES * VECTOR_STEPS:
+                        vector_step(next_tile + tap // VECTOR_STEPS, tap % VECTOR_STEPS)
+                    late = tap - VECTOR_STEPS
+                    if 0 <= late < BLOCK_TILES * EXP_STEPS:
+                        scalar_step(next_tile + late // EXP_STEPS, late % EXP_STEPS)
+            if step - LAG - 1 >= 0 and (step - LAG - 1) % TAPS == TAPS - 1:
+                finish((step - LAG - 1) // TAPS)
+            if 0 <= step - LAG < STEPS:
+                accumulate(step - LAG)

@@ -10,6 +10,7 @@ U32 = mybir.dt.uint32
 U8 = mybir.dt.uint8
 FP8X4 = mybir.dt.float8_e4m3fn_x4
 ADD = mybir.AluOpType.add
+SUB = mybir.AluOpType.subtract
 MULT = mybir.AluOpType.mult
 MAX = mybir.AluOpType.max
 EXP = mybir.ActivationFunctionType.Exp
@@ -28,29 +29,26 @@ O = GROUPS * TAPS
 H = 32
 W = 32
 PIX = H * W
-N_MAX = 512
-PIX_TILES = PIX // P
-TILE_ROWS = P // W
-BLOCK_TILES = 2
-BLOCK_PIX = BLOCK_TILES * P
-BLOCK_ROWS = BLOCK_TILES * TILE_ROWS
-N_BLOCKS = PIX_TILES // BLOCK_TILES
+HALF = PIX // 2
+BLOCK_ROWS = 8
+BLOCK_PIX = BLOCK_ROWS * W
+BLOCK_TILES = BLOCK_PIX // P
+N_BLOCKS = PIX // BLOCK_PIX
 STEPS = N_BLOCKS * TAPS
-LOGIT_CHUNKS = -(-O // N_MAX)
-VECTOR_STEPS = LOGIT_CHUNKS + 1
-EXPS_PER_STEP = 8
-EXP_STEPS = GROUPS // EXPS_PER_STEP
-GPSIMD_EVERY = 2
-AHEAD = 2
+LEFT = 4
+ROW = LEFT + W
+WIN = 512
+CH_LEN = (H + 2 * PAD) * ROW + 8
 LAG = 4
-assert BLOCK_TILES * VECTOR_STEPS <= TAPS
-assert VECTOR_STEPS + BLOCK_TILES * EXP_STEPS <= TAPS
+LEAD = 2
+G_CHUNKS = 4
+G_CHUNK = GROUPS // G_CHUNKS
+PLANE_SPLIT = 25
 
 FLOPS = 2 * PIX * (C * R + R * O) + 2 * TAPS * C * PIX
 
 
 def load_scale_plane(nc, plane, scales):
-    nc.vector.memset(plane[:].bitcast(I32), 0)
     for quadrant in range(4):
         nc.sync.dma_start(
             out=plane[32 * quadrant : 32 * quadrant + 4, :].bitcast(I32),
@@ -68,207 +66,265 @@ def tile_involution_kernel(
     with ExitStack() as stack:
         stack.enter_context(tc.manual_schedule())
         keep = stack.enter_context(tc.tile_pool(name="keep", bufs=1))
-        logit_pool = stack.enter_context(tc.tile_pool(name="logits", bufs=2 * BLOCK_TILES))
-        stat_pool = stack.enter_context(tc.tile_pool(name="stats", bufs=2 * BLOCK_TILES))
-        psum_sums = stack.enter_context(tc.psum_pool(name="psum_sums", bufs=BLOCK_TILES + 1))
-        psum_turned = stack.enter_context(tc.psum_pool(name="psum_turned", bufs=AHEAD))
-        psum_kern = stack.enter_context(tc.psum_pool(name="psum_kern", bufs=2))
-        psum_back = stack.enter_context(tc.psum_pool(name="psum_back", bufs=1))
+        max_pool = stack.enter_context(tc.tile_pool(name="maxima", bufs=2))
+        diff_pool = stack.enter_context(tc.tile_pool(name="diffs", bufs=3))
+        exp_pool = stack.enter_context(tc.tile_pool(name="exps", bufs=14))
+        prod_pool = stack.enter_context(tc.tile_pool(name="products", bufs=10))
+        out_pool = stack.enter_context(tc.tile_pool(name="results", bufs=2))
+        psum_x = stack.enter_context(tc.psum_pool(name="psum_x", bufs=2))
+        psum_sums = stack.enter_context(tc.psum_pool(name="psum_sums", bufs=2))
+        psum_den = stack.enter_context(tc.psum_pool(name="psum_den", bufs=1))
+        psum_kern = stack.enter_context(tc.psum_pool(name="psum_kern", bufs=3))
 
         x_sb = keep.tile([P, CH, PIX], BF16)
-        nc.sync.dma_start(out=x_sb[:], in_=x_by_group)
-        x_pad = keep.tile([P, CH, H + 2 * PAD, W + 2 * PAD], BF16)
-        nc.vector.memset(x_pad[:], 0.0)
-        span_bias = keep.tile([P, O], BF16)
-        span_words = keep.tile([P, O], I32, align_bytes=64)
-        span_plane = keep.tile([P, O], U8, align_bytes=64)
+        x_pad = keep.tile([P, CH, CH_LEN], BF16)
+        x_grouped = keep.tile([P, PIX, PACK], BF16, align_bytes=64)
+        x_words = keep.tile([P, PIX], U32, align_bytes=64)
+        x_plane = keep.tile([P, PIX], U8, align_bytes=64)
+        reduce_raw = keep.tile([P, R], I32, align_bytes=64)
+        reduce_raw_plane = keep.tile([P, R], U8, align_bytes=64)
+        reduce_words = keep.tile([P, PACK, P], I32, align_bytes=64)
+        reduce_plane = keep.tile([P, PACK, P], U8, align_bytes=64)
+        reduce_bias = keep.tile([P, PACK], BF16)
+        reduce_bias_f32 = keep.tile([P, PACK], F32)
+        span_raw = keep.tile([P, O], I32, align_bytes=64)
+        span_raw_plane = keep.tile([P, O], U8, align_bytes=64)
+        span_words = keep.tile([P, TAPS, GROUPS], I32, align_bytes=64)
+        span_plane = keep.tile([P, TAPS, GROUPS], U8, align_bytes=64)
+        span_bias = keep.tile([P, TAPS], BF16)
+        span_bias_f32 = keep.tile([P, TAPS], F32)
+        red = keep.tile([P, PACK, PIX], BF16)
+        red_grouped = keep.tile([P, PIX, PACK], BF16, align_bytes=64)
         red_words = keep.tile([P, PIX], U32, align_bytes=64)
         red_plane = keep.tile([P, PIX], U8, align_bytes=64)
         ident_f32 = keep.tile([P, P], F32)
         ident_bf16 = keep.tile([P, P], BF16)
-        make_identity(nc, ident_f32[:])
-        make_identity(nc, ident_bf16[:])
+        warm = keep.tile([P, 1], F32)
 
-        with tc.tile_pool(name="first", bufs=1) as first, tc.tile_pool(name="first_work", bufs=2) as work:
-            reduce_words = first.tile([P, R], I32, align_bytes=64)
-            reduce_plane = first.tile([P, R], U8, align_bytes=64)
-            reduce_bias = first.tile([P, R], BF16)
-            nc.sync.dma_start(
-                out=reduce_words[:],
-                in_=w_reduce_words.rearrange("o p n t -> (o p) (n t)").bitcast(I32),
-            )
-            load_scale_plane(nc, reduce_plane, w_reduce_scales)
-            nc.scalar.dma_start(out=reduce_bias[:], in_=b_reduce.partition_broadcast(P))
-            load_scale_plane(nc, span_plane, w_span_scales)
-            span_words_dram = w_span_words.rearrange("o p n t -> (o p) (n t)").bitcast(I32)
-            for quarter in range(4):
-                cols = slice(quarter * (O // 4), (quarter + 1) * (O // 4))
-                nc.sync.dma_start(out=span_words[:, cols], in_=span_words_dram[:, cols])
-            nc.scalar.dma_start(out=span_bias[:], in_=b_span.partition_broadcast(P))
-
-            x_grouped = first.tile([P, PIX, PACK], BF16, align_bytes=64)
-            x_words = first.tile([P, PIX], U32, align_bytes=64)
-            x_plane = first.tile([P, PIX], U8, align_bytes=64)
-            halves = [slice(0, PIX // 2), slice(PIX // 2, PIX)]
-            for half in halves:
-                nc.vector.tensor_copy(
-                    out=x_grouped[:, half, :], in_=x_sb[:, :, half].rearrange("p t w -> p w t")
-                )
-            for half in halves:
-                nc.vector.quantize_mx(
-                    out=x_words[:, half].bitcast(FP8X4),
-                    scales=x_plane[:, half],
-                    in_=x_grouped[:, half, :].rearrange("p w t -> p (w t)"),
-                )
-
-            red_rows = {}
-
-            def project(pt):
-                pixels = slice(pt * P, (pt + 1) * P)
-                red_ps = psum_sums.tile([P, R], F32, tag="sums")
-                nc.tensor.matmul_mx(
-                    out=red_ps[:],
-                    lhsT=x_words[:, pixels].bitcast(FP8X4),
-                    lhsT_scale=x_plane[:, pixels],
-                    rhs=reduce_words[:].bitcast(FP8X4),
-                    rhs_scale=reduce_plane[:],
-                    start=True,
-                    stop=True,
-                )
-                red_f32 = work.tile([P, R], F32)
-                nc.vector.tensor_tensor(out=red_f32[:], in0=red_ps[:], in1=reduce_bias[:], op=ADD)
-                red_bf16 = work.tile([P, R], BF16)
-                nc.scalar.activation(out=red_bf16[:], in_=red_f32[:], func=RELU)
-                red_rows[pt] = red_bf16
-
-            def requantise(pt):
-                pixels = slice(pt * P, (pt + 1) * P)
-                red_bf16 = red_rows[pt]
-                red_t = psum_sums.tile([P, PACK, P], BF16, tag="sums")
-                for t in range(PACK):
-                    nc.tensor.transpose(red_t[:, t, :], red_bf16[:, t:R:PACK], ident_bf16[:])
-                red_grouped = work.tile([P, P, PACK], BF16, align_bytes=64)
-                nc.vector.tensor_copy(out=red_grouped[:], in_=red_t[:].rearrange("p t w -> p w t"))
-                nc.vector.quantize_mx(
-                    out=red_words[:, pixels].bitcast(FP8X4),
-                    scales=red_plane[:, pixels],
-                    in_=red_grouped[:].rearrange("p w t -> p (w t)"),
-                )
-
-            project(0)
-            for pt in range(PIX_TILES):
-                if pt + 1 < PIX_TILES:
-                    project(pt + 1)
-                requantise(pt)
-
-        nc.scalar.copy(
-            out=x_pad[:, :, PAD : PAD + H, PAD : PAD + W],
-            in_=x_sb[:].rearrange("p c (h w) -> p c h w", w=W),
+        nc.vector.memset(reduce_raw_plane[:].bitcast(I32), 0)
+        nc.vector.memset(span_raw_plane[:].bitcast(I32), 0)
+        halves = [slice(0, HALF), slice(HALF, PIX)]
+        nc.sync.dma_start(out=x_sb[:, :, halves[0]], in_=x_by_group[:, :, halves[0]])
+        nc.sync.dma_start(
+            out=reduce_raw[:],
+            in_=w_reduce_words.rearrange("o p n t -> (o p) (n t)").bitcast(I32),
         )
+        load_scale_plane(nc, reduce_raw_plane, w_reduce_scales)
+        nc.sync.dma_start(out=x_sb[:, :, halves[1]], in_=x_by_group[:, :, halves[1]])
+        load_scale_plane(nc, span_raw_plane, w_span_scales)
+        span_words_dram = w_span_words.rearrange("o p n t -> (o p) (n t)").bitcast(I32)
+        for chunk in range(G_CHUNKS):
+            cols = slice(chunk * G_CHUNK * TAPS, (chunk + 1) * G_CHUNK * TAPS)
+            nc.sync.dma_start(out=span_raw[:, cols], in_=span_words_dram[:, cols])
+        nc.scalar.dma_start(out=reduce_bias[:], in_=b_reduce.rearrange("(p t) -> p t", t=PACK))
+        nc.scalar.dma_start(out=span_bias[:], in_=b_span.rearrange("(g t) -> g t", t=TAPS))
 
-        prod_pool = stack.enter_context(tc.tile_pool(name="products", bufs=2 * LAG))
-        copy_pool = stack.enter_context(tc.tile_pool(name="copies", bufs=3))
-        out_pool = stack.enter_context(tc.tile_pool(name="results", bufs=2))
+        make_identity(nc, ident_bf16[:])
+        make_identity(nc, ident_f32[:])
+        nc.gpsimd.memset(x_pad[:].rearrange("p c n -> p (c n)").bitcast(I32), 0)
+        nc.vector.memset(warm[:], 0.0)
+        nc.scalar.activation(out=warm[:], in_=warm[:], func=EXP)
+
+        def group_x(copy, half):
+            copy(out=x_grouped[:, half, :], in_=x_sb[:, :, half].rearrange("p t w -> p w t"))
+
+        def quantise(words, plane, grouped, half):
+            nc.vector.quantize_mx(
+                out=words[:, half].bitcast(FP8X4),
+                scales=plane[:, half],
+                in_=grouped[:, half, :].rearrange("p w t -> p (w t)"),
+            )
+
+        group_x(nc.vector.tensor_copy, halves[0])
+        nc.vector.tensor_copy(out=reduce_words[:], in_=reduce_raw[:].rearrange("p (m t) -> p t m", t=PACK))
+        quantise(x_words, x_plane, x_grouped, halves[0])
+        nc.vector.tensor_copy(out=reduce_plane[:], in_=reduce_raw_plane[:].rearrange("p (m t) -> p t m", t=PACK))
+        nc.vector.tensor_copy(out=reduce_bias_f32[:], in_=reduce_bias[:])
+        nc.vector.tensor_copy(out=span_bias_f32[:], in_=span_bias[:])
+        group_x(nc.scalar.copy, halves[1])
+
+        def project(psum, tag, t, half):
+            red_ps = psum.tile([P, HALF], F32, tag=tag, name="red_ps")
+            nc.tensor.matmul_mx(
+                out=red_ps[:],
+                lhsT=reduce_words[:, t, :].bitcast(FP8X4),
+                lhsT_scale=reduce_plane[:, t, :],
+                rhs=x_words[:, half].bitcast(FP8X4),
+                rhs_scale=x_plane[:, half],
+                start=True,
+                stop=True,
+            )
+            return red_ps
+
+        def relu_on_scalar(red_ps, t, half):
+            nc.scalar.activation(
+                out=red[:, t, half], in_=red_ps[:], func=RELU, bias=reduce_bias_f32[:, t : t + 1]
+            )
+
+        def relu_on_vector(red_ps, t, half):
+            nc.vector.tensor_scalar(
+                out=red[:, t, half],
+                in0=red_ps[:],
+                scalar1=reduce_bias_f32[:, t : t + 1],
+                scalar2=0.0,
+                op0=ADD,
+                op1=MAX,
+            )
+
+        def group_red(copy, pixels):
+            copy(out=red_grouped[:, pixels, :], in_=red[:, :, pixels].rearrange("p t w -> p w t"))
+
+        first = [
+            project(psum_sums, "sums", 0, halves[0]),
+            project(psum_kern, "kern", 1, halves[0]),
+            project(psum_sums, "sums", 2, halves[0]),
+            project(psum_kern, "kern", 3, halves[0]),
+        ]
+        relu_on_scalar(first[0], 0, halves[0])
+        relu_on_vector(first[1], 1, halves[0])
+        relu_on_scalar(first[2], 2, halves[0])
+        relu_on_vector(first[3], 3, halves[0])
+        group_red(nc.vector.tensor_copy, halves[0])
+        quantise(red_words, red_plane, red_grouped, halves[0])
+        quantise(x_words, x_plane, x_grouped, halves[1])
+
+        nc.vector.tensor_copy(
+            out=span_plane[:, :PLANE_SPLIT, :],
+            in_=span_raw_plane[:].rearrange("p (g t) -> p t g", t=TAPS)[:, :PLANE_SPLIT, :],
+        )
+        nc.gpsimd.tensor_copy(
+            out=span_plane[:, PLANE_SPLIT:, :],
+            in_=span_raw_plane[:].rearrange("p (g t) -> p t g", t=TAPS)[:, PLANE_SPLIT:, :],
+        )
+        for chunk in range(G_CHUNKS):
+            groups = slice(chunk * G_CHUNK, (chunk + 1) * G_CHUNK)
+            nc.vector.tensor_copy(
+                out=span_words[:, :, groups],
+                in_=span_raw[:].rearrange("p (g t) -> p t g", t=TAPS)[:, :, groups],
+            )
+
+        for c in range(CH):
+            nc.scalar.copy(
+                out=x_pad[:, c, PAD * ROW : (PAD + H) * ROW].rearrange("p (h w) -> p h w", w=ROW)[:, :, LEFT:],
+                in_=x_sb[:, c, :].rearrange("p (h w) -> p h w", w=W),
+            )
 
         kern_of = {}
-        minus_top_of = {}
-        total_of = {}
-        inverse_of = {}
-        turned_of = {}
+        top_of = {}
+        exp_of = {}
         prod_of = {}
+        window_of = {}
         sums_of = {}
+        scaled_of = {}
+        den_of = {}
 
-        def vector_step(pt, k):
-            pixels = slice(pt * P, (pt + 1) * P)
-            if k == 0:
-                kern = logit_pool.tile([P, GROUPS, TAPS], F32)
-                kern_of[pt] = kern
-            kern = kern_of[pt]
-            if k < LOGIT_CHUNKS:
-                n0 = k * N_MAX
-                width = min(N_MAX, O - n0)
-                kern_ps = psum_kern.tile([P, N_MAX], F32)
-                nc.tensor.matmul_mx(
-                    out=kern_ps[:, :width],
-                    lhsT=red_words[:, pixels].bitcast(FP8X4),
-                    lhsT_scale=red_plane[:, pixels],
-                    rhs=span_words[:, n0 : n0 + width].bitcast(FP8X4),
-                    rhs_scale=span_plane[:, n0 : n0 + width],
-                    start=True,
-                    stop=True,
-                )
-                nc.vector.tensor_tensor(
-                    out=kern[:].rearrange("p g k -> p (g k)")[:, n0 : n0 + width],
-                    in0=kern_ps[:, :width],
-                    in1=span_bias[:, n0 : n0 + width],
-                    op=ADD,
-                )
+        def make_kern(tap, first_block, last_block):
+            pixels = slice(first_block * BLOCK_PIX, (last_block + 1) * BLOCK_PIX)
+            kern = psum_kern.tile([P, 2 * BLOCK_PIX], F32, tag="kern", name="kern")
+            nc.tensor.matmul_mx(
+                out=kern[:, : (last_block + 1 - first_block) * BLOCK_PIX],
+                lhsT=span_words[:, tap, :].bitcast(FP8X4),
+                lhsT_scale=span_plane[:, tap, :],
+                rhs=red_words[:, pixels].bitcast(FP8X4),
+                rhs_scale=red_plane[:, pixels],
+                start=True,
+                stop=True,
+            )
+            return kern
+
+        def take_max(kern_cols, block, tap):
+            bias = span_bias_f32[:, tap : tap + 1]
+            if tap == 0:
+                top = max_pool.tile([P, BLOCK_PIX], F32, name="top")
+                top_of[block] = top
+                nc.vector.tensor_scalar(out=top[:], in0=kern_cols, scalar1=bias, scalar2=None, op0=ADD)
             else:
-                top = stat_pool.tile([P, GROUPS], F32)
-                nc.vector.tensor_reduce(out=top[:], in_=kern[:], axis=mybir.AxisListType.X, op=MAX)
-                minus_top = stat_pool.tile([P, GROUPS], F32)
-                nc.vector.tensor_scalar_mul(out=minus_top[:], in0=top[:], scalar1=-1.0)
-                minus_top_of[pt] = minus_top
-                total = stat_pool.tile([P, GROUPS], F32)
-                total_of[pt] = total
-
-        def scalar_step(pt, k):
-            kern = kern_of[pt]
-            for g in range(k * EXPS_PER_STEP, (k + 1) * EXPS_PER_STEP):
-                nc.scalar.activation(
-                    out=kern[:, g, :],
-                    in_=kern[:, g, :],
-                    func=EXP,
-                    bias=minus_top_of[pt][:, g : g + 1],
-                    scale=1.0,
-                    accum_out=total_of[pt][:, g : g + 1],
+                top = top_of[block]
+                nc.vector.scalar_tensor_tensor(
+                    out=top[:], in0=kern_cols, scalar=bias, in1=top[:], op0=ADD, op1=MAX
                 )
 
-        def turn(step):
+        def make_step_kern(step):
             block, tap = divmod(step, TAPS)
-            turned = psum_turned.tile([P, BLOCK_PIX], F32)
-            for j in range(BLOCK_TILES):
-                nc.tensor.transpose(
-                    turned[:, j * P : (j + 1) * P],
-                    kern_of[block * BLOCK_TILES + j][:, :, tap],
-                    ident_f32[:],
-                )
-            turned_of[step] = turned
+            kern_of[step] = make_kern(tap, block, min(block + 1, N_BLOCKS - 1))
+
+        def step_max(step):
+            block, tap = divmod(step, TAPS)
+            if block + 1 < N_BLOCKS:
+                take_max(kern_of[step][:, BLOCK_PIX:], block + 1, tap)
+
+        def step_exp(step):
+            block, tap = divmod(step, TAPS)
+            diff = diff_pool.tile([P, BLOCK_PIX], F32, name="diff")
+            nc.vector.tensor_tensor(
+                out=diff[:], in0=kern_of[step][:, :BLOCK_PIX], in1=top_of[block][:], op=SUB
+            )
+            exps = exp_pool.tile([P, BLOCK_PIX], F32, name="exps")
+            nc.scalar.activation(out=exps[:], in_=diff[:], func=EXP, bias=span_bias_f32[:, tap : tap + 1])
+            exp_of[step] = exps
+
+        def load_window(block):
+            base = block * BLOCK_ROWS * ROW
+            for pair in range(CH // 2):
+                window = psum_x.tile([P, 2, WIN], BF16, tag="window", name="window")
+                for j in range(2):
+                    nc.tensor.matmul(
+                        out=window[:, j, :],
+                        lhsT=ident_bf16[:],
+                        rhs=x_pad[:, 2 * pair + j, base : base + WIN],
+                        start=True,
+                        stop=True,
+                    )
+                window_of[pair] = window
 
         def multiply(step):
             block, tap = divmod(step, TAPS)
-            row = block * BLOCK_ROWS + tap // KS
-            col = tap % KS
-            window = x_pad[:, :, row : row + BLOCK_ROWS, col : col + W]
-            prod = prod_pool.tile([P, CH, BLOCK_PIX], F32)
-            prod_img = prod[:].rearrange("p c (h w) -> p c h w", w=W)
-            if tap % GPSIMD_EVERY == GPSIMD_EVERY - 1:
-                copied = copy_pool.tile([P, BLOCK_PIX], F32)
-                nc.scalar.copy(out=copied[:], in_=turned_of[step][:])
-                engine, factor = nc.gpsimd, copied
+            prod = prod_pool.tile([P, CH, BLOCK_PIX], F32, name="prod")
+            offset = (tap // KS) * ROW + (LEFT - PAD) + tap % KS
+            exp_img = exp_of[step][:].rearrange("p (h w) -> p h w", w=W).unsqueeze(1)
+            if tap % 2 == 0 and tap != TAPS - 1:
+                start = block * BLOCK_ROWS * ROW + offset
+                nc.gpsimd.tensor_tensor(
+                    out=prod[:].rearrange("p c (h w) -> p c h w", w=W),
+                    in0=exp_img.to_broadcast([P, CH, BLOCK_ROWS, W]),
+                    in1=x_pad[:, :, start : start + BLOCK_ROWS * ROW].rearrange(
+                        "p c (h w) -> p c h w", w=ROW
+                    )[:, :, :, :W],
+                    op=MULT,
+                )
             else:
-                engine, factor = nc.vector, turned_of[step]
-            engine.tensor_tensor(
-                out=prod_img,
-                in0=factor[:]
-                .rearrange("p (h w) -> p h w", w=W)
-                .unsqueeze(1)
-                .to_broadcast([P, CH, BLOCK_ROWS, W]),
-                in1=window,
-                op=MULT,
-            )
+                for pair in range(CH // 2):
+                    nc.vector.tensor_tensor(
+                        out=prod[:, 2 * pair : 2 * pair + 2, :].rearrange("p c (h w) -> p c h w", w=W),
+                        in0=window_of[pair][:, :, offset : offset + BLOCK_ROWS * ROW].rearrange(
+                            "p c (h w) -> p c h w", w=ROW
+                        )[:, :, :, :W],
+                        in1=exp_img.to_broadcast([P, 2, BLOCK_ROWS, W]),
+                        op=MULT,
+                    )
             prod_of[step] = prod
 
         def accumulate(step):
             block, tap = divmod(step, TAPS)
+            if tap == 0:
+                den = psum_den.tile([P, BLOCK_TILES, GROUPS], F32, name="den")
+                den_of[block] = den
+                for j in range(BLOCK_TILES):
+                    sums = psum_sums.tile([P, CH, GROUPS], F32, tag="sums", name="sums")
+                    sums_of[block, j] = sums
             for j in range(BLOCK_TILES):
-                pt = block * BLOCK_TILES + j
-                if tap == 0:
-                    sums = psum_sums.tile([P, CH, GROUPS], F32, tag="sums")
-                    sums_of[pt] = sums
+                nc.tensor.matmul(
+                    out=den_of[block][:, j, :],
+                    lhsT=exp_of[step][:, j * P : (j + 1) * P],
+                    rhs=ident_f32[:],
+                    start=(tap == 0 and j == 0),
+                    stop=(tap == TAPS - 1 and j == BLOCK_TILES - 1),
+                    is_transpose=True,
+                )
+            for j in range(BLOCK_TILES):
                 for c in range(CH):
                     nc.tensor.matmul(
-                        out=sums_of[pt][:, c, :],
+                        out=sums_of[block, j][:, c, :],
                         lhsT=prod_of[step][:, c, j * P : (j + 1) * P],
                         rhs=ident_f32[:],
                         start=(tap == 0 and c == 0),
@@ -276,48 +332,78 @@ def tile_involution_kernel(
                         is_transpose=True,
                     )
 
-        def finish(block):
-            for pt in range(block * BLOCK_TILES, (block + 1) * BLOCK_TILES):
-                scaled = out_pool.tile([P, CH, GROUPS], F32)
+        def divide(block):
+            inverse = out_pool.tile([P, BLOCK_TILES, GROUPS], F32, name="inverse")
+            nc.vector.reciprocal(out=inverse[:], in_=den_of[block][:])
+            for j in range(BLOCK_TILES):
+                scaled = out_pool.tile([P, CH, GROUPS], F32, name="scaled")
                 nc.vector.tensor_tensor(
                     out=scaled[:],
-                    in0=sums_of[pt][:],
-                    in1=inverse_of[pt][:].unsqueeze(1).to_broadcast([P, CH, GROUPS]),
+                    in0=sums_of[block, j][:],
+                    in1=inverse[:, j, :].unsqueeze(1).to_broadcast([P, CH, GROUPS]),
                     op=MULT,
                 )
-                back = psum_back.tile([P, CH, P], F32)
+                scaled_of[block, j] = scaled
+
+        def store(block):
+            for j in range(BLOCK_TILES):
+                scaled = scaled_of[block, j]
+                back = psum_kern.tile([P, CH, P], F32, tag="kern", name="back")
                 for c in range(CH):
                     nc.tensor.transpose(back[:, c, :], scaled[:, c, :], ident_f32[:])
-                result = out_pool.tile([P, CH, P], F32)
+                result = out_pool.tile([P, CH, P], F32, name="result")
                 nc.scalar.copy(out=result[:], in_=back[:])
+                pt = block * BLOCK_TILES + j
                 nc.sync.dma_start(out=out_by_group[:, :, pt * P : (pt + 1) * P], in_=result[:])
 
-        for pt in range(BLOCK_TILES):
-            for k in range(VECTOR_STEPS):
-                vector_step(pt, k)
-            for k in range(EXP_STEPS):
-                scalar_step(pt, k)
-        for step in range(AHEAD):
-            turn(step)
-        for step in range(STEPS + LAG + 1):
+        AHEAD = 2
+        first_kern = {}
+        for tap in range(TAPS + AHEAD):
+            if tap < TAPS:
+                first_kern[tap] = make_kern(tap, 0, 0)
+            if tap >= AHEAD:
+                take_max(first_kern[tap - AHEAD][:, :BLOCK_PIX], 0, tap - AHEAD)
+
+        def second_half(step):
+            if step in (3, 5, 7, 9):
+                t = (step - 3) // 2
+                relu_on_scalar(project(psum_kern, "kern", t, halves[1]), t, halves[1])
+            elif step in (11, 13, 15, 17):
+                quarter = (step - 11) // 2
+                group_red(nc.scalar.copy, slice(HALF + quarter * P, HALF + (quarter + 1) * P))
+            elif step == 21:
+                quantise(red_words, red_plane, red_grouped, halves[1])
+
+        for step in range(LEAD + 1):
+            make_step_kern(step)
+        for step in range(LEAD):
+            step_exp(step)
+            step_max(step)
+        added = 0
+        divided = None
+        for step in range(STEPS + LAG + 4):
+            done = None
+            if step < STEPS and step % TAPS == 0:
+                load_window(step // TAPS)
+            if step % 2 == 0:
+                for ahead in (step + LEAD + 1, step + LEAD + 2):
+                    if LEAD < ahead < STEPS and ahead not in kern_of:
+                        make_step_kern(ahead)
+                while done is None and added < min(step - LAG + 2, STEPS):
+                    accumulate(added)
+                    if added % TAPS == TAPS - 1:
+                        done = added // TAPS
+                    added += 1
+            if step + LEAD < STEPS:
+                step_exp(step + LEAD)
             if step < STEPS:
-                block, tap = divmod(step, TAPS)
-                if tap == 0:
-                    for pt in range(block * BLOCK_TILES, (block + 1) * BLOCK_TILES):
-                        inverse = stat_pool.tile([P, GROUPS], F32)
-                        nc.vector.reciprocal(out=inverse[:], in_=total_of[pt][:])
-                        inverse_of[pt] = inverse
                 multiply(step)
-                if step + AHEAD < STEPS:
-                    turn(step + AHEAD)
-                if block + 1 < N_BLOCKS:
-                    next_tile = (block + 1) * BLOCK_TILES
-                    if tap < BLOCK_TILES * VECTOR_STEPS:
-                        vector_step(next_tile + tap // VECTOR_STEPS, tap % VECTOR_STEPS)
-                    late = tap - VECTOR_STEPS
-                    if 0 <= late < BLOCK_TILES * EXP_STEPS:
-                        scalar_step(next_tile + late // EXP_STEPS, late % EXP_STEPS)
-            if step - LAG - 1 >= 0 and (step - LAG - 1) % TAPS == TAPS - 1:
-                finish((step - LAG - 1) // TAPS)
-            if 0 <= step - LAG < STEPS:
-                accumulate(step - LAG)
+            if step + LEAD < STEPS:
+                step_max(step + LEAD)
+            second_half(step)
+            if divided is not None:
+                store(divided)
+                divided = None
+            if done is not None:
+                divide(done)
+                divided = done

@@ -14,6 +14,7 @@ SUB = mybir.AluOpType.subtract
 MULT = mybir.AluOpType.mult
 MAX = mybir.AluOpType.max
 EXP = mybir.ActivationFunctionType.Exp
+IDENT = mybir.ActivationFunctionType.Identity
 RELU = mybir.ActivationFunctionType.Relu
 
 P = 128
@@ -34,16 +35,20 @@ BLOCK_ROWS = 8
 BLOCK_PIX = BLOCK_ROWS * W
 BLOCK_TILES = BLOCK_PIX // P
 N_BLOCKS = PIX // BLOCK_PIX
-STEPS = N_BLOCKS * TAPS
 LEFT = 4
 ROW = LEFT + W
 WIN = 512
 CH_LEN = (H + 2 * PAD) * ROW + 8
-LAG = 4
+UNIT_TAPS = 2
+UNITS = -(-TAPS // UNIT_TAPS)
+N_UNITS = N_BLOCKS * UNITS
+LAG = 2
 LEAD = 2
+SWEEP_LEAD = UNITS + 3
+FIRST_AHEAD = 3
 G_CHUNKS = 4
 G_CHUNK = GROUPS // G_CHUNKS
-PLANE_SPLIT = 25
+PLANE_SPLIT = 7
 
 FLOPS = 2 * PIX * (C * R + R * O) + 2 * TAPS * C * PIX
 
@@ -66,15 +71,16 @@ def tile_involution_kernel(
     with ExitStack() as stack:
         stack.enter_context(tc.manual_schedule())
         keep = stack.enter_context(tc.tile_pool(name="keep", bufs=1))
-        max_pool = stack.enter_context(tc.tile_pool(name="maxima", bufs=2))
-        diff_pool = stack.enter_context(tc.tile_pool(name="diffs", bufs=3))
-        exp_pool = stack.enter_context(tc.tile_pool(name="exps", bufs=14))
-        prod_pool = stack.enter_context(tc.tile_pool(name="products", bufs=10))
+        max_pool = stack.enter_context(tc.tile_pool(name="maxima", bufs=4))
+        logit_pool = stack.enter_context(tc.tile_pool(name="logits", bufs=SWEEP_LEAD - LEAD + 4))
+        exp_pool = stack.enter_context(tc.tile_pool(name="exps", bufs=LEAD + LAG + 2))
+        prod_pool = stack.enter_context(tc.tile_pool(name="products", bufs=UNIT_TAPS * (LAG + 2)))
         out_pool = stack.enter_context(tc.tile_pool(name="results", bufs=2))
         psum_x = stack.enter_context(tc.psum_pool(name="psum_x", bufs=2))
         psum_sums = stack.enter_context(tc.psum_pool(name="psum_sums", bufs=2))
         psum_den = stack.enter_context(tc.psum_pool(name="psum_den", bufs=1))
-        psum_kern = stack.enter_context(tc.psum_pool(name="psum_kern", bufs=3))
+        psum_kern = stack.enter_context(tc.psum_pool(name="psum_kern", bufs=2))
+        psum_top = stack.enter_context(tc.psum_pool(name="psum_top", bufs=1))
 
         x_sb = keep.tile([P, CH, PIX], BF16)
         x_pad = keep.tile([P, CH, CH_LEN], BF16)
@@ -110,8 +116,8 @@ def tile_involution_kernel(
             in_=w_reduce_words.rearrange("o p n t -> (o p) (n t)").bitcast(I32),
         )
         load_scale_plane(nc, reduce_raw_plane, w_reduce_scales)
-        nc.sync.dma_start(out=x_sb[:, :, halves[1]], in_=x_by_group[:, :, halves[1]])
         load_scale_plane(nc, span_raw_plane, w_span_scales)
+        nc.sync.dma_start(out=x_sb[:, :, halves[1]], in_=x_by_group[:, :, halves[1]])
         span_words_dram = w_span_words.rearrange("o p n t -> (o p) (n t)").bitcast(I32)
         for chunk in range(G_CHUNKS):
             cols = slice(chunk * G_CHUNK * TAPS, (chunk + 1) * G_CHUNK * TAPS)
@@ -119,9 +125,15 @@ def tile_involution_kernel(
         nc.scalar.dma_start(out=reduce_bias[:], in_=b_reduce.rearrange("(p t) -> p t", t=PACK))
         nc.scalar.dma_start(out=span_bias[:], in_=b_span.rearrange("(g t) -> g t", t=TAPS))
 
+        nc.gpsimd.memset(x_pad[:].rearrange("p c n -> p (c n)").bitcast(I32), 0)
+        span_plane_by_tap = span_raw_plane[:].rearrange("p (g t) -> p t g", t=TAPS)
+        for tap in range(PLANE_SPLIT, TAPS, PLANE_SPLIT):
+            nc.gpsimd.tensor_copy(
+                out=span_plane[:, tap : tap + PLANE_SPLIT, :],
+                in_=span_plane_by_tap[:, tap : tap + PLANE_SPLIT, :],
+            )
         make_identity(nc, ident_bf16[:])
         make_identity(nc, ident_f32[:])
-        nc.gpsimd.memset(x_pad[:].rearrange("p c n -> p (c n)").bitcast(I32), 0)
         nc.vector.memset(warm[:], 0.0)
         nc.scalar.activation(out=warm[:], in_=warm[:], func=EXP)
 
@@ -184,17 +196,15 @@ def tile_involution_kernel(
         relu_on_vector(first[1], 1, halves[0])
         relu_on_scalar(first[2], 2, halves[0])
         relu_on_vector(first[3], 3, halves[0])
+        quantise(x_words, x_plane, x_grouped, halves[1])
         group_red(nc.vector.tensor_copy, halves[0])
         quantise(red_words, red_plane, red_grouped, halves[0])
-        quantise(x_words, x_plane, x_grouped, halves[1])
+        for t in range(PACK):
+            relu_on_scalar(project(psum_sums, "sums", t, halves[1]), t, halves[1])
+        group_red(nc.scalar.copy, halves[1])
 
         nc.vector.tensor_copy(
-            out=span_plane[:, :PLANE_SPLIT, :],
-            in_=span_raw_plane[:].rearrange("p (g t) -> p t g", t=TAPS)[:, :PLANE_SPLIT, :],
-        )
-        nc.gpsimd.tensor_copy(
-            out=span_plane[:, PLANE_SPLIT:, :],
-            in_=span_raw_plane[:].rearrange("p (g t) -> p t g", t=TAPS)[:, PLANE_SPLIT:, :],
+            out=span_plane[:, :PLANE_SPLIT, :], in_=span_plane_by_tap[:, :PLANE_SPLIT, :]
         )
         for chunk in range(G_CHUNKS):
             groups = slice(chunk * G_CHUNK, (chunk + 1) * G_CHUNK)
@@ -203,6 +213,7 @@ def tile_involution_kernel(
                 in_=span_raw[:].rearrange("p (g t) -> p t g", t=TAPS)[:, :, groups],
             )
 
+        quantise(red_words, red_plane, red_grouped, halves[1])
         for c in range(CH):
             nc.scalar.copy(
                 out=x_pad[:, c, PAD * ROW : (PAD + H) * ROW].rearrange("p (h w) -> p h w", w=ROW)[:, :, LEFT:],
@@ -210,58 +221,94 @@ def tile_involution_kernel(
             )
 
         kern_of = {}
+        logit_of = {}
+        tops_of = {}
         top_of = {}
         exp_of = {}
         prod_of = {}
         window_of = {}
         sums_of = {}
-        scaled_of = {}
         den_of = {}
+        scaled_of = {}
 
-        def make_kern(tap, first_block, last_block):
-            pixels = slice(first_block * BLOCK_PIX, (last_block + 1) * BLOCK_PIX)
-            kern = psum_kern.tile([P, 2 * BLOCK_PIX], F32, tag="kern", name="kern")
-            nc.tensor.matmul_mx(
-                out=kern[:, : (last_block + 1 - first_block) * BLOCK_PIX],
-                lhsT=span_words[:, tap, :].bitcast(FP8X4),
-                lhsT_scale=span_plane[:, tap, :],
-                rhs=red_words[:, pixels].bitcast(FP8X4),
-                rhs_scale=red_plane[:, pixels],
-                start=True,
-                stop=True,
-            )
-            return kern
+        def taps_of(unit):
+            block, v = divmod(unit, UNITS)
+            return block, range(UNIT_TAPS * v, min(UNIT_TAPS * (v + 1), TAPS))
 
-        def take_max(kern_cols, block, tap):
-            bias = span_bias_f32[:, tap : tap + 1]
-            if tap == 0:
-                top = max_pool.tile([P, BLOCK_PIX], F32, name="top")
-                top_of[block] = top
-                nc.vector.tensor_scalar(out=top[:], in0=kern_cols, scalar1=bias, scalar2=None, op0=ADD)
+        def make_kern(unit):
+            block, taps = taps_of(unit)
+            pixels = slice(block * BLOCK_PIX, (block + 1) * BLOCK_PIX)
+            if unit < UNITS and unit % 2 == 1:
+                kern = psum_sums.tile([P, UNIT_TAPS, BLOCK_PIX], F32, tag="sums", name="kern")
             else:
-                top = top_of[block]
-                nc.vector.scalar_tensor_tensor(
-                    out=top[:], in0=kern_cols, scalar=bias, in1=top[:], op0=ADD, op1=MAX
+                kern = psum_kern.tile([P, UNIT_TAPS, BLOCK_PIX], F32, tag="kern", name="kern")
+            for i, tap in enumerate(taps):
+                nc.tensor.matmul_mx(
+                    out=kern[:, i, :],
+                    lhsT=span_words[:, tap, :].bitcast(FP8X4),
+                    lhsT_scale=span_plane[:, tap, :],
+                    rhs=red_words[:, pixels].bitcast(FP8X4),
+                    rhs_scale=red_plane[:, pixels],
+                    start=True,
+                    stop=True,
+                )
+            kern_of[unit] = kern
+
+        def keep_logits(unit):
+            block, taps = taps_of(unit)
+            logits = logit_pool.tile([P, UNIT_TAPS, BLOCK_PIX], F32, name="logits")
+            for i, tap in enumerate(taps):
+                nc.scalar.activation(
+                    out=logits[:, i, :],
+                    in_=kern_of[unit][:, i, :],
+                    func=IDENT,
+                    bias=span_bias_f32[:, tap : tap + 1],
+                )
+            logit_of[unit] = logits
+
+        def take_max(unit):
+            block, taps = taps_of(unit)
+            for i, tap in enumerate(taps):
+                kern = kern_of[unit][:, i, :]
+                bias = span_bias_f32[:, tap : tap + 1]
+                if tap < UNIT_TAPS:
+                    top = max_pool.tile([P, BLOCK_PIX], F32, name="top")
+                    tops_of[block, i] = top
+                    nc.vector.tensor_scalar(out=top[:], in0=kern, scalar1=bias, scalar2=None, op0=ADD)
+                else:
+                    top = tops_of[block, i]
+                    nc.vector.scalar_tensor_tensor(
+                        out=top[:], in0=kern, scalar=bias, in1=top[:], op0=ADD, op1=MAX
+                    )
+            if taps[-1] == TAPS - 1:
+                nc.vector.tensor_tensor(
+                    out=tops_of[block, 0][:], in0=tops_of[block, 0][:], in1=tops_of[block, 1][:], op=MAX
                 )
 
-        def make_step_kern(step):
-            block, tap = divmod(step, TAPS)
-            kern_of[step] = make_kern(tap, block, min(block + 1, N_BLOCKS - 1))
-
-        def step_max(step):
-            block, tap = divmod(step, TAPS)
-            if block + 1 < N_BLOCKS:
-                take_max(kern_of[step][:, BLOCK_PIX:], block + 1, tap)
-
-        def step_exp(step):
-            block, tap = divmod(step, TAPS)
-            diff = diff_pool.tile([P, BLOCK_PIX], F32, name="diff")
-            nc.vector.tensor_tensor(
-                out=diff[:], in0=kern_of[step][:, :BLOCK_PIX], in1=top_of[block][:], op=SUB
+        def load_top(block):
+            top = psum_top.tile([P, BLOCK_PIX], F32, name="top_ps")
+            nc.tensor.matmul(
+                out=top[:], lhsT=ident_f32[:], rhs=tops_of[block, 0][:], start=True, stop=True
             )
-            exps = exp_pool.tile([P, BLOCK_PIX], F32, name="exps")
-            nc.scalar.activation(out=exps[:], in_=diff[:], func=EXP, bias=span_bias_f32[:, tap : tap + 1])
-            exp_of[step] = exps
+            top_of[block] = top
+
+        def subtract(unit):
+            block, taps = taps_of(unit)
+            n = len(taps)
+            logits = logit_of[unit][:, :n, :]
+            nc.vector.tensor_tensor(
+                out=logits,
+                in0=logits,
+                in1=top_of[block][:].unsqueeze(1).to_broadcast([P, n, BLOCK_PIX]),
+                op=SUB,
+            )
+
+        def exponentiate(unit):
+            block, taps = taps_of(unit)
+            n = len(taps)
+            exps = exp_pool.tile([P, UNIT_TAPS, BLOCK_PIX], F32, name="exps")
+            nc.scalar.activation(out=exps[:, :n, :], in_=logit_of[unit][:, :n, :], func=EXP)
+            exp_of[unit] = exps
 
         def load_window(block):
             base = block * BLOCK_ROWS * ROW
@@ -277,60 +324,65 @@ def tile_involution_kernel(
                     )
                 window_of[pair] = window
 
-        def multiply(step):
-            block, tap = divmod(step, TAPS)
-            prod = prod_pool.tile([P, CH, BLOCK_PIX], F32, name="prod")
-            offset = (tap // KS) * ROW + (LEFT - PAD) + tap % KS
-            exp_img = exp_of[step][:].rearrange("p (h w) -> p h w", w=W).unsqueeze(1)
-            if tap % 2 == 0 and tap != TAPS - 1:
-                start = block * BLOCK_ROWS * ROW + offset
-                nc.gpsimd.tensor_tensor(
-                    out=prod[:].rearrange("p c (h w) -> p c h w", w=W),
-                    in0=exp_img.to_broadcast([P, CH, BLOCK_ROWS, W]),
-                    in1=x_pad[:, :, start : start + BLOCK_ROWS * ROW].rearrange(
-                        "p c (h w) -> p c h w", w=ROW
-                    )[:, :, :, :W],
-                    op=MULT,
-                )
-            else:
-                for pair in range(CH // 2):
-                    nc.vector.tensor_tensor(
-                        out=prod[:, 2 * pair : 2 * pair + 2, :].rearrange("p c (h w) -> p c h w", w=W),
-                        in0=window_of[pair][:, :, offset : offset + BLOCK_ROWS * ROW].rearrange(
+        def multiply(unit):
+            block, taps = taps_of(unit)
+            for i, tap in enumerate(taps):
+                prod = prod_pool.tile([P, CH, BLOCK_PIX], F32, name="prod")
+                offset = (tap // KS) * ROW + (LEFT - PAD) + tap % KS
+                exp_img = exp_of[unit][:, i, :].rearrange("p (h w) -> p h w", w=W).unsqueeze(1)
+                if i == 0 and len(taps) > 1:
+                    start = block * BLOCK_ROWS * ROW + offset
+                    nc.gpsimd.tensor_tensor(
+                        out=prod[:].rearrange("p c (h w) -> p c h w", w=W),
+                        in0=exp_img.to_broadcast([P, CH, BLOCK_ROWS, W]),
+                        in1=x_pad[:, :, start : start + BLOCK_ROWS * ROW].rearrange(
                             "p c (h w) -> p c h w", w=ROW
                         )[:, :, :, :W],
-                        in1=exp_img.to_broadcast([P, 2, BLOCK_ROWS, W]),
                         op=MULT,
                     )
-            prod_of[step] = prod
+                else:
+                    for pair in range(CH // 2):
+                        nc.vector.tensor_tensor(
+                            out=prod[:, 2 * pair : 2 * pair + 2, :].rearrange("p c (h w) -> p c h w", w=W),
+                            in0=window_of[pair][:, :, offset : offset + BLOCK_ROWS * ROW].rearrange(
+                                "p c (h w) -> p c h w", w=ROW
+                            )[:, :, :, :W],
+                            in1=exp_img.to_broadcast([P, 2, BLOCK_ROWS, W]),
+                            op=MULT,
+                        )
+                prod_of[block, tap] = prod
 
-        def accumulate(step):
-            block, tap = divmod(step, TAPS)
-            if tap == 0:
+        def accumulate(unit):
+            block, taps = taps_of(unit)
+            if taps[0] == 0:
                 den = psum_den.tile([P, BLOCK_TILES, GROUPS], F32, name="den")
                 den_of[block] = den
                 for j in range(BLOCK_TILES):
                     sums = psum_sums.tile([P, CH, GROUPS], F32, tag="sums", name="sums")
                     sums_of[block, j] = sums
-            for j in range(BLOCK_TILES):
-                nc.tensor.matmul(
-                    out=den_of[block][:, j, :],
-                    lhsT=exp_of[step][:, j * P : (j + 1) * P],
-                    rhs=ident_f32[:],
-                    start=(tap == 0 and j == 0),
-                    stop=(tap == TAPS - 1 and j == BLOCK_TILES - 1),
-                    is_transpose=True,
-                )
-            for j in range(BLOCK_TILES):
-                for c in range(CH):
+            for i, tap in enumerate(taps):
+                first, last = tap == 0, tap == TAPS - 1
+                for j in range(BLOCK_TILES):
                     nc.tensor.matmul(
-                        out=sums_of[block, j][:, c, :],
-                        lhsT=prod_of[step][:, c, j * P : (j + 1) * P],
+                        out=den_of[block][:, j, :],
+                        lhsT=exp_of[unit][:, i, j * P : (j + 1) * P],
                         rhs=ident_f32[:],
-                        start=(tap == 0 and c == 0),
-                        stop=(tap == TAPS - 1 and c == CH - 1),
+                        start=(first and j == 0),
+                        stop=(last and j == BLOCK_TILES - 1),
                         is_transpose=True,
                     )
+            for i, tap in reversed(list(enumerate(taps))):
+                first, last = tap == taps[-1] and taps[0] == 0, tap == taps[0] and taps[-1] == TAPS - 1
+                for j in range(BLOCK_TILES):
+                    for c in range(CH):
+                        nc.tensor.matmul(
+                            out=sums_of[block, j][:, c, :],
+                            lhsT=prod_of[block, tap][:, c, j * P : (j + 1) * P],
+                            rhs=ident_f32[:],
+                            start=(first and c == 0),
+                            stop=(last and c == CH - 1),
+                            is_transpose=True,
+                        )
 
         def divide(block):
             inverse = out_pool.tile([P, BLOCK_TILES, GROUPS], F32, name="inverse")
@@ -356,51 +408,44 @@ def tile_involution_kernel(
                 pt = block * BLOCK_TILES + j
                 nc.sync.dma_start(out=out_by_group[:, :, pt * P : (pt + 1) * P], in_=result[:])
 
-        AHEAD = 2
-        first_kern = {}
-        for tap in range(TAPS + AHEAD):
-            if tap < TAPS:
-                first_kern[tap] = make_kern(tap, 0, 0)
-            if tap >= AHEAD:
-                take_max(first_kern[tap - AHEAD][:, :BLOCK_PIX], 0, tap - AHEAD)
+        for unit in range(FIRST_AHEAD):
+            make_kern(unit)
+        for unit in range(SWEEP_LEAD):
+            if unit + FIRST_AHEAD <= SWEEP_LEAD:
+                make_kern(unit + FIRST_AHEAD)
+            take_max(unit)
+            keep_logits(unit)
+            if unit == UNITS - 1:
+                load_top(0)
+        for unit in range(LEAD):
+            subtract(unit)
+            exponentiate(unit)
 
-        def second_half(step):
-            if step in (3, 5, 7, 9):
-                t = (step - 3) // 2
-                relu_on_scalar(project(psum_kern, "kern", t, halves[1]), t, halves[1])
-            elif step in (11, 13, 15, 17):
-                quarter = (step - 11) // 2
-                group_red(nc.scalar.copy, slice(HALF + quarter * P, HALF + (quarter + 1) * P))
-            elif step == 21:
-                quantise(red_words, red_plane, red_grouped, halves[1])
-
-        for step in range(LEAD + 1):
-            make_step_kern(step)
-        for step in range(LEAD):
-            step_exp(step)
-            step_max(step)
-        added = 0
         divided = None
-        for step in range(STEPS + LAG + 4):
+        for unit in range(N_UNITS + LAG + 2):
+            block, v = divmod(unit, UNITS)
+            sweep = unit + SWEEP_LEAD
             done = None
-            if step < STEPS and step % TAPS == 0:
-                load_window(step // TAPS)
-            if step % 2 == 0:
-                for ahead in (step + LEAD + 1, step + LEAD + 2):
-                    if LEAD < ahead < STEPS and ahead not in kern_of:
-                        make_step_kern(ahead)
-                while done is None and added < min(step - LAG + 2, STEPS):
-                    accumulate(added)
-                    if added % TAPS == TAPS - 1:
-                        done = added // TAPS
-                    added += 1
-            if step + LEAD < STEPS:
-                step_exp(step + LEAD)
-            if step < STEPS:
-                multiply(step)
-            if step + LEAD < STEPS:
-                step_max(step + LEAD)
-            second_half(step)
+            if unit < N_UNITS and v == 0:
+                load_window(block)
+            if v == UNITS - LEAD and block + 1 < N_BLOCKS:
+                load_top(block + 1)
+            if sweep + 1 < N_UNITS:
+                make_kern(sweep + 1)
+            if 0 <= unit - LAG < N_UNITS:
+                accumulate(unit - LAG)
+                if (unit - LAG) % UNITS == UNITS - 1:
+                    done = (unit - LAG) // UNITS
+            if unit < N_UNITS and v > 0:
+                multiply(unit)
+            if unit + LEAD < N_UNITS:
+                subtract(unit + LEAD)
+                exponentiate(unit + LEAD)
+            if sweep < N_UNITS:
+                take_max(sweep)
+                keep_logits(sweep)
+            if unit < N_UNITS and v == 0:
+                multiply(unit)
             if divided is not None:
                 store(divided)
                 divided = None

@@ -74,352 +74,356 @@ def tile_involution_kernel(
         max_pool = stack.enter_context(tc.tile_pool(name="maxima", bufs=4))
         logit_pool = stack.enter_context(tc.tile_pool(name="logits", bufs=SWEEP_LEAD - LEAD + 4))
         exp_pool = stack.enter_context(tc.tile_pool(name="exps", bufs=LEAD + LAG + 2))
-        prod_pool = stack.enter_context(tc.tile_pool(name="products", bufs=UNIT_TAPS * (LAG + 2)))
-        out_pool = stack.enter_context(tc.tile_pool(name="results", bufs=2))
         psum_x = stack.enter_context(tc.psum_pool(name="psum_x", bufs=2))
         psum_sums = stack.enter_context(tc.psum_pool(name="psum_sums", bufs=2))
         psum_den = stack.enter_context(tc.psum_pool(name="psum_den", bufs=1))
         psum_kern = stack.enter_context(tc.psum_pool(name="psum_kern", bufs=2))
         psum_top = stack.enter_context(tc.psum_pool(name="psum_top", bufs=1))
 
-        x_sb = keep.tile([P, CH, PIX], BF16)
-        x_pad = keep.tile([P, CH, CH_LEN], BF16)
-        x_grouped = keep.tile([P, PIX, PACK], BF16, align_bytes=64)
-        x_words = keep.tile([P, PIX], U32, align_bytes=64)
-        x_plane = keep.tile([P, PIX], U8, align_bytes=64)
-        reduce_raw = keep.tile([P, R], I32, align_bytes=64)
-        reduce_raw_plane = keep.tile([P, R], U8, align_bytes=64)
-        reduce_words = keep.tile([P, PACK, P], I32, align_bytes=64)
-        reduce_plane = keep.tile([P, PACK, P], U8, align_bytes=64)
-        reduce_bias = keep.tile([P, PACK], BF16)
-        reduce_bias_f32 = keep.tile([P, PACK], F32)
-        span_raw = keep.tile([P, O], I32, align_bytes=64)
-        span_raw_plane = keep.tile([P, O], U8, align_bytes=64)
-        span_words = keep.tile([P, TAPS, GROUPS], I32, align_bytes=64)
-        span_plane = keep.tile([P, TAPS, GROUPS], U8, align_bytes=64)
-        span_bias = keep.tile([P, TAPS], BF16)
-        span_bias_f32 = keep.tile([P, TAPS], F32)
-        red = keep.tile([P, PACK, PIX], BF16)
-        red_grouped = keep.tile([P, PIX, PACK], BF16, align_bytes=64)
-        red_words = keep.tile([P, PIX], U32, align_bytes=64)
-        red_plane = keep.tile([P, PIX], U8, align_bytes=64)
-        ident_f32 = keep.tile([P, P], F32)
-        ident_bf16 = keep.tile([P, P], BF16)
-        warm = keep.tile([P, 1], F32)
+        with tc.tile_pool(name="start", bufs=1) as start:
+            x_sb = start.tile([P, CH, PIX], BF16)
+            x_pad = keep.tile([P, CH, CH_LEN], BF16)
+            x_grouped = start.tile([P, PIX, PACK], BF16, align_bytes=64)
+            x_words = start.tile([P, PIX], U32, align_bytes=64)
+            x_plane = start.tile([P, PIX], U8, align_bytes=64)
+            reduce_raw = start.tile([P, R], I32, align_bytes=64)
+            reduce_raw_plane = start.tile([P, R], U8, align_bytes=64)
+            reduce_words = start.tile([P, PACK, P], I32, align_bytes=64)
+            reduce_plane = start.tile([P, PACK, P], U8, align_bytes=64)
+            reduce_bias = keep.tile([P, PACK], BF16)
+            reduce_bias_f32 = keep.tile([P, PACK], F32)
+            span_raw = start.tile([P, O], I32, align_bytes=64)
+            span_raw_plane = start.tile([P, O], U8, align_bytes=64)
+            span_words = keep.tile([P, TAPS, GROUPS], I32, align_bytes=64)
+            span_plane = keep.tile([P, TAPS, GROUPS], U8, align_bytes=64)
+            span_bias = keep.tile([P, TAPS], BF16)
+            span_bias_f32 = keep.tile([P, TAPS], F32)
+            red = start.tile([P, PACK, PIX], BF16)
+            red_grouped = start.tile([P, PIX, PACK], BF16, align_bytes=64)
+            red_words = keep.tile([P, PIX], U32, align_bytes=64)
+            red_plane = keep.tile([P, PIX], U8, align_bytes=64)
+            ident_f32 = keep.tile([P, P], F32)
+            ident_bf16 = keep.tile([P, P], BF16)
+            warm = keep.tile([P, 1], F32)
 
-        nc.vector.memset(reduce_raw_plane[:].bitcast(I32), 0)
-        nc.vector.memset(span_raw_plane[:].bitcast(I32), 0)
-        halves = [slice(0, HALF), slice(HALF, PIX)]
-        nc.sync.dma_start(out=x_sb[:, :, halves[0]], in_=x_by_group[:, :, halves[0]])
-        nc.sync.dma_start(
-            out=reduce_raw[:],
-            in_=w_reduce_words.rearrange("o p n t -> (o p) (n t)").bitcast(I32),
-        )
-        load_scale_plane(nc, reduce_raw_plane, w_reduce_scales)
-        load_scale_plane(nc, span_raw_plane, w_span_scales)
-        nc.sync.dma_start(out=x_sb[:, :, halves[1]], in_=x_by_group[:, :, halves[1]])
-        span_words_dram = w_span_words.rearrange("o p n t -> (o p) (n t)").bitcast(I32)
-        for chunk in range(G_CHUNKS):
-            cols = slice(chunk * G_CHUNK * TAPS, (chunk + 1) * G_CHUNK * TAPS)
-            nc.sync.dma_start(out=span_raw[:, cols], in_=span_words_dram[:, cols])
-        nc.scalar.dma_start(out=reduce_bias[:], in_=b_reduce.rearrange("(p t) -> p t", t=PACK))
-        nc.scalar.dma_start(out=span_bias[:], in_=b_span.rearrange("(g t) -> g t", t=TAPS))
-
-        nc.gpsimd.memset(x_pad[:].rearrange("p c n -> p (c n)").bitcast(I32), 0)
-        span_plane_by_tap = span_raw_plane[:].rearrange("p (g t) -> p t g", t=TAPS)
-        for tap in range(PLANE_SPLIT, TAPS, PLANE_SPLIT):
-            nc.gpsimd.tensor_copy(
-                out=span_plane[:, tap : tap + PLANE_SPLIT, :],
-                in_=span_plane_by_tap[:, tap : tap + PLANE_SPLIT, :],
+            nc.vector.memset(reduce_raw_plane[:].bitcast(I32), 0)
+            nc.vector.memset(span_raw_plane[:].bitcast(I32), 0)
+            halves = [slice(0, HALF), slice(HALF, PIX)]
+            nc.sync.dma_start(out=x_sb[:, :, halves[0]], in_=x_by_group[:, :, halves[0]])
+            nc.sync.dma_start(
+                out=reduce_raw[:],
+                in_=w_reduce_words.rearrange("o p n t -> (o p) (n t)").bitcast(I32),
             )
-        make_identity(nc, ident_bf16[:])
-        make_identity(nc, ident_f32[:])
-        nc.vector.memset(warm[:], 0.0)
-        nc.scalar.activation(out=warm[:], in_=warm[:], func=EXP)
+            load_scale_plane(nc, reduce_raw_plane, w_reduce_scales)
+            load_scale_plane(nc, span_raw_plane, w_span_scales)
+            nc.sync.dma_start(out=x_sb[:, :, halves[1]], in_=x_by_group[:, :, halves[1]])
+            span_words_dram = w_span_words.rearrange("o p n t -> (o p) (n t)").bitcast(I32)
+            for chunk in range(G_CHUNKS):
+                cols = slice(chunk * G_CHUNK * TAPS, (chunk + 1) * G_CHUNK * TAPS)
+                nc.sync.dma_start(out=span_raw[:, cols], in_=span_words_dram[:, cols])
+            nc.scalar.dma_start(out=reduce_bias[:], in_=b_reduce.rearrange("(p t) -> p t", t=PACK))
+            nc.scalar.dma_start(out=span_bias[:], in_=b_span.rearrange("(g t) -> g t", t=TAPS))
 
-        def group_x(copy, half):
-            copy(out=x_grouped[:, half, :], in_=x_sb[:, :, half].rearrange("p t w -> p w t"))
+            nc.gpsimd.memset(x_pad[:].rearrange("p c n -> p (c n)").bitcast(I32), 0)
+            span_plane_by_tap = span_raw_plane[:].rearrange("p (g t) -> p t g", t=TAPS)
+            for tap in range(PLANE_SPLIT, TAPS, PLANE_SPLIT):
+                nc.gpsimd.tensor_copy(
+                    out=span_plane[:, tap : tap + PLANE_SPLIT, :],
+                    in_=span_plane_by_tap[:, tap : tap + PLANE_SPLIT, :],
+                )
+            make_identity(nc, ident_bf16[:])
+            make_identity(nc, ident_f32[:])
+            nc.vector.memset(warm[:], 0.0)
+            nc.scalar.activation(out=warm[:], in_=warm[:], func=EXP)
 
-        def quantise(words, plane, grouped, half):
-            nc.vector.quantize_mx(
-                out=words[:, half].bitcast(FP8X4),
-                scales=plane[:, half],
-                in_=grouped[:, half, :].rearrange("p w t -> p (w t)"),
-            )
+            def group_x(copy, half):
+                copy(out=x_grouped[:, half, :], in_=x_sb[:, :, half].rearrange("p t w -> p w t"))
 
-        group_x(nc.vector.tensor_copy, halves[0])
-        nc.vector.tensor_copy(out=reduce_words[:], in_=reduce_raw[:].rearrange("p (m t) -> p t m", t=PACK))
-        quantise(x_words, x_plane, x_grouped, halves[0])
-        nc.vector.tensor_copy(out=reduce_plane[:], in_=reduce_raw_plane[:].rearrange("p (m t) -> p t m", t=PACK))
-        nc.vector.tensor_copy(out=reduce_bias_f32[:], in_=reduce_bias[:])
-        nc.vector.tensor_copy(out=span_bias_f32[:], in_=span_bias[:])
-        group_x(nc.scalar.copy, halves[1])
+            def quantise(words, plane, grouped, half):
+                nc.vector.quantize_mx(
+                    out=words[:, half].bitcast(FP8X4),
+                    scales=plane[:, half],
+                    in_=grouped[:, half, :].rearrange("p w t -> p (w t)"),
+                )
 
-        def project(psum, tag, t, half):
-            red_ps = psum.tile([P, HALF], F32, tag=tag, name="red_ps")
-            nc.tensor.matmul_mx(
-                out=red_ps[:],
-                lhsT=reduce_words[:, t, :].bitcast(FP8X4),
-                lhsT_scale=reduce_plane[:, t, :],
-                rhs=x_words[:, half].bitcast(FP8X4),
-                rhs_scale=x_plane[:, half],
-                start=True,
-                stop=True,
-            )
-            return red_ps
+            group_x(nc.vector.tensor_copy, halves[0])
+            nc.vector.tensor_copy(out=reduce_words[:], in_=reduce_raw[:].rearrange("p (m t) -> p t m", t=PACK))
+            quantise(x_words, x_plane, x_grouped, halves[0])
+            nc.vector.tensor_copy(out=reduce_plane[:], in_=reduce_raw_plane[:].rearrange("p (m t) -> p t m", t=PACK))
+            nc.vector.tensor_copy(out=reduce_bias_f32[:], in_=reduce_bias[:])
+            nc.vector.tensor_copy(out=span_bias_f32[:], in_=span_bias[:])
+            group_x(nc.scalar.copy, halves[1])
 
-        def relu_on_scalar(red_ps, t, half):
-            nc.scalar.activation(
-                out=red[:, t, half], in_=red_ps[:], func=RELU, bias=reduce_bias_f32[:, t : t + 1]
-            )
-
-        def relu_on_vector(red_ps, t, half):
-            nc.vector.tensor_scalar(
-                out=red[:, t, half],
-                in0=red_ps[:],
-                scalar1=reduce_bias_f32[:, t : t + 1],
-                scalar2=0.0,
-                op0=ADD,
-                op1=MAX,
-            )
-
-        def group_red(copy, pixels):
-            copy(out=red_grouped[:, pixels, :], in_=red[:, :, pixels].rearrange("p t w -> p w t"))
-
-        first = [
-            project(psum_sums, "sums", 0, halves[0]),
-            project(psum_kern, "kern", 1, halves[0]),
-            project(psum_sums, "sums", 2, halves[0]),
-            project(psum_kern, "kern", 3, halves[0]),
-        ]
-        relu_on_scalar(first[0], 0, halves[0])
-        relu_on_vector(first[1], 1, halves[0])
-        relu_on_scalar(first[2], 2, halves[0])
-        relu_on_vector(first[3], 3, halves[0])
-        quantise(x_words, x_plane, x_grouped, halves[1])
-        group_red(nc.vector.tensor_copy, halves[0])
-        quantise(red_words, red_plane, red_grouped, halves[0])
-        for t in range(PACK):
-            relu_on_scalar(project(psum_sums, "sums", t, halves[1]), t, halves[1])
-        group_red(nc.scalar.copy, halves[1])
-
-        nc.vector.tensor_copy(
-            out=span_plane[:, :PLANE_SPLIT, :], in_=span_plane_by_tap[:, :PLANE_SPLIT, :]
-        )
-        for chunk in range(G_CHUNKS):
-            groups = slice(chunk * G_CHUNK, (chunk + 1) * G_CHUNK)
-            nc.vector.tensor_copy(
-                out=span_words[:, :, groups],
-                in_=span_raw[:].rearrange("p (g t) -> p t g", t=TAPS)[:, :, groups],
-            )
-
-        quantise(red_words, red_plane, red_grouped, halves[1])
-        for c in range(CH):
-            nc.scalar.copy(
-                out=x_pad[:, c, PAD * ROW : (PAD + H) * ROW].rearrange("p (h w) -> p h w", w=ROW)[:, :, LEFT:],
-                in_=x_sb[:, c, :].rearrange("p (h w) -> p h w", w=W),
-            )
-
-        kern_of = {}
-        logit_of = {}
-        tops_of = {}
-        top_of = {}
-        exp_of = {}
-        prod_of = {}
-        window_of = {}
-        sums_of = {}
-        den_of = {}
-        scaled_of = {}
-
-        def taps_of(unit):
-            block, v = divmod(unit, UNITS)
-            return block, range(UNIT_TAPS * v, min(UNIT_TAPS * (v + 1), TAPS))
-
-        def make_kern(unit):
-            block, taps = taps_of(unit)
-            pixels = slice(block * BLOCK_PIX, (block + 1) * BLOCK_PIX)
-            if unit < UNITS and unit % 2 == 1:
-                kern = psum_sums.tile([P, UNIT_TAPS, BLOCK_PIX], F32, tag="sums", name="kern")
-            else:
-                kern = psum_kern.tile([P, UNIT_TAPS, BLOCK_PIX], F32, tag="kern", name="kern")
-            for i, tap in enumerate(taps):
+            def project(psum, tag, t, half):
+                red_ps = psum.tile([P, HALF], F32, tag=tag, name="red_ps")
                 nc.tensor.matmul_mx(
-                    out=kern[:, i, :],
-                    lhsT=span_words[:, tap, :].bitcast(FP8X4),
-                    lhsT_scale=span_plane[:, tap, :],
-                    rhs=red_words[:, pixels].bitcast(FP8X4),
-                    rhs_scale=red_plane[:, pixels],
+                    out=red_ps[:],
+                    lhsT=reduce_words[:, t, :].bitcast(FP8X4),
+                    lhsT_scale=reduce_plane[:, t, :],
+                    rhs=x_words[:, half].bitcast(FP8X4),
+                    rhs_scale=x_plane[:, half],
                     start=True,
                     stop=True,
                 )
-            kern_of[unit] = kern
+                return red_ps
 
-        def keep_logits(unit):
-            block, taps = taps_of(unit)
-            logits = logit_pool.tile([P, UNIT_TAPS, BLOCK_PIX], F32, name="logits")
-            for i, tap in enumerate(taps):
+            def relu_on_scalar(red_ps, t, half):
                 nc.scalar.activation(
-                    out=logits[:, i, :],
-                    in_=kern_of[unit][:, i, :],
-                    func=IDENT,
-                    bias=span_bias_f32[:, tap : tap + 1],
+                    out=red[:, t, half], in_=red_ps[:], func=RELU, bias=reduce_bias_f32[:, t : t + 1]
                 )
-            logit_of[unit] = logits
 
-        def take_max(unit):
-            block, taps = taps_of(unit)
-            for i, tap in enumerate(taps):
-                kern = kern_of[unit][:, i, :]
-                bias = span_bias_f32[:, tap : tap + 1]
-                if tap < UNIT_TAPS:
-                    top = max_pool.tile([P, BLOCK_PIX], F32, name="top")
-                    tops_of[block, i] = top
-                    nc.vector.tensor_scalar(out=top[:], in0=kern, scalar1=bias, scalar2=None, op0=ADD)
+            def relu_on_vector(red_ps, t, half):
+                nc.vector.tensor_scalar(
+                    out=red[:, t, half],
+                    in0=red_ps[:],
+                    scalar1=reduce_bias_f32[:, t : t + 1],
+                    scalar2=0.0,
+                    op0=ADD,
+                    op1=MAX,
+                )
+
+            def group_red(copy, pixels):
+                copy(out=red_grouped[:, pixels, :], in_=red[:, :, pixels].rearrange("p t w -> p w t"))
+
+            first = [
+                project(psum_sums, "sums", 0, halves[0]),
+                project(psum_kern, "kern", 1, halves[0]),
+                project(psum_sums, "sums", 2, halves[0]),
+                project(psum_kern, "kern", 3, halves[0]),
+            ]
+            relu_on_scalar(first[0], 0, halves[0])
+            relu_on_vector(first[1], 1, halves[0])
+            relu_on_scalar(first[2], 2, halves[0])
+            relu_on_vector(first[3], 3, halves[0])
+            quantise(x_words, x_plane, x_grouped, halves[1])
+            group_red(nc.vector.tensor_copy, halves[0])
+            quantise(red_words, red_plane, red_grouped, halves[0])
+            for t in range(PACK):
+                relu_on_scalar(project(psum_sums, "sums", t, halves[1]), t, halves[1])
+            group_red(nc.scalar.copy, halves[1])
+
+            nc.vector.tensor_copy(
+                out=span_plane[:, :PLANE_SPLIT, :], in_=span_plane_by_tap[:, :PLANE_SPLIT, :]
+            )
+            for chunk in range(G_CHUNKS):
+                groups = slice(chunk * G_CHUNK, (chunk + 1) * G_CHUNK)
+                nc.vector.tensor_copy(
+                    out=span_words[:, :, groups],
+                    in_=span_raw[:].rearrange("p (g t) -> p t g", t=TAPS)[:, :, groups],
+                )
+
+            quantise(red_words, red_plane, red_grouped, halves[1])
+            for c in range(CH):
+                nc.scalar.copy(
+                    out=x_pad[:, c, PAD * ROW : (PAD + H) * ROW].rearrange("p (h w) -> p h w", w=ROW)[:, :, LEFT:],
+                    in_=x_sb[:, c, :].rearrange("p (h w) -> p h w", w=W),
+                )
+
+            kern_of = {}
+            logit_of = {}
+            tops_of = {}
+            top_of = {}
+            exp_of = {}
+            prod_of = {}
+            window_of = {}
+            sums_of = {}
+            den_of = {}
+            scaled_of = {}
+
+            vector_units = [{8, 16, UNITS - 1}] * (N_BLOCKS - 1) + [{4, 8, 12, 16, 20, UNITS - 1}]
+
+            def taps_of(unit):
+                block, v = divmod(unit, UNITS)
+                return block, range(UNIT_TAPS * v, min(UNIT_TAPS * (v + 1), TAPS))
+
+            def make_kern(unit):
+                block, taps = taps_of(unit)
+                pixels = slice(block * BLOCK_PIX, (block + 1) * BLOCK_PIX)
+                if unit < UNITS and unit % 2 == 1:
+                    kern = psum_sums.tile([P, UNIT_TAPS, BLOCK_PIX], F32, tag="sums", name="kern")
                 else:
-                    top = tops_of[block, i]
-                    nc.vector.scalar_tensor_tensor(
-                        out=top[:], in0=kern, scalar=bias, in1=top[:], op0=ADD, op1=MAX
-                    )
-            if taps[-1] == TAPS - 1:
-                nc.vector.tensor_tensor(
-                    out=tops_of[block, 0][:], in0=tops_of[block, 0][:], in1=tops_of[block, 1][:], op=MAX
-                )
-
-        def load_top(block):
-            top = psum_top.tile([P, BLOCK_PIX], F32, name="top_ps")
-            nc.tensor.matmul(
-                out=top[:], lhsT=ident_f32[:], rhs=tops_of[block, 0][:], start=True, stop=True
-            )
-            top_of[block] = top
-
-        def subtract(unit):
-            block, taps = taps_of(unit)
-            n = len(taps)
-            logits = logit_of[unit][:, :n, :]
-            nc.vector.tensor_tensor(
-                out=logits,
-                in0=logits,
-                in1=top_of[block][:].unsqueeze(1).to_broadcast([P, n, BLOCK_PIX]),
-                op=SUB,
-            )
-
-        def exponentiate(unit):
-            block, taps = taps_of(unit)
-            n = len(taps)
-            exps = exp_pool.tile([P, UNIT_TAPS, BLOCK_PIX], F32, name="exps")
-            nc.scalar.activation(out=exps[:, :n, :], in_=logit_of[unit][:, :n, :], func=EXP)
-            exp_of[unit] = exps
-
-        def load_window(block):
-            base = block * BLOCK_ROWS * ROW
-            for pair in range(CH // 2):
-                window = psum_x.tile([P, 2, WIN], BF16, tag="window", name="window")
-                for j in range(2):
-                    nc.tensor.matmul(
-                        out=window[:, j, :],
-                        lhsT=ident_bf16[:],
-                        rhs=x_pad[:, 2 * pair + j, base : base + WIN],
+                    kern = psum_kern.tile([P, UNIT_TAPS, BLOCK_PIX], F32, tag="kern", name="kern")
+                for i, tap in enumerate(taps):
+                    nc.tensor.matmul_mx(
+                        out=kern[:, i, :],
+                        lhsT=span_words[:, tap, :].bitcast(FP8X4),
+                        lhsT_scale=span_plane[:, tap, :],
+                        rhs=red_words[:, pixels].bitcast(FP8X4),
+                        rhs_scale=red_plane[:, pixels],
                         start=True,
                         stop=True,
                     )
-                window_of[pair] = window
+                kern_of[unit] = kern
 
-        def multiply(unit):
-            block, taps = taps_of(unit)
-            for i, tap in enumerate(taps):
-                prod = prod_pool.tile([P, CH, BLOCK_PIX], F32, name="prod")
-                offset = (tap // KS) * ROW + (LEFT - PAD) + tap % KS
-                exp_img = exp_of[unit][:, i, :].rearrange("p (h w) -> p h w", w=W).unsqueeze(1)
-                if i == 0 and len(taps) > 1:
-                    start = block * BLOCK_ROWS * ROW + offset
-                    nc.gpsimd.tensor_tensor(
-                        out=prod[:].rearrange("p c (h w) -> p c h w", w=W),
-                        in0=exp_img.to_broadcast([P, CH, BLOCK_ROWS, W]),
-                        in1=x_pad[:, :, start : start + BLOCK_ROWS * ROW].rearrange(
-                            "p c (h w) -> p c h w", w=ROW
-                        )[:, :, :, :W],
-                        op=MULT,
+            def keep_logits(unit):
+                block, taps = taps_of(unit)
+                logits = logit_pool.tile([P, UNIT_TAPS, BLOCK_PIX], F32, name="logits")
+                for i, tap in enumerate(taps):
+                    nc.scalar.activation(
+                        out=logits[:, i, :],
+                        in_=kern_of[unit][:, i, :],
+                        func=IDENT,
+                        bias=span_bias_f32[:, tap : tap + 1],
                     )
-                else:
-                    for pair in range(CH // 2):
-                        nc.vector.tensor_tensor(
-                            out=prod[:, 2 * pair : 2 * pair + 2, :].rearrange("p c (h w) -> p c h w", w=W),
-                            in0=window_of[pair][:, :, offset : offset + BLOCK_ROWS * ROW].rearrange(
+                logit_of[unit] = logits
+
+            def take_max(unit):
+                block, taps = taps_of(unit)
+                for i, tap in enumerate(taps):
+                    kern = kern_of[unit][:, i, :]
+                    bias = span_bias_f32[:, tap : tap + 1]
+                    if tap < UNIT_TAPS:
+                        top = max_pool.tile([P, BLOCK_PIX], F32, name="top")
+                        tops_of[block, i] = top
+                        nc.vector.tensor_scalar(out=top[:], in0=kern, scalar1=bias, scalar2=None, op0=ADD)
+                    else:
+                        top = tops_of[block, i]
+                        nc.vector.scalar_tensor_tensor(
+                            out=top[:], in0=kern, scalar=bias, in1=top[:], op0=ADD, op1=MAX
+                        )
+                if taps[-1] == TAPS - 1:
+                    nc.vector.tensor_tensor(
+                        out=tops_of[block, 0][:], in0=tops_of[block, 0][:], in1=tops_of[block, 1][:], op=MAX
+                    )
+
+            def load_top(block):
+                top = psum_top.tile([P, BLOCK_PIX], F32, name="top_ps")
+                nc.tensor.matmul(
+                    out=top[:], lhsT=ident_f32[:], rhs=tops_of[block, 0][:], start=True, stop=True
+                )
+                top_of[block] = top
+
+            def subtract(unit):
+                block, taps = taps_of(unit)
+                n = len(taps)
+                logits = logit_of[unit][:, :n, :]
+                nc.vector.tensor_tensor(
+                    out=logits,
+                    in0=logits,
+                    in1=top_of[block][:].unsqueeze(1).to_broadcast([P, n, BLOCK_PIX]),
+                    op=SUB,
+                )
+
+            def exponentiate(unit):
+                block, taps = taps_of(unit)
+                n = len(taps)
+                exps = exp_pool.tile([P, UNIT_TAPS, BLOCK_PIX], F32, name="exps")
+                nc.scalar.activation(out=exps[:, :n, :], in_=logit_of[unit][:, :n, :], func=EXP)
+                exp_of[unit] = exps
+
+            def load_window(block):
+                base = block * BLOCK_ROWS * ROW
+                for pair in range(CH // 2):
+                    window = psum_x.tile([P, 2, WIN], BF16, tag="window", name="window")
+                    for j in range(2):
+                        nc.tensor.matmul(
+                            out=window[:, j, :],
+                            lhsT=ident_bf16[:],
+                            rhs=x_pad[:, 2 * pair + j, base : base + WIN],
+                            start=True,
+                            stop=True,
+                        )
+                    window_of[pair] = window
+
+            def multiply(unit):
+                block, taps = taps_of(unit)
+                for i, tap in enumerate(taps):
+                    prod = prod_pool.tile([P, CH, BLOCK_PIX], F32, name="prod")
+                    offset = (tap // KS) * ROW + (LEFT - PAD) + tap % KS
+                    exp_img = exp_of[unit][:, i, :].rearrange("p (h w) -> p h w", w=W).unsqueeze(1)
+                    if i == 0 and unit % UNITS not in vector_units[block]:
+                        base = block * BLOCK_ROWS * ROW + offset
+                        nc.gpsimd.tensor_tensor(
+                            out=prod[:].rearrange("p c (h w) -> p c h w", w=W),
+                            in0=exp_img.to_broadcast([P, CH, BLOCK_ROWS, W]),
+                            in1=x_pad[:, :, base : base + BLOCK_ROWS * ROW].rearrange(
                                 "p c (h w) -> p c h w", w=ROW
                             )[:, :, :, :W],
-                            in1=exp_img.to_broadcast([P, 2, BLOCK_ROWS, W]),
                             op=MULT,
                         )
-                prod_of[block, tap] = prod
+                    else:
+                        for pair in range(CH // 2):
+                            nc.vector.tensor_tensor(
+                                out=prod[:, 2 * pair : 2 * pair + 2, :].rearrange("p c (h w) -> p c h w", w=W),
+                                in0=window_of[pair][:, :, offset : offset + BLOCK_ROWS * ROW].rearrange(
+                                    "p c (h w) -> p c h w", w=ROW
+                                )[:, :, :, :W],
+                                in1=exp_img.to_broadcast([P, 2, BLOCK_ROWS, W]),
+                                op=MULT,
+                            )
+                    prod_of[block, tap] = prod
 
-        def accumulate(unit):
-            block, taps = taps_of(unit)
-            if taps[0] == 0:
-                den = psum_den.tile([P, BLOCK_TILES, GROUPS], F32, name="den")
-                den_of[block] = den
-                for j in range(BLOCK_TILES):
-                    sums = psum_sums.tile([P, CH, GROUPS], F32, tag="sums", name="sums")
-                    sums_of[block, j] = sums
-            for i, tap in enumerate(taps):
-                first, last = tap == 0, tap == TAPS - 1
-                for j in range(BLOCK_TILES):
-                    nc.tensor.matmul(
-                        out=den_of[block][:, j, :],
-                        lhsT=exp_of[unit][:, i, j * P : (j + 1) * P],
-                        rhs=ident_f32[:],
-                        start=(first and j == 0),
-                        stop=(last and j == BLOCK_TILES - 1),
-                        is_transpose=True,
-                    )
-            for i, tap in reversed(list(enumerate(taps))):
-                first, last = tap == taps[-1] and taps[0] == 0, tap == taps[0] and taps[-1] == TAPS - 1
-                for j in range(BLOCK_TILES):
-                    for c in range(CH):
+            def accumulate(unit):
+                block, taps = taps_of(unit)
+                if taps[0] == 0:
+                    den = psum_den.tile([P, BLOCK_TILES, GROUPS], F32, name="den")
+                    den_of[block] = den
+                    for j in range(BLOCK_TILES):
+                        sums = psum_sums.tile([P, CH, GROUPS], F32, tag="sums", name="sums")
+                        sums_of[block, j] = sums
+                for i, tap in enumerate(taps):
+                    first, last = tap == 0, tap == TAPS - 1
+                    for j in range(BLOCK_TILES):
                         nc.tensor.matmul(
-                            out=sums_of[block, j][:, c, :],
-                            lhsT=prod_of[block, tap][:, c, j * P : (j + 1) * P],
+                            out=den_of[block][:, j, :],
+                            lhsT=exp_of[unit][:, i, j * P : (j + 1) * P],
                             rhs=ident_f32[:],
-                            start=(first and c == 0),
-                            stop=(last and c == CH - 1),
+                            start=(first and j == 0),
+                            stop=(last and j == BLOCK_TILES - 1),
                             is_transpose=True,
                         )
+                for i, tap in reversed(list(enumerate(taps))):
+                    first, last = tap == taps[-1] and taps[0] == 0, tap == taps[0] and taps[-1] == TAPS - 1
+                    for j in range(BLOCK_TILES):
+                        for c in range(CH):
+                            nc.tensor.matmul(
+                                out=sums_of[block, j][:, c, :],
+                                lhsT=prod_of[block, tap][:, c, j * P : (j + 1) * P],
+                                rhs=ident_f32[:],
+                                start=(first and c == 0),
+                                stop=(last and c == CH - 1),
+                                is_transpose=True,
+                            )
 
-        def divide(block):
-            inverse = out_pool.tile([P, BLOCK_TILES, GROUPS], F32, name="inverse")
-            nc.vector.reciprocal(out=inverse[:], in_=den_of[block][:])
-            for j in range(BLOCK_TILES):
-                scaled = out_pool.tile([P, CH, GROUPS], F32, name="scaled")
-                nc.vector.tensor_tensor(
-                    out=scaled[:],
-                    in0=sums_of[block, j][:],
-                    in1=inverse[:, j, :].unsqueeze(1).to_broadcast([P, CH, GROUPS]),
-                    op=MULT,
-                )
-                scaled_of[block, j] = scaled
+            def divide(block):
+                inverse = out_pool.tile([P, BLOCK_TILES, GROUPS], F32, name="inverse")
+                nc.vector.reciprocal(out=inverse[:], in_=den_of[block][:])
+                for j in range(BLOCK_TILES):
+                    scaled = out_pool.tile([P, CH, GROUPS], F32, name="scaled")
+                    nc.vector.tensor_tensor(
+                        out=scaled[:],
+                        in0=sums_of[block, j][:],
+                        in1=inverse[:, j, :].unsqueeze(1).to_broadcast([P, CH, GROUPS]),
+                        op=MULT,
+                    )
+                    scaled_of[block, j] = scaled
 
-        def store(block):
-            for j in range(BLOCK_TILES):
-                scaled = scaled_of[block, j]
-                back = psum_kern.tile([P, CH, P], F32, tag="kern", name="back")
-                for c in range(CH):
-                    nc.tensor.transpose(back[:, c, :], scaled[:, c, :], ident_f32[:])
-                result = out_pool.tile([P, CH, P], F32, name="result")
-                nc.scalar.copy(out=result[:], in_=back[:])
-                pt = block * BLOCK_TILES + j
-                nc.sync.dma_start(out=out_by_group[:, :, pt * P : (pt + 1) * P], in_=result[:])
+            def store(block):
+                for j in range(BLOCK_TILES):
+                    scaled = scaled_of[block, j]
+                    back = psum_kern.tile([P, CH, P], F32, tag="kern", name="back")
+                    for c in range(CH):
+                        nc.tensor.transpose(back[:, c, :], scaled[:, c, :], ident_f32[:])
+                    result = out_pool.tile([P, CH, P], F32, name="result")
+                    nc.scalar.copy(out=result[:], in_=back[:])
+                    pt = block * BLOCK_TILES + j
+                    nc.sync.dma_start(out=out_by_group[:, :, pt * P : (pt + 1) * P], in_=result[:])
 
-        for unit in range(FIRST_AHEAD):
-            make_kern(unit)
-        for unit in range(SWEEP_LEAD):
-            if unit + FIRST_AHEAD <= SWEEP_LEAD:
-                make_kern(unit + FIRST_AHEAD)
-            take_max(unit)
-            keep_logits(unit)
-            if unit == UNITS - 1:
-                load_top(0)
-        for unit in range(LEAD):
-            subtract(unit)
-            exponentiate(unit)
+            for unit in range(FIRST_AHEAD):
+                make_kern(unit)
+            for unit in range(SWEEP_LEAD):
+                if unit + FIRST_AHEAD <= SWEEP_LEAD:
+                    make_kern(unit + FIRST_AHEAD)
+                take_max(unit)
+                keep_logits(unit)
+                if unit == UNITS - 1:
+                    load_top(0)
+            for unit in range(LEAD):
+                subtract(unit)
+                exponentiate(unit)
+
+        prod_pool = stack.enter_context(tc.tile_pool(name="products", bufs=UNIT_TAPS * (LAG + 4)))
+        out_pool = stack.enter_context(tc.tile_pool(name="results", bufs=2))
 
         divided = None
         for unit in range(N_UNITS + LAG + 2):

@@ -38,7 +38,10 @@ N_BLOCKS = PIX // BLOCK_PIX
 LEFT = 4
 ROW = LEFT + W
 WIN = 512
-CH_LEN = (H + 2 * PAD) * ROW + 8
+PAD_ROWS = H + 2 * PAD
+CH_LEN = PAD_ROWS * ROW + 8
+COPY_COLS = (0, 2, 4, 6)
+FIRST_ROWS = BLOCK_ROWS + 2 * PAD
 UNIT_TAPS = 2
 UNITS = -(-TAPS // UNIT_TAPS)
 N_UNITS = N_BLOCKS * UNITS
@@ -102,6 +105,7 @@ def tile_involution_kernel(
             red_grouped = start.tile([P, PIX, PACK], BF16, align_bytes=64)
             red_words = keep.tile([P, PIX], U32, align_bytes=64)
             red_plane = keep.tile([P, PIX], U8, align_bytes=64)
+            x_cols = {col: keep.tile([P, CH, PAD_ROWS * W], BF16, name="x_col_%d" % col) for col in COPY_COLS}
             ident_f32 = keep.tile([P, P], F32)
             ident_bf16 = keep.tile([P, P], BF16)
             warm = keep.tile([P, 1], F32)
@@ -219,6 +223,20 @@ def tile_involution_kernel(
                     in_=x_sb[:, c, :].rearrange("p (h w) -> p h w", w=W),
                 )
 
+            def copy_columns(engine_copy, col, channels, row0, row1):
+                engine_copy(
+                    out=x_cols[col][:, channels, row0 * W : row1 * W].rearrange("p c (h w) -> p c h w", w=W),
+                    in_=x_pad[:, channels, LEFT - PAD + col : LEFT - PAD + col + PAD_ROWS * ROW].rearrange(
+                        "p c (h w) -> p c h w", w=ROW
+                    )[:, :, row0:row1, :W],
+                )
+
+            def gpsimd_copy(out, in_):
+                nc.gpsimd.tensor_scalar(out=out, in0=in_, scalar1=1.0, scalar2=0.0, op0=MULT, op1=ADD)
+
+            for col in COPY_COLS:
+                copy_columns(gpsimd_copy, col, slice(0, CH), 0, FIRST_ROWS)
+
             kern_of = {}
             logit_of = {}
             tops_of = {}
@@ -230,11 +248,13 @@ def tile_involution_kernel(
             den_of = {}
             scaled_of = {}
 
-            vector_units = [{8, 16, UNITS - 1}] * (N_BLOCKS - 1) + [{4, 8, 12, 16, 20, UNITS - 1}]
+            vector_units = [{UNITS - 1}] * (N_BLOCKS - 1) + [{6, 12, 18, UNITS - 1}]
+            for_gpsimd = [t for col in COPY_COLS for t in range(col, TAPS, KS)][: UNITS - 1]
+            for_vector = [t for t in range(TAPS) if t not in for_gpsimd]
 
             def taps_of(unit):
                 block, v = divmod(unit, UNITS)
-                return block, range(UNIT_TAPS * v, min(UNIT_TAPS * (v + 1), TAPS))
+                return block, for_gpsimd[v : v + 1] + for_vector[v : v + 1]
 
             def make_kern(unit):
                 block, taps = taps_of(unit)
@@ -272,7 +292,7 @@ def tile_involution_kernel(
                 for i, tap in enumerate(taps):
                     kern = kern_of[unit][:, i, :]
                     bias = span_bias_f32[:, tap : tap + 1]
-                    if tap < UNIT_TAPS:
+                    if unit % UNITS == 0:
                         top = max_pool.tile([P, BLOCK_PIX], F32, name="top")
                         tops_of[block, i] = top
                         nc.vector.tensor_scalar(out=top[:], in0=kern, scalar1=bias, scalar2=None, op0=ADD)
@@ -281,7 +301,7 @@ def tile_involution_kernel(
                         nc.vector.scalar_tensor_tensor(
                             out=top[:], in0=kern, scalar=bias, in1=top[:], op0=ADD, op1=MAX
                         )
-                if taps[-1] == TAPS - 1:
+                if unit % UNITS == UNITS - 1:
                     nc.vector.tensor_tensor(
                         out=tops_of[block, 0][:], in0=tops_of[block, 0][:], in1=tops_of[block, 1][:], op=MAX
                     )
@@ -332,13 +352,11 @@ def tile_involution_kernel(
                     offset = (tap // KS) * ROW + (LEFT - PAD) + tap % KS
                     exp_img = exp_of[unit][:, i, :].rearrange("p (h w) -> p h w", w=W).unsqueeze(1)
                     if i == 0 and unit % UNITS not in vector_units[block]:
-                        base = block * BLOCK_ROWS * ROW + offset
+                        row = block * BLOCK_ROWS + tap // KS
                         nc.gpsimd.tensor_tensor(
-                            out=prod[:].rearrange("p c (h w) -> p c h w", w=W),
-                            in0=exp_img.to_broadcast([P, CH, BLOCK_ROWS, W]),
-                            in1=x_pad[:, :, base : base + BLOCK_ROWS * ROW].rearrange(
-                                "p c (h w) -> p c h w", w=ROW
-                            )[:, :, :, :W],
+                            out=prod[:],
+                            in0=exp_of[unit][:, i, :].unsqueeze(1).to_broadcast([P, CH, BLOCK_PIX]),
+                            in1=x_cols[tap % KS][:, :, row * W : row * W + BLOCK_PIX],
                             op=MULT,
                         )
                     else:
@@ -355,25 +373,25 @@ def tile_involution_kernel(
 
             def accumulate(unit):
                 block, taps = taps_of(unit)
-                if taps[0] == 0:
+                opens, closes = unit % UNITS == 0, unit % UNITS == UNITS - 1
+                if opens:
                     den = psum_den.tile([P, BLOCK_TILES, GROUPS], F32, name="den")
                     den_of[block] = den
                     for j in range(BLOCK_TILES):
                         sums = psum_sums.tile([P, CH, GROUPS], F32, tag="sums", name="sums")
                         sums_of[block, j] = sums
                 for i, tap in enumerate(taps):
-                    first, last = tap == 0, tap == TAPS - 1
                     for j in range(BLOCK_TILES):
                         nc.tensor.matmul(
                             out=den_of[block][:, j, :],
                             lhsT=exp_of[unit][:, i, j * P : (j + 1) * P],
                             rhs=ident_f32[:],
-                            start=(first and j == 0),
-                            stop=(last and j == BLOCK_TILES - 1),
+                            start=(opens and i == 0 and j == 0),
+                            stop=(closes and j == BLOCK_TILES - 1),
                             is_transpose=True,
                         )
                 for i, tap in reversed(list(enumerate(taps))):
-                    first, last = tap == taps[-1] and taps[0] == 0, tap == taps[0] and taps[-1] == TAPS - 1
+                    first, last = opens and i == len(taps) - 1, closes and i == 0
                     for j in range(BLOCK_TILES):
                         for c in range(CH):
                             nc.tensor.matmul(
@@ -450,6 +468,9 @@ def tile_involution_kernel(
                 keep_logits(sweep)
             if unit < N_UNITS and v == 0:
                 multiply(unit)
+            if 1 <= unit <= CH * len(COPY_COLS):
+                index, c = divmod(unit - 1, CH)
+                copy_columns(nc.scalar.copy, COPY_COLS[index], slice(c, c + 1), FIRST_ROWS, PAD_ROWS)
             if divided is not None:
                 store(divided)
                 divided = None

@@ -41,11 +41,14 @@ WIN = 512
 PAD_ROWS = H + 2 * PAD
 CH_LEN = PAD_ROWS * ROW + 8
 COPY_COLS = (0, 2, 4, 6)
+GPSIMD_UNITS = (12, 12, 12, 10)
 FIRST_ROWS = BLOCK_ROWS + 2 * PAD
 UNIT_TAPS = 2
 UNITS = -(-TAPS // UNIT_TAPS)
 N_UNITS = N_BLOCKS * UNITS
-LAG = 2
+VECTOR_LAG = 2
+GPSIMD_LAG = 4
+LAG = max(VECTOR_LAG, GPSIMD_LAG)
 LEAD = 2
 SWEEP_LEAD = UNITS + 3
 FIRST_AHEAD = 3
@@ -76,7 +79,7 @@ def tile_involution_kernel(
         keep = stack.enter_context(tc.tile_pool(name="keep", bufs=1))
         max_pool = stack.enter_context(tc.tile_pool(name="maxima", bufs=4))
         logit_pool = stack.enter_context(tc.tile_pool(name="logits", bufs=SWEEP_LEAD - LEAD + 4))
-        exp_pool = stack.enter_context(tc.tile_pool(name="exps", bufs=LEAD + LAG + 2))
+        exp_pool = stack.enter_context(tc.tile_pool(name="exps", bufs=LEAD + 4))
         psum_x = stack.enter_context(tc.psum_pool(name="psum_x", bufs=2))
         psum_sums = stack.enter_context(tc.psum_pool(name="psum_sums", bufs=2))
         psum_den = stack.enter_context(tc.psum_pool(name="psum_den", bufs=1))
@@ -105,7 +108,7 @@ def tile_involution_kernel(
             red_grouped = start.tile([P, PIX, PACK], BF16, align_bytes=64)
             red_words = keep.tile([P, PIX], U32, align_bytes=64)
             red_plane = keep.tile([P, PIX], U8, align_bytes=64)
-            x_cols = {col: keep.tile([P, CH, PAD_ROWS * W], BF16, name="x_col_%d" % col) for col in COPY_COLS}
+            x_cols = keep.tile([P, len(COPY_COLS), CH, PAD_ROWS * W], BF16)
             ident_f32 = keep.tile([P, P], F32)
             ident_bf16 = keep.tile([P, P], BF16)
             warm = keep.tile([P, 1], F32)
@@ -130,7 +133,7 @@ def tile_involution_kernel(
 
             nc.gpsimd.memset(x_pad[:].rearrange("p c n -> p (c n)").bitcast(I32), 0)
             span_plane_by_tap = span_raw_plane[:].rearrange("p (g t) -> p t g", t=TAPS)
-            for tap in range(PLANE_SPLIT, TAPS, PLANE_SPLIT):
+            for tap in range(0, TAPS, PLANE_SPLIT):
                 nc.gpsimd.tensor_copy(
                     out=span_plane[:, tap : tap + PLANE_SPLIT, :],
                     in_=span_plane_by_tap[:, tap : tap + PLANE_SPLIT, :],
@@ -156,7 +159,6 @@ def tile_involution_kernel(
             nc.vector.tensor_copy(out=reduce_plane[:], in_=reduce_raw_plane[:].rearrange("p (m t) -> p t m", t=PACK))
             nc.vector.tensor_copy(out=reduce_bias_f32[:], in_=reduce_bias[:])
             nc.vector.tensor_copy(out=span_bias_f32[:], in_=span_bias[:])
-            group_x(nc.scalar.copy, halves[1])
 
             def project(psum, tag, t, half):
                 red_ps = psum.tile([P, HALF], F32, tag=tag, name="red_ps")
@@ -198,34 +200,37 @@ def tile_involution_kernel(
             relu_on_scalar(first[0], 0, halves[0])
             relu_on_vector(first[1], 1, halves[0])
             relu_on_scalar(first[2], 2, halves[0])
-            relu_on_vector(first[3], 3, halves[0])
-            quantise(x_words, x_plane, x_grouped, halves[1])
-            group_red(nc.vector.tensor_copy, halves[0])
-            quantise(red_words, red_plane, red_grouped, halves[0])
-            for t in range(PACK):
-                relu_on_scalar(project(psum_sums, "sums", t, halves[1]), t, halves[1])
-            group_red(nc.scalar.copy, halves[1])
-
-            nc.vector.tensor_copy(
-                out=span_plane[:, :PLANE_SPLIT, :], in_=span_plane_by_tap[:, :PLANE_SPLIT, :]
-            )
-            for chunk in range(G_CHUNKS):
-                groups = slice(chunk * G_CHUNK, (chunk + 1) * G_CHUNK)
-                nc.vector.tensor_copy(
-                    out=span_words[:, :, groups],
-                    in_=span_raw[:].rearrange("p (g t) -> p t g", t=TAPS)[:, :, groups],
-                )
-
-            quantise(red_words, red_plane, red_grouped, halves[1])
+            relu_on_scalar(first[3], 3, halves[0])
+            group_x(nc.scalar.copy, halves[1])
             for c in range(CH):
                 nc.scalar.copy(
                     out=x_pad[:, c, PAD * ROW : (PAD + H) * ROW].rearrange("p (h w) -> p h w", w=ROW)[:, :, LEFT:],
                     in_=x_sb[:, c, :].rearrange("p (h w) -> p h w", w=W),
                 )
 
+            def reorder_words(chunk):
+                groups = slice(chunk * G_CHUNK, (chunk + 1) * G_CHUNK)
+                nc.vector.tensor_copy(
+                    out=span_words[:, :, groups],
+                    in_=span_raw[:].rearrange("p (g t) -> p t g", t=TAPS)[:, :, groups],
+                )
+
+            reorder_words(0)
+            group_red(nc.vector.tensor_copy, halves[0])
+            reorder_words(1)
+            quantise(red_words, red_plane, red_grouped, halves[0])
+            quantise(x_words, x_plane, x_grouped, halves[1])
+            reorder_words(2)
+            for t in range(PACK):
+                relu_on_scalar(project(psum_sums, "sums", t, halves[1]), t, halves[1])
+            group_red(nc.scalar.copy, halves[1])
+            reorder_words(3)
+
             def copy_columns(engine_copy, col, channels, row0, row1):
                 engine_copy(
-                    out=x_cols[col][:, channels, row0 * W : row1 * W].rearrange("p c (h w) -> p c h w", w=W),
+                    out=x_cols[:, COPY_COLS.index(col), channels, row0 * W : row1 * W].rearrange(
+                        "p c (h w) -> p c h w", w=W
+                    ),
                     in_=x_pad[:, channels, LEFT - PAD + col : LEFT - PAD + col + PAD_ROWS * ROW].rearrange(
                         "p c (h w) -> p c h w", w=ROW
                     )[:, :, row0:row1, :W],
@@ -246,15 +251,34 @@ def tile_involution_kernel(
             window_of = {}
             sums_of = {}
             den_of = {}
+            inverse_of = {}
             scaled_of = {}
 
-            vector_units = [{UNITS - 1}] * (N_BLOCKS - 1) + [{6, 12, 18, UNITS - 1}]
-            for_gpsimd = [t for col in COPY_COLS for t in range(col, TAPS, KS)][: UNITS - 1]
-            for_vector = [t for t in range(TAPS) if t not in for_gpsimd]
+            def unit_taps(gpsimd_units):
+                pairs = [
+                    [row * KS + col for col in COPY_COLS[n : n + UNIT_TAPS]]
+                    for row in range(KS)
+                    for n in range(0, len(COPY_COLS), UNIT_TAPS)
+                ][:gpsimd_units]
+                others = [t for t in range(TAPS) if not any(t in pair for pair in pairs)]
+                units = [others[n : n + UNIT_TAPS] for n in range(0, len(others), UNIT_TAPS)]
+                turns = [u for n, pair in enumerate(pairs) for u in (pair, units[n])] + units[gpsimd_units:]
+                return turns, pairs
+
+            plans = [unit_taps(n) for n in GPSIMD_UNITS]
 
             def taps_of(unit):
                 block, v = divmod(unit, UNITS)
-                return block, for_gpsimd[v : v + 1] + for_vector[v : v + 1]
+                return block, plans[block][0][v]
+
+            def is_gpsimds(unit):
+                block, v = divmod(unit, UNITS)
+                return plans[block][0][v] in plans[block][1]
+
+            def added_at(unit):
+                return unit + (GPSIMD_LAG if is_gpsimds(unit) else VECTOR_LAG)
+
+            adding_order = sorted(range(N_UNITS), key=lambda u: (u // UNITS, added_at(u), u))
 
             def make_kern(unit):
                 block, taps = taps_of(unit)
@@ -347,71 +371,84 @@ def tile_involution_kernel(
 
             def multiply(unit):
                 block, taps = taps_of(unit)
-                for i, tap in enumerate(taps):
-                    prod = prod_pool.tile([P, CH, BLOCK_PIX], F32, name="prod")
-                    offset = (tap // KS) * ROW + (LEFT - PAD) + tap % KS
-                    exp_img = exp_of[unit][:, i, :].rearrange("p (h w) -> p h w", w=W).unsqueeze(1)
-                    if i == 0 and unit % UNITS not in vector_units[block]:
-                        row = block * BLOCK_ROWS + tap // KS
-                        nc.gpsimd.tensor_tensor(
-                            out=prod[:],
-                            in0=exp_of[unit][:, i, :].unsqueeze(1).to_broadcast([P, CH, BLOCK_PIX]),
-                            in1=x_cols[tap % KS][:, :, row * W : row * W + BLOCK_PIX],
-                            op=MULT,
-                        )
-                    else:
+                if is_gpsimds(unit):
+                    prod = prod_pool.tile([P, UNIT_TAPS, CH, BLOCK_PIX], F32, name="gpsimd_prod")
+                    row, col = divmod(taps[0], KS)
+                    begin = (block * BLOCK_ROWS + row) * W
+                    n = COPY_COLS.index(col)
+                    nc.gpsimd.tensor_tensor(
+                        out=prod[:],
+                        in0=exp_of[unit][:].unsqueeze(2).to_broadcast([P, UNIT_TAPS, CH, BLOCK_PIX]),
+                        in1=x_cols[:, n : n + UNIT_TAPS, :, begin : begin + BLOCK_PIX],
+                        op=MULT,
+                    )
+                else:
+                    prod = prod_pool.tile([P, UNIT_TAPS, CH, BLOCK_PIX], F32, name="vector_prod")
+                    for i, tap in enumerate(taps):
+                        offset = (tap // KS) * ROW + (LEFT - PAD) + tap % KS
+                        exp_img = exp_of[unit][:, i, :].rearrange("p (h w) -> p h w", w=W).unsqueeze(1)
                         for pair in range(CH // 2):
                             nc.vector.tensor_tensor(
-                                out=prod[:, 2 * pair : 2 * pair + 2, :].rearrange("p c (h w) -> p c h w", w=W),
+                                out=prod[:, i, 2 * pair : 2 * pair + 2, :].rearrange(
+                                    "p c (h w) -> p c h w", w=W
+                                ),
                                 in0=window_of[pair][:, :, offset : offset + BLOCK_ROWS * ROW].rearrange(
                                     "p c (h w) -> p c h w", w=ROW
                                 )[:, :, :, :W],
                                 in1=exp_img.to_broadcast([P, 2, BLOCK_ROWS, W]),
                                 op=MULT,
                             )
-                    prod_of[block, tap] = prod
+                prod_of[unit] = prod
 
-            def accumulate(unit):
+            def add_exps(unit):
                 block, taps = taps_of(unit)
                 opens, closes = unit % UNITS == 0, unit % UNITS == UNITS - 1
                 if opens:
                     den = psum_den.tile([P, BLOCK_TILES, GROUPS], F32, name="den")
                     den_of[block] = den
-                    for j in range(BLOCK_TILES):
-                        sums = psum_sums.tile([P, CH, GROUPS], F32, tag="sums", name="sums")
-                        sums_of[block, j] = sums
-                for i, tap in enumerate(taps):
+                for i in range(len(taps)):
                     for j in range(BLOCK_TILES):
                         nc.tensor.matmul(
                             out=den_of[block][:, j, :],
                             lhsT=exp_of[unit][:, i, j * P : (j + 1) * P],
                             rhs=ident_f32[:],
                             start=(opens and i == 0 and j == 0),
-                            stop=(closes and j == BLOCK_TILES - 1),
+                            stop=(closes and i == len(taps) - 1 and j == BLOCK_TILES - 1),
                             is_transpose=True,
                         )
-                for i, tap in reversed(list(enumerate(taps))):
-                    first, last = opens and i == len(taps) - 1, closes and i == 0
+
+            def add_products(unit):
+                block, taps = taps_of(unit)
+                in_block = [u for u in adding_order if u // UNITS == block]
+                opens, closes = unit == in_block[0], unit == in_block[-1]
+                if opens:
                     for j in range(BLOCK_TILES):
+                        sums = psum_sums.tile([P, CH, GROUPS], F32, tag="sums", name="sums")
+                        sums_of[block, j] = sums
+                for j in range(BLOCK_TILES):
+                    for i in range(len(taps)):
                         for c in range(CH):
                             nc.tensor.matmul(
                                 out=sums_of[block, j][:, c, :],
-                                lhsT=prod_of[block, tap][:, c, j * P : (j + 1) * P],
+                                lhsT=prod_of[unit][:, i, c, j * P : (j + 1) * P],
                                 rhs=ident_f32[:],
-                                start=(first and c == 0),
-                                stop=(last and c == CH - 1),
+                                start=(opens and i == 0 and c == 0),
+                                stop=(closes and i == len(taps) - 1 and c == CH - 1),
                                 is_transpose=True,
                             )
 
-            def divide(block):
+            def invert(block):
                 inverse = out_pool.tile([P, BLOCK_TILES, GROUPS], F32, name="inverse")
                 nc.vector.reciprocal(out=inverse[:], in_=den_of[block][:])
+                inverse_of[block] = inverse
+
+            def divide(block):
                 for j in range(BLOCK_TILES):
                     scaled = out_pool.tile([P, CH, GROUPS], F32, name="scaled")
                     nc.vector.tensor_tensor(
                         out=scaled[:],
                         in0=sums_of[block, j][:],
-                        in1=inverse[:, j, :].unsqueeze(1).to_broadcast([P, CH, GROUPS]),
+                        in1=inverse_of[block][:, j, :].unsqueeze(1).to_broadcast([P, CH, GROUPS]),
                         op=MULT,
                     )
                     scaled_of[block, j] = scaled
@@ -430,6 +467,8 @@ def tile_involution_kernel(
             for unit in range(FIRST_AHEAD):
                 make_kern(unit)
             for unit in range(SWEEP_LEAD):
+                if unit == 8:
+                    quantise(red_words, red_plane, red_grouped, halves[1])
                 if unit + FIRST_AHEAD <= SWEEP_LEAD:
                     make_kern(unit + FIRST_AHEAD)
                 take_max(unit)
@@ -440,10 +479,12 @@ def tile_involution_kernel(
                 subtract(unit)
                 exponentiate(unit)
 
-        prod_pool = stack.enter_context(tc.tile_pool(name="products", bufs=UNIT_TAPS * (LAG + 4)))
+        prod_pool = stack.enter_context(tc.tile_pool(name="products", bufs=3))
         out_pool = stack.enter_context(tc.tile_pool(name="results", bufs=2))
 
         divided = None
+        adding = adding_order
+        add_exps(0)
         for unit in range(N_UNITS + LAG + 2):
             block, v = divmod(unit, UNITS)
             sweep = unit + SWEEP_LEAD
@@ -454,10 +495,14 @@ def tile_involution_kernel(
                 load_top(block + 1)
             if sweep + 1 < N_UNITS:
                 make_kern(sweep + 1)
-            if 0 <= unit - LAG < N_UNITS:
-                accumulate(unit - LAG)
-                if (unit - LAG) % UNITS == UNITS - 1:
-                    done = (unit - LAG) // UNITS
+            if unit + 1 < N_UNITS:
+                add_exps(unit + 1)
+            while adding and added_at(adding[0]) <= unit:
+                added = adding[0]
+                adding = adding[1:]
+                add_products(added)
+                if not adding or adding[0] // UNITS > added // UNITS:
+                    done = added // UNITS
             if unit < N_UNITS and v > 0:
                 multiply(unit)
             if unit + LEAD < N_UNITS:
@@ -468,6 +513,8 @@ def tile_involution_kernel(
                 keep_logits(sweep)
             if unit < N_UNITS and v == 0:
                 multiply(unit)
+            if unit + 1 < N_UNITS and (unit + 1) % UNITS == UNITS - 1:
+                invert((unit + 1) // UNITS)
             if 1 <= unit <= CH * len(COPY_COLS):
                 index, c = divmod(unit - 1, CH)
                 copy_columns(nc.scalar.copy, COPY_COLS[index], slice(c, c + 1), FIRST_ROWS, PAD_ROWS)

@@ -40,15 +40,13 @@ ROW = LEFT + W
 WIN = 512
 PAD_ROWS = H + 2 * PAD
 CH_LEN = PAD_ROWS * ROW + 8
-COPY_COLS = (0, 2, 4, 6)
-GPSIMD_UNITS = (12, 12, 12, 10)
-FIRST_ROWS = BLOCK_ROWS + 2 * PAD
 UNIT_TAPS = 2
 UNITS = -(-TAPS // UNIT_TAPS)
 N_UNITS = N_BLOCKS * UNITS
 VECTOR_LAG = 2
-GPSIMD_LAG = 4
+GPSIMD_LAG = 3
 LAG = max(VECTOR_LAG, GPSIMD_LAG)
+VECTOR_UNITS = [{UNITS - 1}] * (N_BLOCKS - 1) + [{6, 12, 18, UNITS - 1}]
 LEAD = 2
 SWEEP_LEAD = UNITS + 3
 FIRST_AHEAD = 3
@@ -108,7 +106,7 @@ def tile_involution_kernel(
             red_grouped = start.tile([P, PIX, PACK], BF16, align_bytes=64)
             red_words = keep.tile([P, PIX], U32, align_bytes=64)
             red_plane = keep.tile([P, PIX], U8, align_bytes=64)
-            x_cols = keep.tile([P, len(COPY_COLS), CH, PAD_ROWS * W], BF16)
+            x_pad_f32 = keep.tile([P, CH, CH_LEN], F32)
             ident_f32 = keep.tile([P, P], F32)
             ident_bf16 = keep.tile([P, P], BF16)
             warm = keep.tile([P, 1], F32)
@@ -226,21 +224,9 @@ def tile_involution_kernel(
             group_red(nc.scalar.copy, halves[1])
             reorder_words(3)
 
-            def copy_columns(engine_copy, col, channels, row0, row1):
-                engine_copy(
-                    out=x_cols[:, COPY_COLS.index(col), channels, row0 * W : row1 * W].rearrange(
-                        "p c (h w) -> p c h w", w=W
-                    ),
-                    in_=x_pad[:, channels, LEFT - PAD + col : LEFT - PAD + col + PAD_ROWS * ROW].rearrange(
-                        "p c (h w) -> p c h w", w=ROW
-                    )[:, :, row0:row1, :W],
-                )
-
-            def gpsimd_copy(out, in_):
-                nc.gpsimd.tensor_scalar(out=out, in0=in_, scalar1=1.0, scalar2=0.0, op0=MULT, op1=ADD)
-
-            for col in COPY_COLS:
-                copy_columns(gpsimd_copy, col, slice(0, CH), 0, FIRST_ROWS)
+            nc.gpsimd.tensor_scalar(
+                out=x_pad_f32[:], in0=x_pad[:], scalar1=1.0, scalar2=0.0, op0=MULT, op1=ADD
+            )
 
             kern_of = {}
             logit_of = {}
@@ -254,31 +240,21 @@ def tile_involution_kernel(
             inverse_of = {}
             scaled_of = {}
 
-            def unit_taps(gpsimd_units):
-                pairs = [
-                    [row * KS + col for col in COPY_COLS[n : n + UNIT_TAPS]]
-                    for row in range(KS)
-                    for n in range(0, len(COPY_COLS), UNIT_TAPS)
-                ][:gpsimd_units]
-                others = [t for t in range(TAPS) if not any(t in pair for pair in pairs)]
-                units = [others[n : n + UNIT_TAPS] for n in range(0, len(others), UNIT_TAPS)]
-                turns = [u for n, pair in enumerate(pairs) for u in (pair, units[n])] + units[gpsimd_units:]
-                return turns, pairs
-
-            plans = [unit_taps(n) for n in GPSIMD_UNITS]
-
             def taps_of(unit):
                 block, v = divmod(unit, UNITS)
-                return block, plans[block][0][v]
+                return block, range(UNIT_TAPS * v, min(UNIT_TAPS * (v + 1), TAPS))
 
-            def is_gpsimds(unit):
+            def is_gpsimds(unit, i):
                 block, v = divmod(unit, UNITS)
-                return plans[block][0][v] in plans[block][1]
+                return i == 0 and v not in VECTOR_UNITS[block]
 
-            def added_at(unit):
-                return unit + (GPSIMD_LAG if is_gpsimds(unit) else VECTOR_LAG)
+            def added_at(unit, i):
+                return unit + (GPSIMD_LAG if is_gpsimds(unit, i) else VECTOR_LAG)
 
-            adding_order = sorted(range(N_UNITS), key=lambda u: (u // UNITS, added_at(u), u))
+            adding_order = sorted(
+                [(unit, i) for unit in range(N_UNITS) for i in range(len(taps_of(unit)[1]))],
+                key=lambda tap: (tap[0] // UNITS, added_at(*tap), tap),
+            )
 
             def make_kern(unit):
                 block, taps = taps_of(unit)
@@ -371,34 +347,31 @@ def tile_involution_kernel(
 
             def multiply(unit):
                 block, taps = taps_of(unit)
-                if is_gpsimds(unit):
-                    prod = prod_pool.tile([P, UNIT_TAPS, CH, BLOCK_PIX], F32, name="gpsimd_prod")
-                    row, col = divmod(taps[0], KS)
-                    begin = (block * BLOCK_ROWS + row) * W
-                    n = COPY_COLS.index(col)
-                    nc.gpsimd.tensor_tensor(
-                        out=prod[:],
-                        in0=exp_of[unit][:].unsqueeze(2).to_broadcast([P, UNIT_TAPS, CH, BLOCK_PIX]),
-                        in1=x_cols[:, n : n + UNIT_TAPS, :, begin : begin + BLOCK_PIX],
-                        op=MULT,
-                    )
-                else:
-                    prod = prod_pool.tile([P, UNIT_TAPS, CH, BLOCK_PIX], F32, name="vector_prod")
-                    for i, tap in enumerate(taps):
-                        offset = (tap // KS) * ROW + (LEFT - PAD) + tap % KS
-                        exp_img = exp_of[unit][:, i, :].rearrange("p (h w) -> p h w", w=W).unsqueeze(1)
+                for i, tap in enumerate(taps):
+                    prod = prod_pool.tile([P, CH, BLOCK_PIX], F32, name="prod")
+                    offset = (tap // KS) * ROW + (LEFT - PAD) + tap % KS
+                    exp_img = exp_of[unit][:, i, :].rearrange("p (h w) -> p h w", w=W).unsqueeze(1)
+                    if is_gpsimds(unit, i):
+                        base = block * BLOCK_ROWS * ROW + offset
+                        nc.gpsimd.tensor_tensor(
+                            out=prod[:].rearrange("p c (h w) -> p c h w", w=W),
+                            in0=exp_img.to_broadcast([P, CH, BLOCK_ROWS, W]),
+                            in1=x_pad_f32[:, :, base : base + BLOCK_ROWS * ROW].rearrange(
+                                "p c (h w) -> p c h w", w=ROW
+                            )[:, :, :, :W],
+                            op=MULT,
+                        )
+                    else:
                         for pair in range(CH // 2):
                             nc.vector.tensor_tensor(
-                                out=prod[:, i, 2 * pair : 2 * pair + 2, :].rearrange(
-                                    "p c (h w) -> p c h w", w=W
-                                ),
+                                out=prod[:, 2 * pair : 2 * pair + 2, :].rearrange("p c (h w) -> p c h w", w=W),
                                 in0=window_of[pair][:, :, offset : offset + BLOCK_ROWS * ROW].rearrange(
                                     "p c (h w) -> p c h w", w=ROW
                                 )[:, :, :, :W],
                                 in1=exp_img.to_broadcast([P, 2, BLOCK_ROWS, W]),
                                 op=MULT,
                             )
-                prod_of[unit] = prod
+                    prod_of[unit, i] = prod
 
             def add_exps(unit):
                 block, taps = taps_of(unit)
@@ -417,25 +390,24 @@ def tile_involution_kernel(
                             is_transpose=True,
                         )
 
-            def add_products(unit):
-                block, taps = taps_of(unit)
-                in_block = [u for u in adding_order if u // UNITS == block]
-                opens, closes = unit == in_block[0], unit == in_block[-1]
+            def add_products(unit, i):
+                block = unit // UNITS
+                in_block = [tap for tap in adding_order if tap[0] // UNITS == block]
+                opens, closes = (unit, i) == in_block[0], (unit, i) == in_block[-1]
                 if opens:
                     for j in range(BLOCK_TILES):
                         sums = psum_sums.tile([P, CH, GROUPS], F32, tag="sums", name="sums")
                         sums_of[block, j] = sums
                 for j in range(BLOCK_TILES):
-                    for i in range(len(taps)):
-                        for c in range(CH):
-                            nc.tensor.matmul(
-                                out=sums_of[block, j][:, c, :],
-                                lhsT=prod_of[unit][:, i, c, j * P : (j + 1) * P],
-                                rhs=ident_f32[:],
-                                start=(opens and i == 0 and c == 0),
-                                stop=(closes and i == len(taps) - 1 and c == CH - 1),
-                                is_transpose=True,
-                            )
+                    for c in range(CH):
+                        nc.tensor.matmul(
+                            out=sums_of[block, j][:, c, :],
+                            lhsT=prod_of[unit, i][:, c, j * P : (j + 1) * P],
+                            rhs=ident_f32[:],
+                            start=(opens and c == 0),
+                            stop=(closes and c == CH - 1),
+                            is_transpose=True,
+                        )
 
             def invert(block):
                 inverse = out_pool.tile([P, BLOCK_TILES, GROUPS], F32, name="inverse")
@@ -479,7 +451,7 @@ def tile_involution_kernel(
                 subtract(unit)
                 exponentiate(unit)
 
-        prod_pool = stack.enter_context(tc.tile_pool(name="products", bufs=3))
+        prod_pool = stack.enter_context(tc.tile_pool(name="products", bufs=12))
         out_pool = stack.enter_context(tc.tile_pool(name="results", bufs=2))
 
         divided = None
@@ -497,12 +469,12 @@ def tile_involution_kernel(
                 make_kern(sweep + 1)
             if unit + 1 < N_UNITS:
                 add_exps(unit + 1)
-            while adding and added_at(adding[0]) <= unit:
+            while adding and added_at(*adding[0]) <= unit and done is None:
                 added = adding[0]
                 adding = adding[1:]
-                add_products(added)
-                if not adding or adding[0] // UNITS > added // UNITS:
-                    done = added // UNITS
+                add_products(*added)
+                if not adding or adding[0][0] // UNITS > added[0] // UNITS:
+                    done = added[0] // UNITS
             if unit < N_UNITS and v > 0:
                 multiply(unit)
             if unit + LEAD < N_UNITS:
@@ -515,9 +487,6 @@ def tile_involution_kernel(
                 multiply(unit)
             if unit + 1 < N_UNITS and (unit + 1) % UNITS == UNITS - 1:
                 invert((unit + 1) // UNITS)
-            if 1 <= unit <= CH * len(COPY_COLS):
-                index, c = divmod(unit - 1, CH)
-                copy_columns(nc.scalar.copy, COPY_COLS[index], slice(c, c + 1), FIRST_ROWS, PAD_ROWS)
             if divided is not None:
                 store(divided)
                 divided = None

@@ -49,6 +49,7 @@ LAG = max(VECTOR_LAG, GPSIMD_LAG)
 VECTOR_UNITS = [{UNITS - 1}] * (N_BLOCKS - 1) + [{6, 12, 18, UNITS - 1}]
 LEAD = 2
 SWEEP_LEAD = UNITS + 3
+CHAINS = 2
 FIRST_AHEAD = 3
 G_CHUNKS = 4
 G_CHUNK = GROUPS // G_CHUNKS
@@ -104,9 +105,9 @@ def tile_involution_kernel(
             span_bias_f32 = keep.tile([P, TAPS], F32)
             red = start.tile([P, PACK, PIX], BF16)
             red_grouped = start.tile([P, PIX, PACK], BF16, align_bytes=64)
+            bias_step = {n: keep.tile([P, TAPS], F32, name="bias_step_%d" % n) for n in (1, CHAINS)}
             red_words = keep.tile([P, PIX], U32, align_bytes=64)
             red_plane = keep.tile([P, PIX], U8, align_bytes=64)
-            x_pad_f32 = keep.tile([P, CH, CH_LEN], F32)
             ident_f32 = keep.tile([P, P], F32)
             ident_bf16 = keep.tile([P, P], BF16)
             warm = keep.tile([P, 1], F32)
@@ -157,6 +158,10 @@ def tile_involution_kernel(
             nc.vector.tensor_copy(out=reduce_plane[:], in_=reduce_raw_plane[:].rearrange("p (m t) -> p t m", t=PACK))
             nc.vector.tensor_copy(out=reduce_bias_f32[:], in_=reduce_bias[:])
             nc.vector.tensor_copy(out=span_bias_f32[:], in_=span_bias[:])
+            for chains, step in bias_step.items():
+                nc.vector.tensor_tensor(
+                    out=step[:, chains:], in0=span_bias_f32[:, : TAPS - chains], in1=span_bias_f32[:, chains:], op=SUB
+                )
 
             def project(psum, tag, t, half):
                 red_ps = psum.tile([P, HALF], F32, tag=tag, name="red_ps")
@@ -224,10 +229,6 @@ def tile_involution_kernel(
             group_red(nc.scalar.copy, halves[1])
             reorder_words(3)
 
-            nc.gpsimd.tensor_scalar(
-                out=x_pad_f32[:], in0=x_pad[:], scalar1=1.0, scalar2=0.0, op0=MULT, op1=ADD
-            )
-
             kern_of = {}
             logit_of = {}
             tops_of = {}
@@ -276,9 +277,8 @@ def tile_involution_kernel(
                 kern_of[unit] = kern
 
             def keep_logits(unit):
-                block, taps = taps_of(unit)
                 logits = logit_pool.tile([P, UNIT_TAPS, BLOCK_PIX], F32, name="logits")
-                for i, tap in enumerate(taps):
+                for i, tap in enumerate(taps_of(unit)[1]):
                     nc.scalar.activation(
                         out=logits[:, i, :],
                         in_=kern_of[unit][:, i, :],
@@ -287,23 +287,39 @@ def tile_involution_kernel(
                     )
                 logit_of[unit] = logits
 
-            def take_max(unit):
+            def take_max(unit, i):
                 block, taps = taps_of(unit)
-                for i, tap in enumerate(taps):
-                    kern = kern_of[unit][:, i, :]
-                    bias = span_bias_f32[:, tap : tap + 1]
-                    if unit % UNITS == 0:
-                        top = max_pool.tile([P, BLOCK_PIX], F32, name="top")
-                        tops_of[block, i] = top
-                        nc.vector.tensor_scalar(out=top[:], in0=kern, scalar1=bias, scalar2=None, op0=ADD)
-                    else:
-                        top = tops_of[block, i]
-                        nc.vector.scalar_tensor_tensor(
-                            out=top[:], in0=kern, scalar=bias, in1=top[:], op0=ADD, op1=MAX
-                        )
-                if unit % UNITS == UNITS - 1:
-                    nc.vector.tensor_tensor(
-                        out=tops_of[block, 0][:], in0=tops_of[block, 0][:], in1=tops_of[block, 1][:], op=MAX
+                tap, kern = taps[i], kern_of[unit][:, i, :]
+                if tap < CHAINS:
+                    top = max_pool.tile([P, BLOCK_PIX], F32, name="top")
+                    tops_of[block, tap] = top
+                    nc.vector.tensor_copy(out=top[:], in_=kern)
+                else:
+                    top = tops_of[block, tap % CHAINS]
+                    nc.vector.scalar_tensor_tensor(
+                        out=top[:],
+                        in0=top[:],
+                        scalar=bias_step[CHAINS][:, tap : tap + 1],
+                        in1=kern,
+                        op0=ADD,
+                        op1=MAX,
+                    )
+                if tap == TAPS - 1:
+                    top = tops_of[block, 0]
+                    nc.vector.scalar_tensor_tensor(
+                        out=top[:],
+                        in0=tops_of[block, 1][:],
+                        scalar=bias_step[1][:, tap : tap + 1],
+                        in1=top[:],
+                        op0=ADD,
+                        op1=MAX,
+                    )
+                    nc.vector.tensor_scalar(
+                        out=top[:],
+                        in0=top[:],
+                        scalar1=span_bias_f32[:, tap : tap + 1],
+                        scalar2=None,
+                        op0=ADD,
                     )
 
             def load_top(block):
@@ -356,7 +372,7 @@ def tile_involution_kernel(
                         nc.gpsimd.tensor_tensor(
                             out=prod[:].rearrange("p c (h w) -> p c h w", w=W),
                             in0=exp_img.to_broadcast([P, CH, BLOCK_ROWS, W]),
-                            in1=x_pad_f32[:, :, base : base + BLOCK_ROWS * ROW].rearrange(
+                            in1=x_pad[:, :, base : base + BLOCK_ROWS * ROW].rearrange(
                                 "p c (h w) -> p c h w", w=ROW
                             )[:, :, :, :W],
                             op=MULT,
@@ -365,10 +381,10 @@ def tile_involution_kernel(
                         for pair in range(CH // 2):
                             nc.vector.tensor_tensor(
                                 out=prod[:, 2 * pair : 2 * pair + 2, :].rearrange("p c (h w) -> p c h w", w=W),
-                                in0=window_of[pair][:, :, offset : offset + BLOCK_ROWS * ROW].rearrange(
+                                in0=exp_img.to_broadcast([P, 2, BLOCK_ROWS, W]),
+                                in1=window_of[pair][:, :, offset : offset + BLOCK_ROWS * ROW].rearrange(
                                     "p c (h w) -> p c h w", w=ROW
                                 )[:, :, :, :W],
-                                in1=exp_img.to_broadcast([P, 2, BLOCK_ROWS, W]),
                                 op=MULT,
                             )
                     prod_of[unit, i] = prod
@@ -443,7 +459,8 @@ def tile_involution_kernel(
                     quantise(red_words, red_plane, red_grouped, halves[1])
                 if unit + FIRST_AHEAD <= SWEEP_LEAD:
                     make_kern(unit + FIRST_AHEAD)
-                take_max(unit)
+                for i in range(len(taps_of(unit)[1])):
+                    take_max(unit, i)
                 keep_logits(unit)
                 if unit == UNITS - 1:
                     load_top(0)
@@ -481,7 +498,8 @@ def tile_involution_kernel(
                 subtract(unit + LEAD)
                 exponentiate(unit + LEAD)
             if sweep < N_UNITS:
-                take_max(sweep)
+                for i in range(len(taps_of(sweep)[1])):
+                    take_max(sweep, i)
                 keep_logits(sweep)
             if unit < N_UNITS and v == 0:
                 multiply(unit)

@@ -46,10 +46,10 @@ N_UNITS = N_BLOCKS * UNITS
 VECTOR_LAG = 2
 GPSIMD_LAG = 3
 LAG = max(VECTOR_LAG, GPSIMD_LAG)
-VECTOR_UNITS = [{UNITS - 1}] * (N_BLOCKS - 1) + [{6, 12, 18, UNITS - 1}]
+VECTOR_UNITS = [{12}, {8, 16}, {8, 16}, {3, 7, 11, 15, 19, 22}]
 LEAD = 2
 SWEEP_LEAD = UNITS + 3
-CHAINS = 2
+EDGE_TILES = {"vector": 4, "gpsimd": 5}
 FIRST_AHEAD = 3
 G_CHUNKS = 4
 G_CHUNK = GROUPS // G_CHUNKS
@@ -105,7 +105,10 @@ def tile_involution_kernel(
             span_bias_f32 = keep.tile([P, TAPS], F32)
             red = start.tile([P, PACK, PIX], BF16)
             red_grouped = start.tile([P, PIX, PACK], BF16, align_bytes=64)
-            bias_step = {n: keep.tile([P, TAPS], F32, name="bias_step_%d" % n) for n in (1, CHAINS)}
+            bias_step = {
+                d: {n: keep.tile([P, TAPS], F32, name="bias_step_%d_%d" % (d + 1, n)) for n in (1, UNIT_TAPS)}
+                for d in (1, -1)
+            }
             red_words = keep.tile([P, PIX], U32, align_bytes=64)
             red_plane = keep.tile([P, PIX], U8, align_bytes=64)
             ident_f32 = keep.tile([P, P], F32)
@@ -158,10 +161,10 @@ def tile_involution_kernel(
             nc.vector.tensor_copy(out=reduce_plane[:], in_=reduce_raw_plane[:].rearrange("p (m t) -> p t m", t=PACK))
             nc.vector.tensor_copy(out=reduce_bias_f32[:], in_=reduce_bias[:])
             nc.vector.tensor_copy(out=span_bias_f32[:], in_=span_bias[:])
-            for chains, step in bias_step.items():
-                nc.vector.tensor_tensor(
-                    out=step[:, chains:], in0=span_bias_f32[:, : TAPS - chains], in1=span_bias_f32[:, chains:], op=SUB
-                )
+            for n in (1, UNIT_TAPS):
+                lower, upper = span_bias_f32[:, : TAPS - n], span_bias_f32[:, n:]
+                nc.vector.tensor_tensor(out=bias_step[1][n][:, n:], in0=lower, in1=upper, op=SUB)
+                nc.vector.tensor_tensor(out=bias_step[-1][n][:, : TAPS - n], in0=upper, in1=lower, op=SUB)
 
             def project(psum, tag, t, half):
                 red_ps = psum.tile([P, HALF], F32, tag=tag, name="red_ps")
@@ -205,11 +208,6 @@ def tile_involution_kernel(
             relu_on_scalar(first[2], 2, halves[0])
             relu_on_scalar(first[3], 3, halves[0])
             group_x(nc.scalar.copy, halves[1])
-            for c in range(CH):
-                nc.scalar.copy(
-                    out=x_pad[:, c, PAD * ROW : (PAD + H) * ROW].rearrange("p (h w) -> p h w", w=ROW)[:, :, LEFT:],
-                    in_=x_sb[:, c, :].rearrange("p (h w) -> p h w", w=W),
-                )
 
             def reorder_words(chunk):
                 groups = slice(chunk * G_CHUNK, (chunk + 1) * G_CHUNK)
@@ -226,8 +224,25 @@ def tile_involution_kernel(
             reorder_words(2)
             for t in range(PACK):
                 relu_on_scalar(project(psum_sums, "sums", t, halves[1]), t, halves[1])
-            group_red(nc.scalar.copy, halves[1])
             reorder_words(3)
+
+            def gpsimd_copy(out, in_):
+                nc.gpsimd.tensor_scalar(out=out, in0=in_, scalar1=1.0, scalar2=0.0, op0=MULT, op1=ADD)
+
+            gpsimd_copy(
+                out=x_pad[:, :, PAD * ROW : (PAD + H) * ROW].rearrange("p c (h w) -> p c h w", w=ROW)[:, :, :, LEFT:],
+                in_=x_sb[:].rearrange("p c (h w) -> p c h w", w=W),
+            )
+            group_red(gpsimd_copy, halves[1])
+            edge_prods = {
+                engine: [keep.tile([P, CH, BLOCK_PIX], F32, name="%s_edge_%d" % (engine, n)) for n in range(count)]
+                for engine, count in EDGE_TILES.items()
+            }
+            zeros = keep.tile([P, CH, PAD * W], F32)
+            nc.gpsimd.memset(zeros[:], 0.0)
+            for tiles in edge_prods.values():
+                for prod in tiles:
+                    nc.gpsimd.memset(prod[:, :, : PAD * W], 0.0)
 
             kern_of = {}
             logit_of = {}
@@ -241,13 +256,24 @@ def tile_involution_kernel(
             inverse_of = {}
             scaled_of = {}
 
+            def direction(block):
+                return -1 if block == N_BLOCKS - 1 else 1
+
             def taps_of(unit):
                 block, v = divmod(unit, UNITS)
-                return block, range(UNIT_TAPS * v, min(UNIT_TAPS * (v + 1), TAPS))
+                order = list(range(TAPS))[:: direction(block)]
+                return block, order[UNIT_TAPS * v : UNIT_TAPS * (v + 1)]
+
+            def live_rows(block, tap):
+                shift = tap // KS - PAD
+                return (
+                    max(0, -shift - block * BLOCK_ROWS),
+                    min(BLOCK_ROWS, H - shift - block * BLOCK_ROWS),
+                )
 
             def is_gpsimds(unit, i):
                 block, v = divmod(unit, UNITS)
-                return i == 0 and v not in VECTOR_UNITS[block]
+                return i == 0 and v != UNITS - 1 and v not in VECTOR_UNITS[block]
 
             def added_at(unit, i):
                 return unit + (GPSIMD_LAG if is_gpsimds(unit, i) else VECTOR_LAG)
@@ -290,26 +316,27 @@ def tile_involution_kernel(
             def take_max(unit, i):
                 block, taps = taps_of(unit)
                 tap, kern = taps[i], kern_of[unit][:, i, :]
-                if tap < CHAINS:
+                v = unit % UNITS
+                steps = bias_step[direction(block)]
+                if v == 0:
                     top = max_pool.tile([P, BLOCK_PIX], F32, name="top")
-                    tops_of[block, tap] = top
+                    tops_of[block, i] = top
                     nc.vector.tensor_copy(out=top[:], in_=kern)
                 else:
-                    top = tops_of[block, tap % CHAINS]
+                    top = tops_of[block, i]
                     nc.vector.scalar_tensor_tensor(
                         out=top[:],
                         in0=top[:],
-                        scalar=bias_step[CHAINS][:, tap : tap + 1],
+                        scalar=steps[UNIT_TAPS][:, tap : tap + 1],
                         in1=kern,
                         op0=ADD,
                         op1=MAX,
                     )
-                if tap == TAPS - 1:
-                    top = tops_of[block, 0]
+                if v == UNITS - 1:
                     nc.vector.scalar_tensor_tensor(
                         out=top[:],
                         in0=tops_of[block, 1][:],
-                        scalar=bias_step[1][:, tap : tap + 1],
+                        scalar=steps[1][:, tap : tap + 1],
                         in1=top[:],
                         op0=ADD,
                         op1=MAX,
@@ -364,27 +391,37 @@ def tile_involution_kernel(
             def multiply(unit):
                 block, taps = taps_of(unit)
                 for i, tap in enumerate(taps):
-                    prod = prod_pool.tile([P, CH, BLOCK_PIX], F32, name="prod")
-                    offset = (tap // KS) * ROW + (LEFT - PAD) + tap % KS
-                    exp_img = exp_of[unit][:, i, :].rearrange("p (h w) -> p h w", w=W).unsqueeze(1)
-                    if is_gpsimds(unit, i):
-                        base = block * BLOCK_ROWS * ROW + offset
+                    engine = "gpsimd" if is_gpsimds(unit, i) else "vector"
+                    row0, row1 = live_rows(block, tap)
+                    if row1 - row0 == BLOCK_ROWS:
+                        prod = prod_pool.tile([P, CH, BLOCK_PIX], F32, name="prod")
+                    else:
+                        prod = edge_prods[engine][0]
+                        edge_prods[engine] = edge_prods[engine][1:] + [prod]
+                    pixels = slice(row0 * W, row1 * W)
+                    offset = (tap // KS + row0) * ROW + (LEFT - PAD) + tap % KS
+                    exp_img = exp_of[unit][:, i, pixels].rearrange("p (h w) -> p h w", w=W).unsqueeze(1)
+
+                    def window(rows, begin):
+                        return rows[:, :, begin : begin + (row1 - row0) * ROW].rearrange(
+                            "p c (h w) -> p c h w", w=ROW
+                        )[:, :, :, :W]
+
+                    if engine == "gpsimd":
                         nc.gpsimd.tensor_tensor(
-                            out=prod[:].rearrange("p c (h w) -> p c h w", w=W),
-                            in0=exp_img.to_broadcast([P, CH, BLOCK_ROWS, W]),
-                            in1=x_pad[:, :, base : base + BLOCK_ROWS * ROW].rearrange(
-                                "p c (h w) -> p c h w", w=ROW
-                            )[:, :, :, :W],
+                            out=prod[:, :, pixels].rearrange("p c (h w) -> p c h w", w=W),
+                            in0=exp_img.to_broadcast([P, CH, row1 - row0, W]),
+                            in1=window(x_pad, block * BLOCK_ROWS * ROW + offset),
                             op=MULT,
                         )
                     else:
                         for pair in range(CH // 2):
                             nc.vector.tensor_tensor(
-                                out=prod[:, 2 * pair : 2 * pair + 2, :].rearrange("p c (h w) -> p c h w", w=W),
-                                in0=exp_img.to_broadcast([P, 2, BLOCK_ROWS, W]),
-                                in1=window_of[pair][:, :, offset : offset + BLOCK_ROWS * ROW].rearrange(
-                                    "p c (h w) -> p c h w", w=ROW
-                                )[:, :, :, :W],
+                                out=prod[:, 2 * pair : 2 * pair + 2, pixels].rearrange(
+                                    "p c (h w) -> p c h w", w=W
+                                ),
+                                in0=exp_img.to_broadcast([P, 2, row1 - row0, W]),
+                                in1=window(window_of[pair], offset),
                                 op=MULT,
                             )
                     prod_of[unit, i] = prod
@@ -505,6 +542,9 @@ def tile_involution_kernel(
                 multiply(unit)
             if unit + 1 < N_UNITS and (unit + 1) % UNITS == UNITS - 1:
                 invert((unit + 1) // UNITS)
+            tiles = edge_prods["vector"] + edge_prods["gpsimd"]
+            if UNITS <= unit < UNITS + len(tiles):
+                nc.scalar.copy(out=tiles[unit - UNITS][:, :, BLOCK_PIX - PAD * W :], in_=zeros[:])
             if divided is not None:
                 store(divided)
                 divided = None

@@ -46,14 +46,15 @@ N_UNITS = N_BLOCKS * UNITS
 VECTOR_LAG = 2
 GPSIMD_LAG = 3
 LAG = max(VECTOR_LAG, GPSIMD_LAG)
-VECTOR_UNITS = [{12}, {8, 16}, {8, 16}, {3, 7, 11, 15, 19, 22}]
+VECTOR_UNITS = [{12}, {8, 16}, {8, 16}, {4, 8, 12, 16, 20}]
 LEAD = 2
 SWEEP_LEAD = UNITS + 3
-EDGE_TILES = {"vector": 4, "gpsimd": 5}
+EDGE_TILES = {"vector": 5, "gpsimd": 6}
 FIRST_AHEAD = 3
 G_CHUNKS = 4
 G_CHUNK = GROUPS // G_CHUNKS
-PLANE_SPLIT = 7
+PLANE_SPLIT = 14
+PLANE_TURN = 7
 
 FLOPS = 2 * PIX * (C * R + R * O) + 2 * TAPS * C * PIX
 
@@ -88,7 +89,7 @@ def tile_involution_kernel(
         with tc.tile_pool(name="start", bufs=1) as start:
             x_sb = start.tile([P, CH, PIX], BF16)
             x_pad = keep.tile([P, CH, CH_LEN], BF16)
-            x_grouped = start.tile([P, PIX, PACK], BF16, align_bytes=64)
+            grouped = start.tile([P, PIX, PACK], BF16, align_bytes=64)
             x_words = start.tile([P, PIX], U32, align_bytes=64)
             x_plane = start.tile([P, PIX], U8, align_bytes=64)
             reduce_raw = start.tile([P, R], I32, align_bytes=64)
@@ -104,7 +105,7 @@ def tile_involution_kernel(
             span_bias = keep.tile([P, TAPS], BF16)
             span_bias_f32 = keep.tile([P, TAPS], F32)
             red = start.tile([P, PACK, PIX], BF16)
-            red_grouped = start.tile([P, PIX, PACK], BF16, align_bytes=64)
+            minus_bias = keep.tile([P, TAPS], F32)
             bias_step = {
                 d: {n: keep.tile([P, TAPS], F32, name="bias_step_%d_%d" % (d + 1, n)) for n in (1, UNIT_TAPS)}
                 for d in (1, -1)
@@ -114,9 +115,12 @@ def tile_involution_kernel(
             ident_f32 = keep.tile([P, P], F32)
             ident_bf16 = keep.tile([P, P], BF16)
             warm = keep.tile([P, 1], F32)
+            after_words = keep.tile([P, 1], I32)
 
             nc.vector.memset(reduce_raw_plane[:].bitcast(I32), 0)
             nc.vector.memset(span_raw_plane[:].bitcast(I32), 0)
+            zeros = keep.tile([P, CH, PAD * W], F32)
+            nc.vector.memset(zeros[:], 0.0)
             halves = [slice(0, HALF), slice(HALF, PIX)]
             nc.sync.dma_start(out=x_sb[:, :, halves[0]], in_=x_by_group[:, :, halves[0]])
             nc.sync.dma_start(
@@ -135,18 +139,21 @@ def tile_involution_kernel(
 
             nc.gpsimd.memset(x_pad[:].rearrange("p c n -> p (c n)").bitcast(I32), 0)
             span_plane_by_tap = span_raw_plane[:].rearrange("p (g t) -> p t g", t=TAPS)
-            for tap in range(0, TAPS, PLANE_SPLIT):
-                nc.gpsimd.tensor_copy(
-                    out=span_plane[:, tap : tap + PLANE_SPLIT, :],
-                    in_=span_plane_by_tap[:, tap : tap + PLANE_SPLIT, :],
-                )
             make_identity(nc, ident_bf16[:])
             make_identity(nc, ident_f32[:])
             nc.vector.memset(warm[:], 0.0)
             nc.scalar.activation(out=warm[:], in_=warm[:], func=EXP)
 
+            edge_prods = {
+                engine: [keep.tile([P, CH, BLOCK_PIX], F32, name="%s_edge_%d" % (engine, n)) for n in range(count)]
+                for engine, count in EDGE_TILES.items()
+            }
+            for tiles in edge_prods.values():
+                for prod in tiles:
+                    nc.scalar.copy(out=prod[:, :, : PAD * W], in_=zeros[:])
+
             def group_x(copy, half):
-                copy(out=x_grouped[:, half, :], in_=x_sb[:, :, half].rearrange("p t w -> p w t"))
+                copy(out=grouped[:, half, :], in_=x_sb[:, :, half].rearrange("p t w -> p w t"))
 
             def quantise(words, plane, grouped, half):
                 nc.vector.quantize_mx(
@@ -157,10 +164,11 @@ def tile_involution_kernel(
 
             group_x(nc.vector.tensor_copy, halves[0])
             nc.vector.tensor_copy(out=reduce_words[:], in_=reduce_raw[:].rearrange("p (m t) -> p t m", t=PACK))
-            quantise(x_words, x_plane, x_grouped, halves[0])
+            quantise(x_words, x_plane, grouped, halves[0])
             nc.vector.tensor_copy(out=reduce_plane[:], in_=reduce_raw_plane[:].rearrange("p (m t) -> p t m", t=PACK))
             nc.vector.tensor_copy(out=reduce_bias_f32[:], in_=reduce_bias[:])
             nc.vector.tensor_copy(out=span_bias_f32[:], in_=span_bias[:])
+            nc.vector.tensor_scalar_mul(out=minus_bias[:], in0=span_bias_f32[:], scalar1=-1.0)
             for n in (1, UNIT_TAPS):
                 lower, upper = span_bias_f32[:, : TAPS - n], span_bias_f32[:, n:]
                 nc.vector.tensor_tensor(out=bias_step[1][n][:, n:], in0=lower, in1=upper, op=SUB)
@@ -195,7 +203,7 @@ def tile_involution_kernel(
                 )
 
             def group_red(copy, pixels):
-                copy(out=red_grouped[:, pixels, :], in_=red[:, :, pixels].rearrange("p t w -> p w t"))
+                copy(out=grouped[:, pixels, :], in_=red[:, :, pixels].rearrange("p t w -> p w t"))
 
             first = [
                 project(psum_sums, "sums", 0, halves[0]),
@@ -208,6 +216,11 @@ def tile_involution_kernel(
             relu_on_scalar(first[2], 2, halves[0])
             relu_on_scalar(first[3], 3, halves[0])
             group_x(nc.scalar.copy, halves[1])
+            for c in range(CH):
+                nc.scalar.copy(
+                    out=x_pad[:, c, PAD * ROW : (PAD + H) * ROW].rearrange("p (h w) -> p h w", w=ROW)[:, :, LEFT:],
+                    in_=x_sb[:, c, :].rearrange("p (h w) -> p h w", w=W),
+                )
 
             def reorder_words(chunk):
                 groups = slice(chunk * G_CHUNK, (chunk + 1) * G_CHUNK)
@@ -219,30 +232,21 @@ def tile_involution_kernel(
             reorder_words(0)
             group_red(nc.vector.tensor_copy, halves[0])
             reorder_words(1)
-            quantise(red_words, red_plane, red_grouped, halves[0])
-            quantise(x_words, x_plane, x_grouped, halves[1])
+            quantise(red_words, red_plane, grouped, halves[0])
+            quantise(x_words, x_plane, grouped, halves[1])
             reorder_words(2)
             for t in range(PACK):
                 relu_on_scalar(project(psum_sums, "sums", t, halves[1]), t, halves[1])
+            group_red(nc.scalar.copy, halves[1])
+            nc.vector.tensor_copy(out=span_plane[:, :PLANE_SPLIT, :], in_=span_plane_by_tap[:, :PLANE_SPLIT, :])
             reorder_words(3)
 
-            def gpsimd_copy(out, in_):
-                nc.gpsimd.tensor_scalar(out=out, in0=in_, scalar1=1.0, scalar2=0.0, op0=MULT, op1=ADD)
-
-            gpsimd_copy(
-                out=x_pad[:, :, PAD * ROW : (PAD + H) * ROW].rearrange("p c (h w) -> p c h w", w=ROW)[:, :, :, LEFT:],
-                in_=x_sb[:].rearrange("p c (h w) -> p c h w", w=W),
-            )
-            group_red(gpsimd_copy, halves[1])
-            edge_prods = {
-                engine: [keep.tile([P, CH, BLOCK_PIX], F32, name="%s_edge_%d" % (engine, n)) for n in range(count)]
-                for engine, count in EDGE_TILES.items()
-            }
-            zeros = keep.tile([P, CH, PAD * W], F32)
-            nc.gpsimd.memset(zeros[:], 0.0)
-            for tiles in edge_prods.values():
-                for prod in tiles:
-                    nc.gpsimd.memset(prod[:, :, : PAD * W], 0.0)
+            nc.gpsimd.tensor_copy(out=after_words[:], in_=span_words[:, TAPS - 1, GROUPS - 1 :])
+            for tap in range(PLANE_SPLIT, TAPS, PLANE_TURN):
+                nc.gpsimd.tensor_copy(
+                    out=span_plane[:, tap : tap + PLANE_TURN, :],
+                    in_=span_plane_by_tap[:, tap : tap + PLANE_TURN, :],
+                )
 
             kern_of = {}
             logit_of = {}
@@ -317,22 +321,23 @@ def tile_involution_kernel(
                 block, taps = taps_of(unit)
                 tap, kern = taps[i], kern_of[unit][:, i, :]
                 v = unit % UNITS
+                chains = UNIT_TAPS if block == 0 else 1
                 steps = bias_step[direction(block)]
-                if v == 0:
+                if v == 0 and i < chains:
                     top = max_pool.tile([P, BLOCK_PIX], F32, name="top")
                     tops_of[block, i] = top
                     nc.vector.tensor_copy(out=top[:], in_=kern)
                 else:
-                    top = tops_of[block, i]
+                    top = tops_of[block, i % chains]
                     nc.vector.scalar_tensor_tensor(
                         out=top[:],
                         in0=top[:],
-                        scalar=steps[UNIT_TAPS][:, tap : tap + 1],
+                        scalar=steps[chains][:, tap : tap + 1],
                         in1=kern,
                         op0=ADD,
                         op1=MAX,
                     )
-                if v == UNITS - 1:
+                if v == UNITS - 1 and chains > 1:
                     nc.vector.scalar_tensor_tensor(
                         out=top[:],
                         in0=tops_of[block, 1][:],
@@ -340,13 +345,6 @@ def tile_involution_kernel(
                         in1=top[:],
                         op0=ADD,
                         op1=MAX,
-                    )
-                    nc.vector.tensor_scalar(
-                        out=top[:],
-                        in0=top[:],
-                        scalar1=span_bias_f32[:, tap : tap + 1],
-                        scalar2=None,
-                        op0=ADD,
                     )
 
             def load_top(block):
@@ -371,7 +369,13 @@ def tile_involution_kernel(
                 block, taps = taps_of(unit)
                 n = len(taps)
                 exps = exp_pool.tile([P, UNIT_TAPS, BLOCK_PIX], F32, name="exps")
-                nc.scalar.activation(out=exps[:, :n, :], in_=logit_of[unit][:, :n, :], func=EXP)
+                last = taps_of(block * UNITS + UNITS - 1)[1][-1]
+                nc.scalar.activation(
+                    out=exps[:, :n, :],
+                    in_=logit_of[unit][:, :n, :],
+                    func=EXP,
+                    bias=minus_bias[:, last : last + 1],
+                )
                 exp_of[unit] = exps
 
             def load_window(block):
@@ -493,7 +497,7 @@ def tile_involution_kernel(
                 make_kern(unit)
             for unit in range(SWEEP_LEAD):
                 if unit == 8:
-                    quantise(red_words, red_plane, red_grouped, halves[1])
+                    quantise(red_words, red_plane, grouped, halves[1])
                 if unit + FIRST_AHEAD <= SWEEP_LEAD:
                     make_kern(unit + FIRST_AHEAD)
                 for i in range(len(taps_of(unit)[1])):
@@ -531,12 +535,14 @@ def tile_involution_kernel(
                     done = added[0] // UNITS
             if unit < N_UNITS and v > 0:
                 multiply(unit)
+            if sweep < N_UNITS:
+                take_max(sweep, 0)
             if unit + LEAD < N_UNITS:
                 subtract(unit + LEAD)
                 exponentiate(unit + LEAD)
             if sweep < N_UNITS:
-                for i in range(len(taps_of(sweep)[1])):
-                    take_max(sweep, i)
+                if len(taps_of(sweep)[1]) > 1:
+                    take_max(sweep, 1)
                 keep_logits(sweep)
             if unit < N_UNITS and v == 0:
                 multiply(unit)

@@ -46,7 +46,7 @@ N_UNITS = N_BLOCKS * UNITS
 VECTOR_LAG = 2
 GPSIMD_LAG = 3
 LAG = max(VECTOR_LAG, GPSIMD_LAG)
-VECTOR_UNITS = [{12}, {8, 16}, {8, 16}, {4, 8, 12, 16, 20}]
+VECTOR_UNITS = [{12}, {12}, {12}, {4, 8, 12, 16, 20}]
 LEAD = 2
 SWEEP_LEAD = UNITS + 3
 EDGE_TILES = {"vector": 5, "gpsimd": 6}
@@ -485,7 +485,7 @@ def tile_involution_kernel(
             def store(block):
                 for j in range(BLOCK_TILES):
                     scaled = scaled_of[block, j]
-                    back = psum_kern.tile([P, CH, P], F32, tag="kern", name="back")
+                    back = psum_sums.tile([P, CH, P], F32, tag="sums", name="back")
                     for c in range(CH):
                         nc.tensor.transpose(back[:, c, :], scaled[:, c, :], ident_f32[:])
                     result = out_pool.tile([P, CH, P], F32, name="result")
@@ -527,7 +527,7 @@ def tile_involution_kernel(
                 make_kern(sweep + 1)
             if unit + 1 < N_UNITS:
                 add_exps(unit + 1)
-            while adding and added_at(*adding[0]) <= unit and done is None:
+            while adding and added_at(*adding[0]) <= unit and done is None and divided is None:
                 added = adding[0]
                 adding = adding[1:]
                 add_products(*added)

@@ -47,14 +47,14 @@ VECTOR_LAG = 2
 GPSIMD_LAG = 3
 LAG = max(VECTOR_LAG, GPSIMD_LAG)
 VECTOR_UNITS = [{12}, {12}, {12}, {4, 8, 12, 16, 20}]
-LEAD = 2
+LEAD = 3
 SWEEP_LEAD = UNITS + 3
 EDGE_TILES = {"vector": 5, "gpsimd": 6}
 FIRST_AHEAD = 3
 G_CHUNKS = 4
 G_CHUNK = GROUPS // G_CHUNKS
-PLANE_SPLIT = 14
-PLANE_TURN = 7
+PLANE_SPLIT = 20
+PLANE_TURN = 8
 
 FLOPS = 2 * PIX * (C * R + R * O) + 2 * TAPS * C * PIX
 
@@ -243,10 +243,8 @@ def tile_involution_kernel(
 
             nc.gpsimd.tensor_copy(out=after_words[:], in_=span_words[:, TAPS - 1, GROUPS - 1 :])
             for tap in range(PLANE_SPLIT, TAPS, PLANE_TURN):
-                nc.gpsimd.tensor_copy(
-                    out=span_plane[:, tap : tap + PLANE_TURN, :],
-                    in_=span_plane_by_tap[:, tap : tap + PLANE_TURN, :],
-                )
+                turn = slice(tap, min(tap + PLANE_TURN, TAPS))
+                nc.gpsimd.tensor_copy(out=span_plane[:, turn, :], in_=span_plane_by_tap[:, turn, :])
 
             kern_of = {}
             logit_of = {}
@@ -521,18 +519,10 @@ def tile_involution_kernel(
             done = None
             if unit < N_UNITS and v == 0:
                 load_window(block)
-            if v == UNITS - LEAD and block + 1 < N_BLOCKS:
-                load_top(block + 1)
             if sweep + 1 < N_UNITS:
                 make_kern(sweep + 1)
             if unit + 1 < N_UNITS:
                 add_exps(unit + 1)
-            while adding and added_at(*adding[0]) <= unit and done is None and divided is None:
-                added = adding[0]
-                adding = adding[1:]
-                add_products(*added)
-                if not adding or adding[0][0] // UNITS > added[0] // UNITS:
-                    done = added[0] // UNITS
             if unit < N_UNITS and v > 0:
                 multiply(unit)
             if sweep < N_UNITS:
@@ -546,6 +536,14 @@ def tile_involution_kernel(
                 keep_logits(sweep)
             if unit < N_UNITS and v == 0:
                 multiply(unit)
+            if v == UNITS - 1 - LEAD and block + 1 < N_BLOCKS:
+                load_top(block + 1)
+            while adding and added_at(*adding[0]) <= unit and done is None and divided is None:
+                added = adding[0]
+                adding = adding[1:]
+                add_products(*added)
+                if not adding or adding[0][0] // UNITS > added[0] // UNITS:
+                    done = added[0] // UNITS
             if unit + 1 < N_UNITS and (unit + 1) % UNITS == UNITS - 1:
                 invert((unit + 1) // UNITS)
             tiles = edge_prods["vector"] + edge_prods["gpsimd"]

@@ -46,7 +46,7 @@ N_UNITS = N_BLOCKS * UNITS
 VECTOR_LAG = 2
 GPSIMD_LAG = 3
 LAG = max(VECTOR_LAG, GPSIMD_LAG)
-VECTOR_UNITS = [{12}, {12}, {12}, {4, 8, 12, 16, 20}]
+VECTOR_UNITS = [set(), set(), set(), {4, 8, 12, 16}]
 LEAD = 3
 SWEEP_LEAD = UNITS + 3
 EDGE_TILES = {"vector": 5, "gpsimd": 6}

@@ -45,8 +45,9 @@ UNITS = -(-TAPS // UNIT_TAPS)
 N_UNITS = N_BLOCKS * UNITS
 VECTOR_LAG = 2
 GPSIMD_LAG = 3
-LAG = max(VECTOR_LAG, GPSIMD_LAG)
-VECTOR_UNITS = [set(), set(), set(), {4, 8, 12, 16}]
+LAG = max(VECTOR_LAG, GPSIMD_LAG + 1)
+VECTOR_UNITS = [set(), set(), set(), {6, 12, 18}]
+GPSIMD_UNITS = [{8, 16}, {8, 16}, {8, 16}, set()]
 LEAD = 3
 SWEEP_LEAD = UNITS + 3
 EDGE_TILES = {"vector": 5, "gpsimd": 6}
@@ -275,10 +276,12 @@ def tile_involution_kernel(
 
             def is_gpsimds(unit, i):
                 block, v = divmod(unit, UNITS)
+                if v in GPSIMD_UNITS[block]:
+                    return True
                 return i == 0 and v != UNITS - 1 and v not in VECTOR_UNITS[block]
 
             def added_at(unit, i):
-                return unit + (GPSIMD_LAG if is_gpsimds(unit, i) else VECTOR_LAG)
+                return unit + (GPSIMD_LAG + i if is_gpsimds(unit, i) else VECTOR_LAG)
 
             adding_order = sorted(
                 [(unit, i) for unit in range(N_UNITS) for i in range(len(taps_of(unit)[1]))],

@@ -47,15 +47,15 @@ VECTOR_LAG = 2
 GPSIMD_LAG = 3
 LAG = max(VECTOR_LAG, GPSIMD_LAG + 1)
 VECTOR_UNITS = [set(), set(), set(), {6, 12, 18}]
-GPSIMD_UNITS = [{8, 16}, {8, 16}, {8, 16}, set()]
+GPSIMD_UNITS = [{12}, {12}, {12}, set()]
 LEAD = 3
 SWEEP_LEAD = UNITS + 3
 EDGE_TILES = {"vector": 5, "gpsimd": 6}
 FIRST_AHEAD = 3
 G_CHUNKS = 4
 G_CHUNK = GROUPS // G_CHUNKS
-PLANE_SPLIT = 20
-PLANE_TURN = 8
+PLANE_SPLIT = 28
+PLANE_TURN = 7
 
 FLOPS = 2 * PIX * (C * R + R * O) + 2 * TAPS * C * PIX
 
@@ -216,6 +216,7 @@ def tile_involution_kernel(
             relu_on_vector(first[1], 1, halves[0])
             relu_on_scalar(first[2], 2, halves[0])
             relu_on_scalar(first[3], 3, halves[0])
+            group_red(nc.scalar.copy, halves[0])
             group_x(nc.scalar.copy, halves[1])
             for c in range(CH):
                 nc.scalar.copy(
@@ -231,7 +232,6 @@ def tile_involution_kernel(
                 )
 
             reorder_words(0)
-            group_red(nc.vector.tensor_copy, halves[0])
             reorder_words(1)
             quantise(red_words, red_plane, grouped, halves[0])
             quantise(x_words, x_plane, grouped, halves[1])
@@ -494,21 +494,26 @@ def tile_involution_kernel(
                     pt = block * BLOCK_TILES + j
                     nc.sync.dma_start(out=out_by_group[:, :, pt * P : (pt + 1) * P], in_=result[:])
 
-            for unit in range(FIRST_AHEAD):
-                make_kern(unit)
-            for unit in range(SWEEP_LEAD):
-                if unit == 8:
-                    quantise(red_words, red_plane, grouped, halves[1])
-                if unit + FIRST_AHEAD <= SWEEP_LEAD:
-                    make_kern(unit + FIRST_AHEAD)
+            def sweep_over(unit):
                 for i in range(len(taps_of(unit)[1])):
                     take_max(unit, i)
                 keep_logits(unit)
-                if unit == UNITS - 1:
-                    load_top(0)
-            for unit in range(LEAD):
-                subtract(unit)
-                exponentiate(unit)
+
+            for unit in range(FIRST_AHEAD):
+                make_kern(unit)
+            for unit in range(UNITS):
+                if unit == 8:
+                    quantise(red_words, red_plane, grouped, halves[1])
+                if unit + FIRST_AHEAD <= UNITS:
+                    make_kern(unit + FIRST_AHEAD)
+                sweep_over(unit)
+            load_top(0)
+            for unit in range(UNITS, SWEEP_LEAD):
+                sweep_over(unit)
+                make_kern(unit + 1)
+                if unit - UNITS < LEAD:
+                    subtract(unit - UNITS)
+                    exponentiate(unit - UNITS)
 
         prod_pool = stack.enter_context(tc.tile_pool(name="products", bufs=12))
         out_pool = stack.enter_context(tc.tile_pool(name="results", bufs=2))

@@ -1,4 +1,5 @@
 from contextlib import ExitStack
+from functools import partial
 
 import concourse.mybir as mybir
 from concourse.masks import make_identity
@@ -49,11 +50,15 @@ LAG = max(VECTOR_LAG, GPSIMD_LAG + 1)
 VECTOR_UNITS = [set(), set(), set(), {6, 12, 18}]
 GPSIMD_UNITS = [{12}, {12}, {12}, set()]
 LEAD = 3
-SWEEP_LEAD = UNITS + 3
+SWEEP_LEAD = UNITS + LEAD
+SUB_UNITS = 2
+LOGIT_TILES = SWEEP_LEAD // SUB_UNITS + 2
 EDGE_TILES = {"vector": 5, "gpsimd": 6}
+FIRST_TURNS = 9
 FIRST_AHEAD = 3
 G_CHUNKS = 4
 G_CHUNK = GROUPS // G_CHUNKS
+RUN = 4
 PLANE_SPLIT = 28
 PLANE_TURN = 7
 
@@ -79,7 +84,7 @@ def tile_involution_kernel(
         stack.enter_context(tc.manual_schedule())
         keep = stack.enter_context(tc.tile_pool(name="keep", bufs=1))
         max_pool = stack.enter_context(tc.tile_pool(name="maxima", bufs=4))
-        logit_pool = stack.enter_context(tc.tile_pool(name="logits", bufs=SWEEP_LEAD - LEAD + 4))
+        logit_pool = stack.enter_context(tc.tile_pool(name="logits", bufs=LOGIT_TILES))
         exp_pool = stack.enter_context(tc.tile_pool(name="exps", bufs=LEAD + 4))
         psum_x = stack.enter_context(tc.psum_pool(name="psum_x", bufs=2))
         psum_sums = stack.enter_context(tc.psum_pool(name="psum_sums", bufs=2))
@@ -88,7 +93,7 @@ def tile_involution_kernel(
         psum_top = stack.enter_context(tc.psum_pool(name="psum_top", bufs=1))
 
         with tc.tile_pool(name="start", bufs=1) as start:
-            x_sb = start.tile([P, CH, PIX], BF16)
+            x_sb = [start.tile([P, CH, HALF], BF16, name="x_half_%d" % half) for half in range(2)]
             x_pad = keep.tile([P, CH, CH_LEN], BF16)
             grouped = start.tile([P, PIX, PACK], BF16, align_bytes=64)
             x_words = start.tile([P, PIX], U32, align_bytes=64)
@@ -105,7 +110,6 @@ def tile_involution_kernel(
             span_plane = keep.tile([P, TAPS, GROUPS], U8, align_bytes=64)
             span_bias = keep.tile([P, TAPS], BF16)
             span_bias_f32 = keep.tile([P, TAPS], F32)
-            red = start.tile([P, PACK, PIX], BF16)
             minus_bias = keep.tile([P, TAPS], F32)
             bias_step = {
                 d: {n: keep.tile([P, TAPS], F32, name="bias_step_%d_%d" % (d + 1, n)) for n in (1, UNIT_TAPS)}
@@ -121,20 +125,21 @@ def tile_involution_kernel(
             nc.vector.memset(reduce_raw_plane[:].bitcast(I32), 0)
             nc.vector.memset(span_raw_plane[:].bitcast(I32), 0)
             zeros = keep.tile([P, CH, PAD * W], F32)
-            nc.vector.memset(zeros[:], 0.0)
+            nc.gpsimd.memset(zeros[:], 0.0)
             halves = [slice(0, HALF), slice(HALF, PIX)]
-            nc.sync.dma_start(out=x_sb[:, :, halves[0]], in_=x_by_group[:, :, halves[0]])
+            nc.sync.dma_start(out=x_sb[0][:], in_=x_by_group[:, :, halves[0]])
             nc.sync.dma_start(
                 out=reduce_raw[:],
                 in_=w_reduce_words.rearrange("o p n t -> (o p) (n t)").bitcast(I32),
             )
             load_scale_plane(nc, reduce_raw_plane, w_reduce_scales)
             load_scale_plane(nc, span_raw_plane, w_span_scales)
-            nc.sync.dma_start(out=x_sb[:, :, halves[1]], in_=x_by_group[:, :, halves[1]])
             span_words_dram = w_span_words.rearrange("o p n t -> (o p) (n t)").bitcast(I32)
             for chunk in range(G_CHUNKS):
                 cols = slice(chunk * G_CHUNK * TAPS, (chunk + 1) * G_CHUNK * TAPS)
                 nc.sync.dma_start(out=span_raw[:, cols], in_=span_words_dram[:, cols])
+                if chunk == 1:
+                    nc.sync.dma_start(out=x_sb[1][:], in_=x_by_group[:, :, halves[1]])
             nc.scalar.dma_start(out=reduce_bias[:], in_=b_reduce.rearrange("(p t) -> p t", t=PACK))
             nc.scalar.dma_start(out=span_bias[:], in_=b_span.rearrange("(g t) -> g t", t=TAPS))
 
@@ -142,7 +147,7 @@ def tile_involution_kernel(
             span_plane_by_tap = span_raw_plane[:].rearrange("p (g t) -> p t g", t=TAPS)
             make_identity(nc, ident_bf16[:])
             make_identity(nc, ident_f32[:])
-            nc.vector.memset(warm[:], 0.0)
+            nc.vector.memset(warm[:], 1.0)
             nc.scalar.activation(out=warm[:], in_=warm[:], func=EXP)
 
             edge_prods = {
@@ -153,8 +158,13 @@ def tile_involution_kernel(
                 for prod in tiles:
                     nc.scalar.copy(out=prod[:, :, : PAD * W], in_=zeros[:])
 
-            def group_x(copy, half):
-                copy(out=grouped[:, half, :], in_=x_sb[:, :, half].rearrange("p t w -> p w t"))
+            def by_runs(grouped):
+                return grouped.rearrange("p (w i) t -> p w t i", i=RUN)
+
+            def group_x(copy, h):
+                copy(
+                    out=by_runs(grouped[:, halves[h], :]), in_=x_sb[h][:].rearrange("p t (w i) -> p w t i", i=RUN)
+                )
 
             def quantise(words, plane, grouped, half):
                 nc.vector.quantize_mx(
@@ -163,17 +173,19 @@ def tile_involution_kernel(
                     in_=grouped[:, half, :].rearrange("p w t -> p (w t)"),
                 )
 
-            group_x(nc.vector.tensor_copy, halves[0])
+            group_x(nc.vector.tensor_copy, 0)
             nc.vector.tensor_copy(out=reduce_words[:], in_=reduce_raw[:].rearrange("p (m t) -> p t m", t=PACK))
             quantise(x_words, x_plane, grouped, halves[0])
             nc.vector.tensor_copy(out=reduce_plane[:], in_=reduce_raw_plane[:].rearrange("p (m t) -> p t m", t=PACK))
             nc.vector.tensor_copy(out=reduce_bias_f32[:], in_=reduce_bias[:])
-            nc.vector.tensor_copy(out=span_bias_f32[:], in_=span_bias[:])
-            nc.vector.tensor_scalar_mul(out=minus_bias[:], in0=span_bias_f32[:], scalar1=-1.0)
+            nc.gpsimd.tensor_copy(out=span_bias_f32[:], in_=span_bias[:])
+            nc.gpsimd.tensor_scalar(
+                out=minus_bias[:], in0=span_bias_f32[:], scalar1=-1.0, scalar2=0.0, op0=MULT, op1=ADD
+            )
             for n in (1, UNIT_TAPS):
                 lower, upper = span_bias_f32[:, : TAPS - n], span_bias_f32[:, n:]
-                nc.vector.tensor_tensor(out=bias_step[1][n][:, n:], in0=lower, in1=upper, op=SUB)
-                nc.vector.tensor_tensor(out=bias_step[-1][n][:, : TAPS - n], in0=upper, in1=lower, op=SUB)
+                nc.gpsimd.tensor_tensor(out=bias_step[1][n][:, n:], in0=lower, in1=upper, op=SUB)
+                nc.gpsimd.tensor_tensor(out=bias_step[-1][n][:, : TAPS - n], in0=upper, in1=lower, op=SUB)
 
             def project(psum, tag, t, half):
                 red_ps = psum.tile([P, HALF], F32, tag=tag, name="red_ps")
@@ -188,14 +200,14 @@ def tile_involution_kernel(
                 )
                 return red_ps
 
-            def relu_on_scalar(red_ps, t, half):
+            def relu_on_scalar(red, red_ps, t):
                 nc.scalar.activation(
-                    out=red[:, t, half], in_=red_ps[:], func=RELU, bias=reduce_bias_f32[:, t : t + 1]
+                    out=red[:, t, :], in_=red_ps[:], func=RELU, bias=reduce_bias_f32[:, t : t + 1]
                 )
 
-            def relu_on_vector(red_ps, t, half):
+            def relu_on_vector(red, red_ps, t):
                 nc.vector.tensor_scalar(
-                    out=red[:, t, half],
+                    out=red[:, t, :],
                     in0=red_ps[:],
                     scalar1=reduce_bias_f32[:, t : t + 1],
                     scalar2=0.0,
@@ -203,8 +215,8 @@ def tile_involution_kernel(
                     op1=MAX,
                 )
 
-            def group_red(copy, pixels):
-                copy(out=grouped[:, pixels, :], in_=red[:, :, pixels].rearrange("p t w -> p w t"))
+            def group_red(copy, red, half):
+                copy(by_runs(grouped[:, half, :]), red[:].rearrange("p t (w i) -> p w t i", i=RUN))
 
             first = [
                 project(psum_sums, "sums", 0, halves[0]),
@@ -212,40 +224,49 @@ def tile_involution_kernel(
                 project(psum_sums, "sums", 2, halves[0]),
                 project(psum_kern, "kern", 3, halves[0]),
             ]
-            relu_on_scalar(first[0], 0, halves[0])
-            relu_on_vector(first[1], 1, halves[0])
-            relu_on_scalar(first[2], 2, halves[0])
-            relu_on_scalar(first[3], 3, halves[0])
-            group_red(nc.scalar.copy, halves[0])
-            group_x(nc.scalar.copy, halves[1])
-            for c in range(CH):
+            red = start.tile([P, PACK, HALF], BF16, name="red")
+            relu_on_scalar(red, first[0], 0)
+            relu_on_vector(red, first[1], 1)
+            relu_on_scalar(red, first[2], 2)
+            relu_on_scalar(red, first[3], 3)
+            group_red(nc.scalar.copy, red, halves[0])
+            group_x(nc.scalar.copy, 1)
+            for h in range(2):
+                first_row = PAD + h * (H // 2)
                 nc.scalar.copy(
-                    out=x_pad[:, c, PAD * ROW : (PAD + H) * ROW].rearrange("p (h w) -> p h w", w=ROW)[:, :, LEFT:],
-                    in_=x_sb[:, c, :].rearrange("p (h w) -> p h w", w=W),
+                    out=x_pad[:, :, first_row * ROW : (first_row + H // 2) * ROW].rearrange(
+                        "p c (h w) -> p c h w", w=ROW
+                    )[:, :, :, LEFT:],
+                    in_=x_sb[h][:].rearrange("p c (h w) -> p c h w", w=W),
                 )
 
             def reorder_words(chunk):
                 groups = slice(chunk * G_CHUNK, (chunk + 1) * G_CHUNK)
+                by_group = span_raw[:].rearrange("p (g t) -> p g t", t=TAPS)[:, groups, :]
+                runs = TAPS // RUN * RUN
                 nc.vector.tensor_copy(
-                    out=span_words[:, :, groups],
-                    in_=span_raw[:].rearrange("p (g t) -> p t g", t=TAPS)[:, :, groups],
+                    out=span_words[:, :runs, groups].rearrange("p (k i) g -> p k g i", i=RUN),
+                    in_=by_group[:, :, :runs].rearrange("p g (k i) -> p k g i", i=RUN),
+                )
+                nc.vector.tensor_copy(
+                    out=span_words[:, runs:, groups].rearrange("p t g -> p g t"), in_=by_group[:, :, runs:]
                 )
 
+            def reorder_plane(copy, taps):
+                copy(out=span_plane[:, taps, :], in_=span_plane_by_tap[:, taps, :])
+
+            reorder_plane(nc.vector.tensor_copy, slice(0, PLANE_SPLIT))
             reorder_words(0)
             reorder_words(1)
             quantise(red_words, red_plane, grouped, halves[0])
-            quantise(x_words, x_plane, grouped, halves[1])
             reorder_words(2)
-            for t in range(PACK):
-                relu_on_scalar(project(psum_sums, "sums", t, halves[1]), t, halves[1])
-            group_red(nc.scalar.copy, halves[1])
-            nc.vector.tensor_copy(out=span_plane[:, :PLANE_SPLIT, :], in_=span_plane_by_tap[:, :PLANE_SPLIT, :])
             reorder_words(3)
 
             nc.gpsimd.tensor_copy(out=after_words[:], in_=span_words[:, TAPS - 1, GROUPS - 1 :])
             for tap in range(PLANE_SPLIT, TAPS, PLANE_TURN):
-                turn = slice(tap, min(tap + PLANE_TURN, TAPS))
-                nc.gpsimd.tensor_copy(out=span_plane[:, turn, :], in_=span_plane_by_tap[:, turn, :])
+                reorder_plane(nc.gpsimd.tensor_copy, slice(tap, min(tap + PLANE_TURN, TAPS)))
+
+            pools = {}
 
             kern_of = {}
             logit_of = {}
@@ -307,8 +328,17 @@ def tile_involution_kernel(
                     )
                 kern_of[unit] = kern
 
+            def logits_of(unit):
+                block, v = divmod(unit, UNITS)
+                begin = v % SUB_UNITS * UNIT_TAPS
+                return logit_of[block, v // SUB_UNITS][:, begin : begin + len(taps_of(unit)[1]), :]
+
             def keep_logits(unit):
-                logits = logit_pool.tile([P, UNIT_TAPS, BLOCK_PIX], F32, name="logits")
+                v = unit % UNITS
+                if v % SUB_UNITS == 0:
+                    logits = logit_pool.tile([P, SUB_UNITS * UNIT_TAPS, BLOCK_PIX], F32, name="logits")
+                    logit_of[unit // UNITS, v // SUB_UNITS] = logits
+                logits = logits_of(unit)
                 for i, tap in enumerate(taps_of(unit)[1]):
                     nc.scalar.activation(
                         out=logits[:, i, :],
@@ -316,7 +346,6 @@ def tile_involution_kernel(
                         func=IDENT,
                         bias=span_bias_f32[:, tap : tap + 1],
                     )
-                logit_of[unit] = logits
 
             def take_max(unit, i):
                 block, taps = taps_of(unit)
@@ -356,9 +385,11 @@ def tile_involution_kernel(
                 top_of[block] = top
 
             def subtract(unit):
-                block, taps = taps_of(unit)
-                n = len(taps)
-                logits = logit_of[unit][:, :n, :]
+                block, v = divmod(unit, UNITS)
+                if v % SUB_UNITS > 0:
+                    return
+                n = min(SUB_UNITS * UNIT_TAPS, TAPS - v * UNIT_TAPS)
+                logits = logit_of[block, v // SUB_UNITS][:, :n, :]
                 nc.vector.tensor_tensor(
                     out=logits,
                     in0=logits,
@@ -373,7 +404,7 @@ def tile_involution_kernel(
                 last = taps_of(block * UNITS + UNITS - 1)[1][-1]
                 nc.scalar.activation(
                     out=exps[:, :n, :],
-                    in_=logit_of[unit][:, :n, :],
+                    in_=logits_of(unit),
                     func=EXP,
                     bias=minus_bias[:, last : last + 1],
                 )
@@ -395,41 +426,41 @@ def tile_involution_kernel(
 
             def multiply(unit):
                 block, taps = taps_of(unit)
+                calls = []
                 for i, tap in enumerate(taps):
                     engine = "gpsimd" if is_gpsimds(unit, i) else "vector"
                     row0, row1 = live_rows(block, tap)
                     if row1 - row0 == BLOCK_ROWS:
-                        prod = prod_pool.tile([P, CH, BLOCK_PIX], F32, name="prod")
+                        prod = pools["products"].tile([P, CH, BLOCK_PIX], F32, name="prod")
                     else:
                         prod = edge_prods[engine][0]
                         edge_prods[engine] = edge_prods[engine][1:] + [prod]
+                    prod_of[unit, i] = prod
                     pixels = slice(row0 * W, row1 * W)
                     offset = (tap // KS + row0) * ROW + (LEFT - PAD) + tap % KS
                     exp_img = exp_of[unit][:, i, pixels].rearrange("p (h w) -> p h w", w=W).unsqueeze(1)
 
-                    def window(rows, begin):
-                        return rows[:, :, begin : begin + (row1 - row0) * ROW].rearrange(
-                            "p c (h w) -> p c h w", w=ROW
-                        )[:, :, :, :W]
+                    def window(rows, begin, length):
+                        return rows[:, :, begin : begin + length].rearrange("p c (h w) -> p c h w", w=ROW)[:, :, :, :W]
 
-                    if engine == "gpsimd":
-                        nc.gpsimd.tensor_tensor(
-                            out=prod[:, :, pixels].rearrange("p c (h w) -> p c h w", w=W),
-                            in0=exp_img.to_broadcast([P, CH, row1 - row0, W]),
-                            in1=window(x_pad, block * BLOCK_ROWS * ROW + offset),
+                    def product(engine, prod, exp_img, x, channels, pixels):
+                        engine.tensor_tensor(
+                            out=prod[:, channels, pixels].rearrange("p c (h w) -> p c h w", w=W),
+                            in0=exp_img.to_broadcast(list(x.shape)),
+                            in1=x,
                             op=MULT,
                         )
+
+                    length = (row1 - row0) * ROW
+                    if engine == "gpsimd":
+                        x = window(x_pad, block * BLOCK_ROWS * ROW + offset, length)
+                        product(nc.gpsimd, prod, exp_img, x, slice(0, CH), pixels)
                     else:
                         for pair in range(CH // 2):
-                            nc.vector.tensor_tensor(
-                                out=prod[:, 2 * pair : 2 * pair + 2, pixels].rearrange(
-                                    "p c (h w) -> p c h w", w=W
-                                ),
-                                in0=exp_img.to_broadcast([P, 2, row1 - row0, W]),
-                                in1=window(window_of[pair], offset),
-                                op=MULT,
-                            )
-                    prod_of[unit, i] = prod
+                            x = window(window_of[pair], offset, length)
+                            channels = slice(2 * pair, 2 * pair + 2)
+                            calls.append(partial(product, nc.vector, prod, exp_img, x, channels, pixels))
+                return calls
 
             def add_exps(unit):
                 block, taps = taps_of(unit)
@@ -448,33 +479,33 @@ def tile_involution_kernel(
                             is_transpose=True,
                         )
 
-            def add_products(unit, i):
-                block = unit // UNITS
+            def add_products(taps, tiles):
+                block = taps[0][0] // UNITS
                 in_block = [tap for tap in adding_order if tap[0] // UNITS == block]
-                opens, closes = (unit, i) == in_block[0], (unit, i) == in_block[-1]
-                if opens:
-                    for j in range(BLOCK_TILES):
+                for j in tiles:
+                    if (block, j) not in sums_of:
                         sums = psum_sums.tile([P, CH, GROUPS], F32, tag="sums", name="sums")
                         sums_of[block, j] = sums
-                for j in range(BLOCK_TILES):
-                    for c in range(CH):
-                        nc.tensor.matmul(
-                            out=sums_of[block, j][:, c, :],
-                            lhsT=prod_of[unit, i][:, c, j * P : (j + 1) * P],
-                            rhs=ident_f32[:],
-                            start=(opens and c == 0),
-                            stop=(closes and c == CH - 1),
-                            is_transpose=True,
-                        )
+                for j in tiles:
+                    for tap in taps:
+                        for c in range(CH):
+                            nc.tensor.matmul(
+                                out=sums_of[block, j][:, c, :],
+                                lhsT=prod_of[tap][:, c, j * P : (j + 1) * P],
+                                rhs=ident_f32[:],
+                                start=(tap == in_block[0] and c == 0),
+                                stop=(tap == in_block[-1] and c == CH - 1),
+                                is_transpose=True,
+                            )
 
             def invert(block):
-                inverse = out_pool.tile([P, BLOCK_TILES, GROUPS], F32, name="inverse")
+                inverse = pools["results"].tile([P, BLOCK_TILES, GROUPS], F32, name="inverse")
                 nc.vector.reciprocal(out=inverse[:], in_=den_of[block][:])
                 inverse_of[block] = inverse
 
             def divide(block):
                 for j in range(BLOCK_TILES):
-                    scaled = out_pool.tile([P, CH, GROUPS], F32, name="scaled")
+                    scaled = pools["results"].tile([P, CH, GROUPS], F32, name="scaled")
                     nc.vector.tensor_tensor(
                         out=scaled[:],
                         in0=sums_of[block, j][:],
@@ -489,10 +520,65 @@ def tile_involution_kernel(
                     back = psum_sums.tile([P, CH, P], F32, tag="sums", name="back")
                     for c in range(CH):
                         nc.tensor.transpose(back[:, c, :], scaled[:, c, :], ident_f32[:])
-                    result = out_pool.tile([P, CH, P], F32, name="result")
+                    result = pools["results"].tile([P, CH, P], F32, name="result")
                     nc.scalar.copy(out=result[:], in_=back[:])
                     pt = block * BLOCK_TILES + j
                     nc.sync.dma_start(out=out_by_group[:, :, pt * P : (pt + 1) * P], in_=result[:])
+
+            def turn(unit):
+                block, v = divmod(unit, UNITS)
+                sweep = unit + SWEEP_LEAD
+                done = None
+                if unit < N_UNITS and v == 0:
+                    load_window(block)
+                if sweep + 1 < N_UNITS:
+                    make_kern(sweep + 1)
+                if unit + 1 < N_UNITS:
+                    add_exps(unit + 1)
+                calls = multiply(unit) if unit < N_UNITS else []
+                if v > 0:
+                    for call in calls[:1]:
+                        call()
+                    calls = calls[1:]
+                if sweep < N_UNITS:
+                    take_max(sweep, 0)
+                if unit + LEAD < N_UNITS:
+                    subtract(unit + LEAD)
+                    exponentiate(unit + LEAD)
+                if v > 0:
+                    for call in calls[:1]:
+                        call()
+                    calls = calls[1:]
+                if sweep < N_UNITS:
+                    if len(taps_of(sweep)[1]) > 1:
+                        take_max(sweep, 1)
+                    keep_logits(sweep)
+                for call in calls:
+                    call()
+                if v == UNITS - 1 - LEAD and block + 1 < N_BLOCKS:
+                    load_top(block + 1)
+                adding = state["adding"]
+                if adding and state["divided"] is None:
+                    block_taps = [tap for tap in adding if tap[0] // UNITS == adding[0][0] // UNITS]
+                    ready = [tap for tap in block_taps if added_at(*tap) <= unit]
+                    state["adding"] = adding[len(ready) :]
+                    if ready and len(ready) == len(block_taps):
+                        done = ready[0][0] // UNITS
+                        add_products(ready, range(BLOCK_TILES))
+                    else:
+                        for tap in ready:
+                            add_products([tap], range(BLOCK_TILES))
+                if unit + 1 < N_UNITS and (unit + 1) % UNITS == UNITS - 1:
+                    invert((unit + 1) // UNITS)
+                tiles = edge_prods["vector"] + edge_prods["gpsimd"]
+                if UNITS <= unit < UNITS + len(tiles):
+                    nc.scalar.copy(out=tiles[unit - UNITS][:, :, BLOCK_PIX - PAD * W :], in_=zeros[:])
+                if state["divided"] is not None:
+                    store(state["divided"])
+                    state["divided"] = None
+                if done is not None:
+                    divide(done)
+                    state["divided"] = done
 
             def sweep_over(unit):
                 for i in range(len(taps_of(unit)[1])):
@@ -502,8 +588,6 @@ def tile_involution_kernel(
             for unit in range(FIRST_AHEAD):
                 make_kern(unit)
             for unit in range(UNITS):
-                if unit == 8:
-                    quantise(red_words, red_plane, grouped, halves[1])
                 if unit + FIRST_AHEAD <= UNITS:
                     make_kern(unit + FIRST_AHEAD)
                 sweep_over(unit)
@@ -515,51 +599,24 @@ def tile_involution_kernel(
                     subtract(unit - UNITS)
                     exponentiate(unit - UNITS)
 
-        prod_pool = stack.enter_context(tc.tile_pool(name="products", bufs=12))
-        out_pool = stack.enter_context(tc.tile_pool(name="results", bufs=2))
+            state = {
+                "divided": None,
+                "adding": adding_order,
+            }
+            add_exps(0)
+            red = start.tile([P, PACK, HALF], BF16, name="red")
+            for unit in range(FIRST_TURNS):
+                if unit == 0:
+                    quantise(x_words, x_plane, grouped, halves[1])
+                turn(unit)
+                for t in range(2 * unit, min(2 * unit + 2, PACK)):
+                    relu_on_scalar(red, project(psum_sums, "sums", t, halves[1]), t)
+                if unit == 4:
+                    group_red(nc.scalar.copy, red, halves[1])
+            quantise(red_words, red_plane, grouped, halves[1])
 
-        divided = None
-        adding = adding_order
-        add_exps(0)
-        for unit in range(N_UNITS + LAG + 2):
-            block, v = divmod(unit, UNITS)
-            sweep = unit + SWEEP_LEAD
-            done = None
-            if unit < N_UNITS and v == 0:
-                load_window(block)
-            if sweep + 1 < N_UNITS:
-                make_kern(sweep + 1)
-            if unit + 1 < N_UNITS:
-                add_exps(unit + 1)
-            if unit < N_UNITS and v > 0:
-                multiply(unit)
-            if sweep < N_UNITS:
-                take_max(sweep, 0)
-            if unit + LEAD < N_UNITS:
-                subtract(unit + LEAD)
-                exponentiate(unit + LEAD)
-            if sweep < N_UNITS:
-                if len(taps_of(sweep)[1]) > 1:
-                    take_max(sweep, 1)
-                keep_logits(sweep)
-            if unit < N_UNITS and v == 0:
-                multiply(unit)
-            if v == UNITS - 1 - LEAD and block + 1 < N_BLOCKS:
-                load_top(block + 1)
-            while adding and added_at(*adding[0]) <= unit and done is None and divided is None:
-                added = adding[0]
-                adding = adding[1:]
-                add_products(*added)
-                if not adding or adding[0][0] // UNITS > added[0] // UNITS:
-                    done = added[0] // UNITS
-            if unit + 1 < N_UNITS and (unit + 1) % UNITS == UNITS - 1:
-                invert((unit + 1) // UNITS)
-            tiles = edge_prods["vector"] + edge_prods["gpsimd"]
-            if UNITS <= unit < UNITS + len(tiles):
-                nc.scalar.copy(out=tiles[unit - UNITS][:, :, BLOCK_PIX - PAD * W :], in_=zeros[:])
-            if divided is not None:
-                store(divided)
-                divided = None
-            if done is not None:
-                divide(done)
-                divided = done
+        pools["products"] = stack.enter_context(tc.tile_pool(name="products", bufs=12))
+        pools["results"] = stack.enter_context(tc.tile_pool(name="results", bufs=2))
+
+        for unit in range(FIRST_TURNS, N_UNITS + LAG + 2):
+            turn(unit)

@@ -51,7 +51,7 @@ VECTOR_UNITS = [set(), set(), set(), {6, 12, 18}]
 GPSIMD_UNITS = [{12}, {12}, {12}, set()]
 LEAD = 3
 SWEEP_LEAD = UNITS + LEAD
-SUB_UNITS = 2
+SUB_UNITS = 1
 LOGIT_TILES = SWEEP_LEAD // SUB_UNITS + 2
 EDGE_TILES = {"vector": 5, "gpsimd": 6}
 FIRST_TURNS = 9
@@ -260,6 +260,7 @@ def tile_involution_kernel(
             reorder_words(1)
             quantise(red_words, red_plane, grouped, halves[0])
             reorder_words(2)
+            quantise(x_words, x_plane, grouped, halves[1])
             reorder_words(3)
 
             nc.gpsimd.tensor_copy(out=after_words[:], in_=span_words[:, TAPS - 1, GROUPS - 1 :])
@@ -606,8 +607,6 @@ def tile_involution_kernel(
             add_exps(0)
             red = start.tile([P, PACK, HALF], BF16, name="red")
             for unit in range(FIRST_TURNS):
-                if unit == 0:
-                    quantise(x_words, x_plane, grouped, halves[1])
                 turn(unit)
                 for t in range(2 * unit, min(2 * unit + 2, PACK)):
                     relu_on_scalar(red, project(psum_sums, "sums", t, halves[1]), t)

@@ -124,8 +124,7 @@ def tile_involution_kernel(
 
             nc.vector.memset(reduce_raw_plane[:].bitcast(I32), 0)
             nc.vector.memset(span_raw_plane[:].bitcast(I32), 0)
-            zeros = keep.tile([P, CH, PAD * W], F32)
-            nc.gpsimd.memset(zeros[:], 0.0)
+            zeros = keep.tile([P, CH, H * LEFT], F32)
             halves = [slice(0, HALF), slice(HALF, PIX)]
             nc.sync.dma_start(out=x_sb[0][:], in_=x_by_group[:, :, halves[0]])
             nc.sync.dma_start(
@@ -143,10 +142,10 @@ def tile_involution_kernel(
             nc.scalar.dma_start(out=reduce_bias[:], in_=b_reduce.rearrange("(p t) -> p t", t=PACK))
             nc.scalar.dma_start(out=span_bias[:], in_=b_span.rearrange("(g t) -> g t", t=TAPS))
 
-            nc.gpsimd.memset(x_pad[:].rearrange("p c n -> p (c n)").bitcast(I32), 0)
             span_plane_by_tap = span_raw_plane[:].rearrange("p (g t) -> p t g", t=TAPS)
             make_identity(nc, ident_bf16[:])
             make_identity(nc, ident_f32[:])
+            nc.vector.memset(zeros[:], 0.0)
             nc.vector.memset(warm[:], 1.0)
             nc.scalar.activation(out=warm[:], in_=warm[:], func=EXP)
 
@@ -156,7 +155,7 @@ def tile_involution_kernel(
             }
             for tiles in edge_prods.values():
                 for prod in tiles:
-                    nc.scalar.copy(out=prod[:, :, : PAD * W], in_=zeros[:])
+                    nc.scalar.copy(out=prod[:, :, : PAD * W], in_=zeros[:, :, : PAD * W])
 
             def by_runs(grouped):
                 return grouped.rearrange("p (w i) t -> p w t i", i=RUN)
@@ -178,14 +177,6 @@ def tile_involution_kernel(
             quantise(x_words, x_plane, grouped, halves[0])
             nc.vector.tensor_copy(out=reduce_plane[:], in_=reduce_raw_plane[:].rearrange("p (m t) -> p t m", t=PACK))
             nc.vector.tensor_copy(out=reduce_bias_f32[:], in_=reduce_bias[:])
-            nc.gpsimd.tensor_copy(out=span_bias_f32[:], in_=span_bias[:])
-            nc.gpsimd.tensor_scalar(
-                out=minus_bias[:], in0=span_bias_f32[:], scalar1=-1.0, scalar2=0.0, op0=MULT, op1=ADD
-            )
-            for n in (1, UNIT_TAPS):
-                lower, upper = span_bias_f32[:, : TAPS - n], span_bias_f32[:, n:]
-                nc.gpsimd.tensor_tensor(out=bias_step[1][n][:, n:], in0=lower, in1=upper, op=SUB)
-                nc.gpsimd.tensor_tensor(out=bias_step[-1][n][:, : TAPS - n], in0=upper, in1=lower, op=SUB)
 
             def project(psum, tag, t, half):
                 red_ps = psum.tile([P, HALF], F32, tag=tag, name="red_ps")
@@ -205,16 +196,6 @@ def tile_involution_kernel(
                     out=red[:, t, :], in_=red_ps[:], func=RELU, bias=reduce_bias_f32[:, t : t + 1]
                 )
 
-            def relu_on_vector(red, red_ps, t):
-                nc.vector.tensor_scalar(
-                    out=red[:, t, :],
-                    in0=red_ps[:],
-                    scalar1=reduce_bias_f32[:, t : t + 1],
-                    scalar2=0.0,
-                    op0=ADD,
-                    op1=MAX,
-                )
-
             def group_red(copy, red, half):
                 copy(by_runs(grouped[:, half, :]), red[:].rearrange("p t (w i) -> p w t i", i=RUN))
 
@@ -226,7 +207,7 @@ def tile_involution_kernel(
             ]
             red = start.tile([P, PACK, HALF], BF16, name="red")
             relu_on_scalar(red, first[0], 0)
-            relu_on_vector(red, first[1], 1)
+            relu_on_scalar(red, first[1], 1)
             relu_on_scalar(red, first[2], 2)
             relu_on_scalar(red, first[3], 3)
             group_red(nc.scalar.copy, red, halves[0])
@@ -239,6 +220,13 @@ def tile_involution_kernel(
                     )[:, :, :, LEFT:],
                     in_=x_sb[h][:].rearrange("p c (h w) -> p c h w", w=W),
                 )
+            inside = slice(PAD * ROW, (PAD + H) * ROW)
+            nc.scalar.copy(out=x_pad[:, :, : inside.start], in_=zeros[:, :, : inside.start])
+            nc.scalar.copy(out=x_pad[:, :, inside.stop :], in_=zeros[:, :, : CH_LEN - inside.stop])
+            nc.scalar.copy(
+                out=x_pad[:, :, inside].rearrange("p c (h w) -> p c h w", w=ROW)[:, :, :, :LEFT],
+                in_=zeros[:].rearrange("p c (h w) -> p c h w", w=LEFT),
+            )
 
             def reorder_words(chunk):
                 groups = slice(chunk * G_CHUNK, (chunk + 1) * G_CHUNK)
@@ -264,8 +252,23 @@ def tile_involution_kernel(
             reorder_words(3)
 
             nc.gpsimd.tensor_copy(out=after_words[:], in_=span_words[:, TAPS - 1, GROUPS - 1 :])
+
+            def make_bias_step(d, n):
+                lower, upper = span_bias_f32[:, : TAPS - n], span_bias_f32[:, n:]
+                if d == 1:
+                    nc.gpsimd.tensor_tensor(out=bias_step[d][n][:, n:], in0=lower, in1=upper, op=SUB)
+                else:
+                    nc.gpsimd.tensor_tensor(out=bias_step[d][n][:, : TAPS - n], in0=upper, in1=lower, op=SUB)
+
+            nc.gpsimd.tensor_copy(out=span_bias_f32[:], in_=span_bias[:])
+            make_bias_step(1, UNIT_TAPS)
             for tap in range(PLANE_SPLIT, TAPS, PLANE_TURN):
                 reorder_plane(nc.gpsimd.tensor_copy, slice(tap, min(tap + PLANE_TURN, TAPS)))
+            make_bias_step(1, 1)
+            make_bias_step(-1, 1)
+            nc.gpsimd.tensor_scalar(
+                out=minus_bias[:], in0=span_bias_f32[:], scalar1=-1.0, scalar2=0.0, op0=MULT, op1=ADD
+            )
 
             pools = {}
 
@@ -532,10 +535,10 @@ def tile_involution_kernel(
                 done = None
                 if unit < N_UNITS and v == 0:
                     load_window(block)
-                if sweep + 1 < N_UNITS:
-                    make_kern(sweep + 1)
                 if unit + 1 < N_UNITS:
                     add_exps(unit + 1)
+                if sweep + 1 < N_UNITS:
+                    make_kern(sweep + 1)
                 calls = multiply(unit) if unit < N_UNITS else []
                 if v > 0:
                     for call in calls[:1]:
@@ -573,7 +576,7 @@ def tile_involution_kernel(
                     invert((unit + 1) // UNITS)
                 tiles = edge_prods["vector"] + edge_prods["gpsimd"]
                 if UNITS <= unit < UNITS + len(tiles):
-                    nc.scalar.copy(out=tiles[unit - UNITS][:, :, BLOCK_PIX - PAD * W :], in_=zeros[:])
+                    nc.scalar.copy(out=tiles[unit - UNITS][:, :, BLOCK_PIX - PAD * W :], in_=zeros[:, :, : PAD * W])
                 if state["divided"] is not None:
                     store(state["divided"])
                     state["divided"] = None

from contextlib import ExitStack
from functools import partial

import concourse.mybir as mybir
from concourse.masks import make_identity

F32 = mybir.dt.float32
BF16 = mybir.dt.bfloat16
I32 = mybir.dt.int32
U32 = mybir.dt.uint32
U8 = mybir.dt.uint8
FP8X4 = mybir.dt.float8_e4m3fn_x4
ADD = mybir.AluOpType.add
SUB = mybir.AluOpType.subtract
MULT = mybir.AluOpType.mult
MAX = mybir.AluOpType.max
EXP = mybir.ActivationFunctionType.Exp
IDENT = mybir.ActivationFunctionType.Identity
RELU = mybir.ActivationFunctionType.Relu

P = 128
PACK = 4
C = 512
R = 512
GROUPS = 128
CH = C // GROUPS
KS = 7
PAD = KS // 2
TAPS = KS * KS
O = GROUPS * TAPS
H = 32
W = 32
PIX = H * W
HALF = PIX // 2
BLOCK_ROWS = 8
BLOCK_PIX = BLOCK_ROWS * W
BLOCK_TILES = BLOCK_PIX // P
N_BLOCKS = PIX // BLOCK_PIX
LEFT = 4
ROW = LEFT + W
WIN = 512
PAD_ROWS = H + 2 * PAD
CH_LEN = PAD_ROWS * ROW + 8
UNIT_TAPS = 2
UNITS = -(-TAPS // UNIT_TAPS)
N_UNITS = N_BLOCKS * UNITS
VECTOR_LAG = 2
GPSIMD_LAG = 3
LAG = max(VECTOR_LAG, GPSIMD_LAG + 1)
VECTOR_UNITS = [set(), set(), set(), {6, 12, 18}]
GPSIMD_UNITS = [{12}, {12}, {12}, set()]
LEAD = 3
SWEEP_LEAD = UNITS + LEAD
SUB_UNITS = 1
LOGIT_TILES = SWEEP_LEAD // SUB_UNITS + 2
EDGE_TILES = {"vector": 5, "gpsimd": 6}
FIRST_TURNS = 9
FIRST_AHEAD = 3
G_CHUNKS = 4
G_CHUNK = GROUPS // G_CHUNKS
RUN = 4
PLANE_SPLIT = 28
PLANE_TURN = 7

FLOPS = 2 * PIX * (C * R + R * O) + 2 * TAPS * C * PIX


def load_scale_plane(nc, plane, scales):
    for quadrant in range(4):
        nc.sync.dma_start(
            out=plane[32 * quadrant : 32 * quadrant + 4, :].bitcast(I32),
            in_=scales[0, 4 * quadrant : 4 * quadrant + 4, :].bitcast(I32),
        )


def tile_involution_kernel(
    tc, x, w_reduce_words, w_reduce_scales, b_reduce, w_span_words, w_span_scales, b_span, out
):
    nc = tc.nc
    x_by_group = x.rearrange("b (g c) h w -> (b g) c (h w)", c=CH)
    out_by_group = out.rearrange("b (g c) h w -> (b g) c (h w)", c=CH)

    with ExitStack() as stack:
        stack.enter_context(tc.manual_schedule())
        keep = stack.enter_context(tc.tile_pool(name="keep", bufs=1))
        max_pool = stack.enter_context(tc.tile_pool(name="maxima", bufs=4))
        logit_pool = stack.enter_context(tc.tile_pool(name="logits", bufs=LOGIT_TILES))
        exp_pool = stack.enter_context(tc.tile_pool(name="exps", bufs=LEAD + 4))
        psum_x = stack.enter_context(tc.psum_pool(name="psum_x", bufs=2))
        psum_sums = stack.enter_context(tc.psum_pool(name="psum_sums", bufs=2))
        psum_den = stack.enter_context(tc.psum_pool(name="psum_den", bufs=1))
        psum_kern = stack.enter_context(tc.psum_pool(name="psum_kern", bufs=2))
        psum_top = stack.enter_context(tc.psum_pool(name="psum_top", bufs=1))

        with tc.tile_pool(name="start", bufs=1) as start:
            x_sb = [start.tile([P, CH, HALF], BF16, name="x_half_%d" % half) for half in range(2)]
            x_pad = keep.tile([P, CH, CH_LEN], BF16)
            grouped = start.tile([P, PIX, PACK], BF16, align_bytes=64)
            x_words = start.tile([P, PIX], U32, align_bytes=64)
            x_plane = start.tile([P, PIX], U8, align_bytes=64)
            reduce_raw = start.tile([P, R], I32, align_bytes=64)
            reduce_raw_plane = start.tile([P, R], U8, align_bytes=64)
            reduce_words = start.tile([P, PACK, P], I32, align_bytes=64)
            reduce_plane = start.tile([P, PACK, P], U8, align_bytes=64)
            reduce_bias = keep.tile([P, PACK], BF16)
            reduce_bias_f32 = keep.tile([P, PACK], F32)
            span_raw = start.tile([P, O], I32, align_bytes=64)
            span_raw_plane = start.tile([P, O], U8, align_bytes=64)
            span_words = keep.tile([P, TAPS, GROUPS], I32, align_bytes=64)
            span_plane = keep.tile([P, TAPS, GROUPS], U8, align_bytes=64)
            span_bias = keep.tile([P, TAPS], BF16)
            span_bias_f32 = keep.tile([P, TAPS], F32)
            minus_bias = keep.tile([P, TAPS], F32)
            bias_step = {
                d: {n: keep.tile([P, TAPS], F32, name="bias_step_%d_%d" % (d + 1, n)) for n in (1, UNIT_TAPS)}
                for d in (1, -1)
            }
            red_words = keep.tile([P, PIX], U32, align_bytes=64)
            red_plane = keep.tile([P, PIX], U8, align_bytes=64)
            ident_f32 = keep.tile([P, P], F32)
            ident_bf16 = keep.tile([P, P], BF16)
            warm = keep.tile([P, 1], F32)
            after_words = keep.tile([P, 1], I32)

            nc.vector.memset(reduce_raw_plane[:].bitcast(I32), 0)
            nc.vector.memset(span_raw_plane[:].bitcast(I32), 0)
            zeros = keep.tile([P, CH, H * LEFT], F32)
            halves = [slice(0, HALF), slice(HALF, PIX)]
            nc.sync.dma_start(out=x_sb[0][:], in_=x_by_group[:, :, halves[0]])
            nc.sync.dma_start(
                out=reduce_raw[:],
                in_=w_reduce_words.rearrange("o p n t -> (o p) (n t)").bitcast(I32),
            )
            load_scale_plane(nc, reduce_raw_plane, w_reduce_scales)
            load_scale_plane(nc, span_raw_plane, w_span_scales)
            span_words_dram = w_span_words.rearrange("o p n t -> (o p) (n t)").bitcast(I32)
            for chunk in range(G_CHUNKS):
                cols = slice(chunk * G_CHUNK * TAPS, (chunk + 1) * G_CHUNK * TAPS)
                nc.sync.dma_start(out=span_raw[:, cols], in_=span_words_dram[:, cols])
                if chunk == 1:
                    nc.sync.dma_start(out=x_sb[1][:], in_=x_by_group[:, :, halves[1]])
            nc.scalar.dma_start(out=reduce_bias[:], in_=b_reduce.rearrange("(p t) -> p t", t=PACK))
            nc.scalar.dma_start(out=span_bias[:], in_=b_span.rearrange("(g t) -> g t", t=TAPS))

            span_plane_by_tap = span_raw_plane[:].rearrange("p (g t) -> p t g", t=TAPS)
            make_identity(nc, ident_bf16[:])
            make_identity(nc, ident_f32[:])
            nc.vector.memset(zeros[:], 0.0)
            nc.vector.memset(warm[:], 1.0)
            nc.scalar.activation(out=warm[:], in_=warm[:], func=EXP)

            edge_prods = {
                engine: [keep.tile([P, CH, BLOCK_PIX], F32, name="%s_edge_%d" % (engine, n)) for n in range(count)]
                for engine, count in EDGE_TILES.items()
            }
            for tiles in edge_prods.values():
                for prod in tiles:
                    nc.scalar.copy(out=prod[:, :, : PAD * W], in_=zeros[:, :, : PAD * W])

            def by_runs(grouped):
                return grouped.rearrange("p (w i) t -> p w t i", i=RUN)

            def group_x(copy, h):
                copy(
                    out=by_runs(grouped[:, halves[h], :]), in_=x_sb[h][:].rearrange("p t (w i) -> p w t i", i=RUN)
                )

            def quantise(words, plane, grouped, half):
                nc.vector.quantize_mx(
                    out=words[:, half].bitcast(FP8X4),
                    scales=plane[:, half],
                    in_=grouped[:, half, :].rearrange("p w t -> p (w t)"),
                )

            group_x(nc.vector.tensor_copy, 0)
            nc.vector.tensor_copy(out=reduce_words[:], in_=reduce_raw[:].rearrange("p (m t) -> p t m", t=PACK))
            quantise(x_words, x_plane, grouped, halves[0])
            nc.vector.tensor_copy(out=reduce_plane[:], in_=reduce_raw_plane[:].rearrange("p (m t) -> p t m", t=PACK))
            nc.vector.tensor_copy(out=reduce_bias_f32[:], in_=reduce_bias[:])

            def project(psum, tag, t, half):
                red_ps = psum.tile([P, HALF], F32, tag=tag, name="red_ps")
                nc.tensor.matmul_mx(
                    out=red_ps[:],
                    lhsT=reduce_words[:, t, :].bitcast(FP8X4),
                    lhsT_scale=reduce_plane[:, t, :],
                    rhs=x_words[:, half].bitcast(FP8X4),
                    rhs_scale=x_plane[:, half],
                    start=True,
                    stop=True,
                )
                return red_ps

            def relu_on_scalar(red, red_ps, t):
                nc.scalar.activation(
                    out=red[:, t, :], in_=red_ps[:], func=RELU, bias=reduce_bias_f32[:, t : t + 1]
                )

            def group_red(copy, red, half):
                copy(by_runs(grouped[:, half, :]), red[:].rearrange("p t (w i) -> p w t i", i=RUN))

            first = [
                project(psum_sums, "sums", 0, halves[0]),
                project(psum_kern, "kern", 1, halves[0]),
                project(psum_sums, "sums", 2, halves[0]),
                project(psum_kern, "kern", 3, halves[0]),
            ]
            red = start.tile([P, PACK, HALF], BF16, name="red")
            relu_on_scalar(red, first[0], 0)
            relu_on_scalar(red, first[1], 1)
            relu_on_scalar(red, first[2], 2)
            relu_on_scalar(red, first[3], 3)
            group_red(nc.scalar.copy, red, halves[0])
            group_x(nc.scalar.copy, 1)
            for h in range(2):
                first_row = PAD + h * (H // 2)
                nc.scalar.copy(
                    out=x_pad[:, :, first_row * ROW : (first_row + H // 2) * ROW].rearrange(
                        "p c (h w) -> p c h w", w=ROW
                    )[:, :, :, LEFT:],
                    in_=x_sb[h][:].rearrange("p c (h w) -> p c h w", w=W),
                )
            inside = slice(PAD * ROW, (PAD + H) * ROW)
            nc.scalar.copy(out=x_pad[:, :, : inside.start], in_=zeros[:, :, : inside.start])
            nc.scalar.copy(out=x_pad[:, :, inside.stop :], in_=zeros[:, :, : CH_LEN - inside.stop])
            nc.scalar.copy(
                out=x_pad[:, :, inside].rearrange("p c (h w) -> p c h w", w=ROW)[:, :, :, :LEFT],
                in_=zeros[:].rearrange("p c (h w) -> p c h w", w=LEFT),
            )

            def reorder_words(chunk):
                groups = slice(chunk * G_CHUNK, (chunk + 1) * G_CHUNK)
                by_group = span_raw[:].rearrange("p (g t) -> p g t", t=TAPS)[:, groups, :]
                runs = TAPS // RUN * RUN
                nc.vector.tensor_copy(
                    out=span_words[:, :runs, groups].rearrange("p (k i) g -> p k g i", i=RUN),
                    in_=by_group[:, :, :runs].rearrange("p g (k i) -> p k g i", i=RUN),
                )
                nc.vector.tensor_copy(
                    out=span_words[:, runs:, groups].rearrange("p t g -> p g t"), in_=by_group[:, :, runs:]
                )

            def reorder_plane(copy, taps):
                copy(out=span_plane[:, taps, :], in_=span_plane_by_tap[:, taps, :])

            reorder_plane(nc.vector.tensor_copy, slice(0, PLANE_SPLIT))
            reorder_words(0)
            reorder_words(1)
            quantise(red_words, red_plane, grouped, halves[0])
            reorder_words(2)
            quantise(x_words, x_plane, grouped, halves[1])
            reorder_words(3)

            nc.gpsimd.tensor_copy(out=after_words[:], in_=span_words[:, TAPS - 1, GROUPS - 1 :])

            def make_bias_step(d, n):
                lower, upper = span_bias_f32[:, : TAPS - n], span_bias_f32[:, n:]
                if d == 1:
                    nc.gpsimd.tensor_tensor(out=bias_step[d][n][:, n:], in0=lower, in1=upper, op=SUB)
                else:
                    nc.gpsimd.tensor_tensor(out=bias_step[d][n][:, : TAPS - n], in0=upper, in1=lower, op=SUB)

            nc.gpsimd.tensor_copy(out=span_bias_f32[:], in_=span_bias[:])
            make_bias_step(1, UNIT_TAPS)
            for tap in range(PLANE_SPLIT, TAPS, PLANE_TURN):
                reorder_plane(nc.gpsimd.tensor_copy, slice(tap, min(tap + PLANE_TURN, TAPS)))
            make_bias_step(1, 1)
            make_bias_step(-1, 1)
            nc.gpsimd.tensor_scalar(
                out=minus_bias[:], in0=span_bias_f32[:], scalar1=-1.0, scalar2=0.0, op0=MULT, op1=ADD
            )

            pools = {}

            kern_of = {}
            logit_of = {}
            tops_of = {}
            top_of = {}
            exp_of = {}
            prod_of = {}
            window_of = {}
            sums_of = {}
            den_of = {}
            inverse_of = {}
            scaled_of = {}

            def direction(block):
                return -1 if block == N_BLOCKS - 1 else 1

            def taps_of(unit):
                block, v = divmod(unit, UNITS)
                order = list(range(TAPS))[:: direction(block)]
                return block, order[UNIT_TAPS * v : UNIT_TAPS * (v + 1)]

            def live_rows(block, tap):
                shift = tap // KS - PAD
                return (
                    max(0, -shift - block * BLOCK_ROWS),
                    min(BLOCK_ROWS, H - shift - block * BLOCK_ROWS),
                )

            def is_gpsimds(unit, i):
                block, v = divmod(unit, UNITS)
                if v in GPSIMD_UNITS[block]:
                    return True
                return i == 0 and v != UNITS - 1 and v not in VECTOR_UNITS[block]

            def added_at(unit, i):
                return unit + (GPSIMD_LAG + i if is_gpsimds(unit, i) else VECTOR_LAG)

            adding_order = sorted(
                [(unit, i) for unit in range(N_UNITS) for i in range(len(taps_of(unit)[1]))],
                key=lambda tap: (tap[0] // UNITS, added_at(*tap), tap),
            )

            def make_kern(unit):
                block, taps = taps_of(unit)
                pixels = slice(block * BLOCK_PIX, (block + 1) * BLOCK_PIX)
                if unit < UNITS and unit % 2 == 1:
                    kern = psum_sums.tile([P, UNIT_TAPS, BLOCK_PIX], F32, tag="sums", name="kern")
                else:
                    kern = psum_kern.tile([P, UNIT_TAPS, BLOCK_PIX], F32, tag="kern", name="kern")
                for i, tap in enumerate(taps):
                    nc.tensor.matmul_mx(
                        out=kern[:, i, :],
                        lhsT=span_words[:, tap, :].bitcast(FP8X4),
                        lhsT_scale=span_plane[:, tap, :],
                        rhs=red_words[:, pixels].bitcast(FP8X4),
                        rhs_scale=red_plane[:, pixels],
                        start=True,
                        stop=True,
                    )
                kern_of[unit] = kern

            def logits_of(unit):
                block, v = divmod(unit, UNITS)
                begin = v % SUB_UNITS * UNIT_TAPS
                return logit_of[block, v // SUB_UNITS][:, begin : begin + len(taps_of(unit)[1]), :]

            def keep_logits(unit):
                v = unit % UNITS
                if v % SUB_UNITS == 0:
                    logits = logit_pool.tile([P, SUB_UNITS * UNIT_TAPS, BLOCK_PIX], F32, name="logits")
                    logit_of[unit // UNITS, v // SUB_UNITS] = logits
                logits = logits_of(unit)
                for i, tap in enumerate(taps_of(unit)[1]):
                    nc.scalar.activation(
                        out=logits[:, i, :],
                        in_=kern_of[unit][:, i, :],
                        func=IDENT,
                        bias=span_bias_f32[:, tap : tap + 1],
                    )

            def take_max(unit, i):
                block, taps = taps_of(unit)
                tap, kern = taps[i], kern_of[unit][:, i, :]
                v = unit % UNITS
                chains = UNIT_TAPS if block == 0 else 1
                steps = bias_step[direction(block)]
                if v == 0 and i < chains:
                    top = max_pool.tile([P, BLOCK_PIX], F32, name="top")
                    tops_of[block, i] = top
                    nc.vector.tensor_copy(out=top[:], in_=kern)
                else:
                    top = tops_of[block, i % chains]
                    nc.vector.scalar_tensor_tensor(
                        out=top[:],
                        in0=top[:],
                        scalar=steps[chains][:, tap : tap + 1],
                        in1=kern,
                        op0=ADD,
                        op1=MAX,
                    )
                if v == UNITS - 1 and chains > 1:
                    nc.vector.scalar_tensor_tensor(
                        out=top[:],
                        in0=tops_of[block, 1][:],
                        scalar=steps[1][:, tap : tap + 1],
                        in1=top[:],
                        op0=ADD,
                        op1=MAX,
                    )

            def load_top(block):
                top = psum_top.tile([P, BLOCK_PIX], F32, name="top_ps")
                nc.tensor.matmul(
                    out=top[:], lhsT=ident_f32[:], rhs=tops_of[block, 0][:], start=True, stop=True
                )
                top_of[block] = top

            def subtract(unit):
                block, v = divmod(unit, UNITS)
                if v % SUB_UNITS > 0:
                    return
                n = min(SUB_UNITS * UNIT_TAPS, TAPS - v * UNIT_TAPS)
                logits = logit_of[block, v // SUB_UNITS][:, :n, :]
                nc.vector.tensor_tensor(
                    out=logits,
                    in0=logits,
                    in1=top_of[block][:].unsqueeze(1).to_broadcast([P, n, BLOCK_PIX]),
                    op=SUB,
                )

            def exponentiate(unit):
                block, taps = taps_of(unit)
                n = len(taps)
                exps = exp_pool.tile([P, UNIT_TAPS, BLOCK_PIX], F32, name="exps")
                last = taps_of(block * UNITS + UNITS - 1)[1][-1]
                nc.scalar.activation(
                    out=exps[:, :n, :],
                    in_=logits_of(unit),
                    func=EXP,
                    bias=minus_bias[:, last : last + 1],
                )
                exp_of[unit] = exps

            def load_window(block):
                base = block * BLOCK_ROWS * ROW
                for pair in range(CH // 2):
                    window = psum_x.tile([P, 2, WIN], BF16, tag="window", name="window")
                    for j in range(2):
                        nc.tensor.matmul(
                            out=window[:, j, :],
                            lhsT=ident_bf16[:],
                            rhs=x_pad[:, 2 * pair + j, base : base + WIN],
                            start=True,
                            stop=True,
                        )
                    window_of[pair] = window

            def multiply(unit):
                block, taps = taps_of(unit)
                calls = []
                for i, tap in enumerate(taps):
                    engine = "gpsimd" if is_gpsimds(unit, i) else "vector"
                    row0, row1 = live_rows(block, tap)
                    if row1 - row0 == BLOCK_ROWS:
                        prod = pools["products"].tile([P, CH, BLOCK_PIX], F32, name="prod")
                    else:
                        prod = edge_prods[engine][0]
                        edge_prods[engine] = edge_prods[engine][1:] + [prod]
                    prod_of[unit, i] = prod
                    pixels = slice(row0 * W, row1 * W)
                    offset = (tap // KS + row0) * ROW + (LEFT - PAD) + tap % KS
                    exp_img = exp_of[unit][:, i, pixels].rearrange("p (h w) -> p h w", w=W).unsqueeze(1)

                    def window(rows, begin, length):
                        return rows[:, :, begin : begin + length].rearrange("p c (h w) -> p c h w", w=ROW)[:, :, :, :W]

                    def product(engine, prod, exp_img, x, channels, pixels):
                        engine.tensor_tensor(
                            out=prod[:, channels, pixels].rearrange("p c (h w) -> p c h w", w=W),
                            in0=exp_img.to_broadcast(list(x.shape)),
                            in1=x,
                            op=MULT,
                        )

                    length = (row1 - row0) * ROW
                    if engine == "gpsimd":
                        x = window(x_pad, block * BLOCK_ROWS * ROW + offset, length)
                        product(nc.gpsimd, prod, exp_img, x, slice(0, CH), pixels)
                    else:
                        for pair in range(CH // 2):
                            x = window(window_of[pair], offset, length)
                            channels = slice(2 * pair, 2 * pair + 2)
                            calls.append(partial(product, nc.vector, prod, exp_img, x, channels, pixels))
                return calls

            def add_exps(unit):
                block, taps = taps_of(unit)
                opens, closes = unit % UNITS == 0, unit % UNITS == UNITS - 1
                if opens:
                    den = psum_den.tile([P, BLOCK_TILES, GROUPS], F32, name="den")
                    den_of[block] = den
                for i in range(len(taps)):
                    for j in range(BLOCK_TILES):
                        nc.tensor.matmul(
                            out=den_of[block][:, j, :],
                            lhsT=exp_of[unit][:, i, j * P : (j + 1) * P],
                            rhs=ident_f32[:],
                            start=(opens and i == 0 and j == 0),
                            stop=(closes and i == len(taps) - 1 and j == BLOCK_TILES - 1),
                            is_transpose=True,
                        )

            def add_products(taps, tiles):
                block = taps[0][0] // UNITS
                in_block = [tap for tap in adding_order if tap[0] // UNITS == block]
                for j in tiles:
                    if (block, j) not in sums_of:
                        sums = psum_sums.tile([P, CH, GROUPS], F32, tag="sums", name="sums")
                        sums_of[block, j] = sums
                for j in tiles:
                    for tap in taps:
                        for c in range(CH):
                            nc.tensor.matmul(
                                out=sums_of[block, j][:, c, :],
                                lhsT=prod_of[tap][:, c, j * P : (j + 1) * P],
                                rhs=ident_f32[:],
                                start=(tap == in_block[0] and c == 0),
                                stop=(tap == in_block[-1] and c == CH - 1),
                                is_transpose=True,
                            )

            def invert(block):
                inverse = pools["results"].tile([P, BLOCK_TILES, GROUPS], F32, name="inverse")
                nc.vector.reciprocal(out=inverse[:], in_=den_of[block][:])
                inverse_of[block] = inverse

            def divide(block):
                for j in range(BLOCK_TILES):
                    scaled = pools["results"].tile([P, CH, GROUPS], F32, name="scaled")
                    nc.vector.tensor_tensor(
                        out=scaled[:],
                        in0=sums_of[block, j][:],
                        in1=inverse_of[block][:, j, :].unsqueeze(1).to_broadcast([P, CH, GROUPS]),
                        op=MULT,
                    )
                    scaled_of[block, j] = scaled

            def store(block):
                for j in range(BLOCK_TILES):
                    scaled = scaled_of[block, j]
                    back = psum_sums.tile([P, CH, P], F32, tag="sums", name="back")
                    for c in range(CH):
                        nc.tensor.transpose(back[:, c, :], scaled[:, c, :], ident_f32[:])
                    result = pools["results"].tile([P, CH, P], F32, name="result")
                    nc.scalar.copy(out=result[:], in_=back[:])
                    pt = block * BLOCK_TILES + j
                    nc.sync.dma_start(out=out_by_group[:, :, pt * P : (pt + 1) * P], in_=result[:])

            def turn(unit):
                block, v = divmod(unit, UNITS)
                sweep = unit + SWEEP_LEAD
                done = None
                if unit < N_UNITS and v == 0:
                    load_window(block)
                if unit + 1 < N_UNITS:
                    add_exps(unit + 1)
                if sweep + 1 < N_UNITS:
                    make_kern(sweep + 1)
                calls = multiply(unit) if unit < N_UNITS else []
                if v > 0:
                    for call in calls[:1]:
                        call()
                    calls = calls[1:]
                if sweep < N_UNITS:
                    take_max(sweep, 0)
                if unit + LEAD < N_UNITS:
                    subtract(unit + LEAD)
                    exponentiate(unit + LEAD)
                if v > 0:
                    for call in calls[:1]:
                        call()
                    calls = calls[1:]
                if sweep < N_UNITS:
                    if len(taps_of(sweep)[1]) > 1:
                        take_max(sweep, 1)
                    keep_logits(sweep)
                for call in calls:
                    call()
                if v == UNITS - 1 - LEAD and block + 1 < N_BLOCKS:
                    load_top(block + 1)
                adding = state["adding"]
                if adding and state["divided"] is None:
                    block_taps = [tap for tap in adding if tap[0] // UNITS == adding[0][0] // UNITS]
                    ready = [tap for tap in block_taps if added_at(*tap) <= unit]
                    state["adding"] = adding[len(ready) :]
                    if ready and len(ready) == len(block_taps):
                        done = ready[0][0] // UNITS
                        add_products(ready, range(BLOCK_TILES))
                    else:
                        for tap in ready:
                            add_products([tap], range(BLOCK_TILES))
                if unit + 1 < N_UNITS and (unit + 1) % UNITS == UNITS - 1:
                    invert((unit + 1) // UNITS)
                tiles = edge_prods["vector"] + edge_prods["gpsimd"]
                if UNITS <= unit < UNITS + len(tiles):
                    nc.scalar.copy(out=tiles[unit - UNITS][:, :, BLOCK_PIX - PAD * W :], in_=zeros[:, :, : PAD * W])
                if state["divided"] is not None:
                    store(state["divided"])
                    state["divided"] = None
                if done is not None:
                    divide(done)
                    state["divided"] = done

            def sweep_over(unit):
                for i in range(len(taps_of(unit)[1])):
                    take_max(unit, i)
                keep_logits(unit)

            for unit in range(FIRST_AHEAD):
                make_kern(unit)
            for unit in range(UNITS):
                if unit + FIRST_AHEAD <= UNITS:
                    make_kern(unit + FIRST_AHEAD)
                sweep_over(unit)
            load_top(0)
            for unit in range(UNITS, SWEEP_LEAD):
                sweep_over(unit)
                make_kern(unit + 1)
                if unit - UNITS < LEAD:
                    subtract(unit - UNITS)
                    exponentiate(unit - UNITS)

            state = {
                "divided": None,
                "adding": adding_order,
            }
            add_exps(0)
            red = start.tile([P, PACK, HALF], BF16, name="red")
            for unit in range(FIRST_TURNS):
                turn(unit)
                for t in range(2 * unit, min(2 * unit + 2, PACK)):
                    relu_on_scalar(red, project(psum_sums, "sums", t, halves[1]), t)
                if unit == 4:
                    group_red(nc.scalar.copy, red, halves[1])
            quantise(red_words, red_plane, grouped, halves[1])

        pools["products"] = stack.enter_context(tc.tile_pool(name="products", bufs=12))
        pools["results"] = stack.enter_context(tc.tile_pool(name="results", bufs=2))

        for unit in range(FIRST_TURNS, N_UNITS + LAG + 2):
            turn(unit)
